import numpy as np
import ml_dtypes


def mxq(x, axis, fmt="e4m3"):
    dtype, down = {"e4m3": (ml_dtypes.float8_e4m3fn, 7), "e5m2": (ml_dtypes.float8_e5m2, 14)}[fmt]
    v = np.moveaxis(np.asarray(x, np.float32).astype(ml_dtypes.bfloat16).astype(np.float64), axis, -1)
    blocks = v.reshape(v.shape[:-1] + (-1, 32))
    amax = np.abs(blocks).max(-1, keepdims=True)
    byte = np.maximum(np.where(amax > 0, np.frexp(amax)[1] - 1 + 127, 0) - down, 1)
    scale = np.exp2(byte - 127.0)
    codes = (blocks / scale).astype(np.float32).astype(dtype).astype(np.float64)
    return np.moveaxis((codes * scale).reshape(v.shape), -1, axis)


WIDE = False


def mx_kscale(k):
    if not WIDE:
        return np.ones(k)
    levels = np.array([30, -30])
    if k % 512:
        return np.exp2(np.random.permutation(np.resize(levels, k // 32))).repeat(32)
    a = np.empty((k // 512, 16))
    for p in range(k // 512):
        a[p, :8] = np.random.permutation(np.resize(levels, 8))
        for g in range(8):
            far = levels[np.abs(levels - a[p, g]) >= 10]
            a[p, g + 8] = far[np.random.randint(len(far))]
    return np.exp2(a.ravel()).repeat(32)


BF16 = ml_dtypes.bfloat16


def bf(x):
    return np.asarray(x, np.float32).astype(BF16)


def f64(x):
    return np.asarray(x).astype(np.float64)


B, N, C, DIM, H = 4, 128, 2048, 2048, 16
D = DIM // H // 2
LAYER_NUM = 12
LAM_INIT = 0.8 - 0.6 * np.exp(-0.3 * LAYER_NUM)
SCALE = D ** -0.5


def split_qk(y):
    y = y.reshape(B, N, H, D, 2)
    return np.moveaxis(y, -1, 2).reshape(B, N, 2 * H, D)


def setup_inputs():
    s = mx_kscale(C)
    ls = 0.45 / D ** 0.25
    return {"x": bf(np.random.standard_normal((B, N, C)) * s),
            "Wq": bf(np.random.standard_normal((DIM, C)) / np.sqrt(C) / s),
            "Wk": bf(np.random.standard_normal((DIM, C)) / np.sqrt(C) / s),
            "lq1": bf(np.random.standard_normal(D) * ls),
            "lq2": bf(np.random.standard_normal(D) * ls),
            "lk1": bf(np.random.standard_normal(D) * ls),
            "lk2": bf(np.random.standard_normal(D) * ls)}


def reference(x, Wq, Wk, lq1, lq2, lk1, lk2):
    xq = mxq(f64(x), 2, "e5m2")
    q = split_qk(xq @ mxq(f64(Wq), 1, "e4m3").T) * SCALE
    k = split_qk(xq @ mxq(f64(Wk), 1, "e4m3").T)
    sc = np.stack([(q[:, :, i:i + 1, :] * k).sum(-1) for i in range(2 * H)], axis=2)
    e = np.exp(sc - sc.max(-1, keepdims=True))
    att = e / e.sum(-1, keepdims=True)
    lam = np.exp(np.sum(f64(lq1) * f64(lk1))) - np.exp(np.sum(f64(lq2) * f64(lk2))) + LAM_INIT
    return att[:, :, :H, :H] - lam * att[:, :, H:, H:]

@@ -1,0 +1,324 @@
+from contextlib import ExitStack
+
+import concourse.masks as masks
+import concourse.mybir as mybir
+
+F32 = mybir.dt.float32
+BF16 = mybir.dt.bfloat16
+U32 = mybir.dt.uint32
+U8 = mybir.dt.uint8
+E4M3 = mybir.dt.float8_e4m3fn_x4
+E5M2 = mybir.dt.float8_e5m2_x4
+ALU = mybir.AluOpType
+ACT = mybir.ActivationFunctionType
+AX = mybir.AxisListType
+
+P = 128
+C = 2048
+H = 16
+D = 64
+TOK = 512
+NB = 4
+PASSES = 4
+SCALE = 0.125
+LAM_INIT = 0.8 - 0.6 * 2.718281828459045 ** (-3.6)
+CW = 320
+CHUNK = 16
+
+FLOPS = 2 * TOK * C * 2 * C + 2 * TOK * 32 * 32 * D
+
+
+def tile_differentialattention_pa_kernel(tc, x, Wq, Wk, lq1, lq2, lk1, lk2, out):
+    nc = tc.nc
+    x_rows = x.flatten_outer_dims()
+    pairs = [("x", x_rows, m) for m in range(2)]
+    pairs += [("q", Wq, m) for m in range(8)]
+    pairs += [("k", Wk, m) for m in range(8)]
+    n_pairs = len(pairs)
+
+    with ExitStack() as ctx:
+        const = ctx.enter_context(tc.tile_pool(name="const", bufs=1))
+        big = ctx.enter_context(tc.tile_pool(name="big", bufs=1))
+        rawp = ctx.enter_context(tc.tile_pool(name="rawp", bufs=3))
+        grp = ctx.enter_context(tc.tile_pool(name="grp", bufs=2))
+        cdp = ctx.enter_context(tc.tile_pool(name="cdp", bufs=2))
+        sm = ctx.enter_context(tc.tile_pool(name="sm", bufs=2))
+        ps_t = ctx.enter_context(tc.psum_pool(name="ps_t", bufs=4))
+        ps_m = ctx.enter_context(tc.psum_pool(name="ps_m", bufs=4))
+        ctx.enter_context(tc.manual_schedule())
+
+        raw_of = {}
+        banks_of = {}
+        grouped_of = {}
+        codes_of = {}
+        acc_of = {}
+
+        def load(n):
+            kind, src, m = pairs[n]
+            raw = rawp.tile([P, 2, C], BF16, tag="raw", name="raw")
+            nc.sync.dma_start(
+                out=raw[:],
+                in_=src[256 * m:256 * (m + 1), :].rearrange("(r p) k -> p r k", p=P),
+            )
+            raw_of[n] = raw
+
+        for n in range(3):
+            load(n)
+
+        ident = const.tile([P, P], F32, name="ident")
+        masks.make_identity(nc, ident[:])
+        perm = const.tile([P, P], F32, name="perm")
+        nc.vector.tensor_copy(
+            out=perm[:].rearrange("p (j d) -> p j d", j=2),
+            in_=ident[:].rearrange("p (d j) -> p j d", j=2),
+        )
+        slot = const.tile([P, 2], F32, name="slot")
+        nc.vector.memset(slot[0:64, 0:1], SCALE)
+        nc.vector.memset(slot[64:128, 0:1], 0.0)
+        nc.vector.memset(slot[0:64, 1:2], 0.0)
+        nc.vector.memset(slot[64:128, 1:2], SCALE)
+        warm = const.tile([P, 2], F32, name="warm")
+        nc.vector.memset(warm[:, 0:1], 0.0)
+        nc.scalar.activation(out=warm[:, 1:2], in_=warm[:, 0:1], func=ACT.Exp)
+
+        x_codes = big.tile([P, PASSES * TOK], U32, name="x_codes", align_bytes=64)
+        x_scales = big.tile([P, PASSES * TOK], U8, name="x_scales", align_bytes=64)
+        q_pad = big.tile([P, NB * 32 * P], F32, name="q_pad")
+        k_two = big.tile([P, NB * 32 * P], F32, name="k_two")
+        att = big.tile([P, P, H], F32, name="att")
+        res = big.tile([P, NB, H, H], F32, name="res")
+        q_rows = q_pad[:].rearrange("p (t i g) -> p t i g", t=NB, i=32)
+        k_rows = k_two[:].rearrange("p (t c g) -> p t c g", t=NB, c=32)
+
+        def transposes(n):
+            kind = pairs[n][0]
+            moving = ident if kind == "x" else perm
+            words = raw_of[n][:].bitcast(F32)
+            banks = []
+            for gp in range(2):
+                for r in range(2):
+                    tb = ps_t.tile([P, 512], F32, tag="tb", name="tb")
+                    for gg in range(2):
+                        for u in range(2):
+                            base = 256 * (2 * gp + gg)
+                            col = 128 * (2 * gg + u)
+                            nc.tensor.transpose(
+                                tb[:, col:col + 128],
+                                words[:, r, base + u:base + 256:2],
+                                moving[:],
+                            )
+                    banks.append((gp, r, tb))
+            banks_of[n] = banks
+
+        def interleave(n):
+            grouped = grp.tile([P, PASSES * 1024], BF16, tag="grouped", name="grouped", align_bytes=64)
+            gw = grouped[:].bitcast(F32).rearrange("p (g c u) -> p g c u", g=PASSES, u=2)
+            for i, (gp, r, tb) in enumerate(banks_of[n]):
+                dst = gw[:, 2 * gp:2 * gp + 2, 128 * r:128 * r + 128, :]
+                src = tb[:].rearrange("p (g u c) -> p g c u", g=2, u=2)
+                if i % 2 == 0:
+                    nc.scalar.copy(out=dst, in_=src)
+                else:
+                    nc.vector.tensor_copy(out=dst, in_=src)
+            grouped_of[n] = grouped
+
+        def quantize(n):
+            kind, src, m = pairs[n]
+            grouped = grouped_of[n]
+            if kind == "x":
+                for g in range(PASSES):
+                    cols = slice(TOK * g + 256 * m, TOK * g + 256 * m + 256)
+                    nc.vector.quantize_mx(
+                        out=x_codes[:, cols].bitcast(E5M2),
+                        scales=x_scales[:, cols],
+                        in_=grouped[:, 1024 * g:1024 * (g + 1)],
+                    )
+                return
+            codes = cdp.tile([P, PASSES * CW], U32, tag="codes", name="codes", align_bytes=64)
+            scales = cdp.tile([P, PASSES * CW], U8, tag="scales", name="scales", align_bytes=64)
+            for g in range(PASSES):
+                cols = slice(CW * g, CW * g + 256)
+                nc.vector.quantize_mx(
+                    out=codes[:, cols].bitcast(E4M3),
+                    scales=scales[:, cols],
+                    in_=grouped[:, 1024 * g:1024 * (g + 1)],
+                )
+            if kind == "k":
+                for g in range(PASSES):
+                    cols = slice(CW * g + 256, CW * g + 320)
+                    nc.vector.quantize_mx(
+                        out=codes[:, cols].bitcast(E4M3),
+                        scales=scales[:, cols],
+                        in_=grouped[:, 1024 * g:1024 * g + 256],
+                    )
+            codes_of[n] = (codes, scales)
+
+        def project(n):
+            kind = pairs[n][0]
+            codes, scales = codes_of[n]
+            starts = (0, 128) if kind == "q" else (0, 64, 128, 192)
+            accs = []
+            for w in starts:
+                acc = ps_m.tile([P, TOK], F32, tag="acc", name="acc")
+                for g in range(PASSES):
+                    cols = slice(CW * g + w, CW * g + w + 128)
+                    toks = slice(TOK * g, TOK * (g + 1))
+                    nc.tensor.matmul_mx(
+                        out=acc[:],
+                        lhsT=codes[:, cols].bitcast(E4M3),
+                        lhsT_scale=scales[:, cols],
+                        rhs=x_codes[:, toks].bitcast(E5M2),
+                        rhs_scale=x_scales[:, toks],
+                        start=(g == 0),
+                        stop=(g == PASSES - 1),
+                    )
+                accs.append(acc)
+            acc_of[n] = accs
+
+        def keep(n):
+            kind, src, m = pairs[n]
+            for i, acc in enumerate(acc_of[n]):
+                view = acc[:].rearrange("p (t g) -> p t g", t=NB)
+                if kind == "q":
+                    h = 2 * m + i
+                    for j in range(2):
+                        dst = q_rows[:, :, H * j + h, :]
+                        if i == 0:
+                            nc.scalar.activation(out=dst, in_=view, func=ACT.Copy, scale=slot[:, j:j + 1])
+                        else:
+                            nc.vector.tensor_scalar(
+                                out=dst, in0=view, scalar1=slot[:, j:j + 1], scalar2=None, op0=ALU.mult
+                            )
+                else:
+                    c = (2 * m + i // 2) + H * (i % 2)
+                    dst = k_rows[:, :, c, :]
+                    if i == 3:
+                        nc.vector.tensor_copy(out=dst, in_=view)
+                    else:
+                        nc.scalar.copy(out=dst, in_=view)
+
+        transposes(0)
+        load(3)
+        for n in range(n_pairs + 1):
+            if n - 1 >= 2:
+                project(n - 1)
+            if n < n_pairs:
+                interleave(n)
+                quantize(n)
+            if n - 1 >= 2:
+                keep(n - 1)
+            if n + 1 < n_pairs:
+                transposes(n + 1)
+                if n + 4 < n_pairs:
+                    load(n + 4)
+
+        lqk = const.tile([P, 4, D], BF16, name="lqk")
+        for i, v in enumerate((lq1, lq2, lk1, lk2)):
+            nc.sync.dma_start(out=lqk[:, i, :], in_=v.partition_broadcast(P))
+        prod = const.tile([P, 2, D], F32, name="prod")
+        nc.vector.tensor_tensor(out=prod[:], in0=lqk[:, 0:2, :], in1=lqk[:, 2:4, :], op=ALU.mult)
+        dots = const.tile([P, 2, 1], F32, name="dots")
+        nc.vector.tensor_reduce(out=dots[:], in_=prod[:], axis=AX.X, op=ALU.add)
+        expd = const.tile([P, 2, 1], F32, name="expd")
+        nc.scalar.activation(out=expd[:], in_=dots[:], func=ACT.Exp)
+        neg_lam = const.tile([P, 1], F32, name="neg_lam")
+        nc.vector.scalar_tensor_tensor(
+            out=neg_lam[:], in0=expd[:, 1, :], scalar=-LAM_INIT, in1=expd[:, 0, :],
+            op0=ALU.add, op1=ALU.subtract,
+        )
+        comb = const.tile([P, NB * H], F32, name="comb")
+        iv = ident[:].rearrange("p (t j a) -> p t j a", t=NB, j=2)
+        nc.vector.scalar_tensor_tensor(
+            out=comb[:].rearrange("p (t a) -> p t a", t=NB),
+            in0=iv[:, :, 1, :], scalar=neg_lam[:, 0:1], in1=iv[:, :, 0, :],
+            op0=ALU.mult, op1=ALU.add,
+        )
+
+        q_cols = q_pad[:].rearrange("p (m g) -> p m g", g=P)
+        k_cols = k_two[:].rearrange("p (m g) -> p m g", g=P)
+        n_chunks = P // CHUNK
+        score_of = {}
+        exp_of = {}
+
+        def scores(ch):
+            pool, tag = (ps_t, "tb") if ch % 2 == 0 else (ps_m, "acc")
+            banks = []
+            for b in range(CHUNK // 4):
+                sb = pool.tile([P, 512], F32, tag=tag, name="sb")
+                for s in range(4):
+                    g = CHUNK * ch + 4 * b + s
+                    nc.tensor.matmul(
+                        out=sb[:, 128 * s:128 * s + 128],
+                        lhsT=q_cols[:, :, g],
+                        rhs=k_cols[:, :, g],
+                        start=True,
+                        stop=True,
+                    )
+                banks.append(sb)
+            score_of[ch] = banks
+
+        def soft_front(ch):
+            sc = sm.tile([P, CHUNK, 32], F32, tag="sc", name="sc")
+            for b, sb in enumerate(score_of[ch]):
+                view = sb[:].rearrange("p (s m) -> p s m", s=4)
+                for t in range(NB):
+                    rows = slice(32 * t, 32 * t + 32)
+                    dst = sc[rows, 4 * b:4 * b + 4, :]
+                    src = view[rows, :, 32 * t:32 * t + 32]
+                    if b % 2 == 0:
+                        nc.scalar.copy(out=dst, in_=src)
+                    else:
+                        nc.vector.tensor_copy(out=dst, in_=src)
+            top = sm.tile([P, CHUNK, 1], F32, tag="top", name="top")
+            nc.vector.tensor_reduce(out=top[:], in_=sc[:], axis=AX.X, op=ALU.max)
+            sd = sm.tile([P, CHUNK, 32], F32, tag="sd", name="sd")
+            nc.vector.tensor_tensor(
+                out=sd[:], in0=sc[:], in1=top[:].to_broadcast([P, CHUNK, 32]), op=ALU.subtract
+            )
+            ex = sm.tile([P, CHUNK, 32], F32, tag="ex", name="ex")
+            nc.scalar.activation(out=ex[:], in_=sd[:], func=ACT.Exp)
+            exp_of[ch] = ex
+
+        def soft_back(ch):
+            ex = exp_of[ch]
+            tot = sm.tile([P, CHUNK, 1], F32, tag="tot", name="tot")
+            nc.vector.tensor_reduce(out=tot[:], in_=ex[:], axis=AX.X, op=ALU.add)
+            rec = sm.tile([P, CHUNK, 1], F32, tag="rec", name="rec")
+            nc.vector.reciprocal(out=rec[:], in_=tot[:])
+            nc.vector.tensor_tensor(
+                out=att[:, CHUNK * ch:CHUNK * (ch + 1), :],
+                in0=ex[:, :, 0:H],
+                in1=rec[:].to_broadcast([P, CHUNK, H]),
+                op=ALU.mult,
+            )
+
+        scores(0)
+        for ch in range(n_chunks):
+            if ch + 1 < n_chunks:
+                scores(ch + 1)
+            soft_front(ch)
+            if ch >= 1:
+                soft_back(ch - 1)
+        soft_back(n_chunks - 1)
+
+        res_v = res[:].rearrange("p t a h -> p (t a) h")
+        for fb in range(2):
+            fin = ps_t.tile([P, 512], F32, tag="tb", name="fin")
+            for s in range(8):
+                nc.tensor.matmul(
+                    out=fin[:, 64 * s:64 * s + 64],
+                    lhsT=att[:, :, 8 * fb + s],
+                    rhs=comb[:],
+                    start=True,
+                    stop=True,
+                )
+            dst = res_v[:, :, 8 * fb:8 * fb + 8]
+            src = fin[:].rearrange("p (s m) -> p m s", s=8)
+            if fb == 0:
+                nc.scalar.copy(out=dst, in_=src)
+            else:
+                nc.vector.tensor_copy(out=dst, in_=src)
+        nc.sync.dma_start(
+            out=out.rearrange("b n a h -> n b (a h)"),
+            in_=res[:].rearrange("p t a h -> p t (a h)"),
+        )

@@ -18,12 +18,13 @@ C = 2048
 H = 16
 D = 64
 TOK = 512
-NB = 4
+GT = 4
 PASSES = 4
 SCALE = 0.125
 LAM_INIT = 0.8 - 0.6 * 2.718281828459045 ** (-3.6)
 CW = 320
-CHUNK = 16
+SIZES = [16] * 7 + [8, 4, 4]
+SWAP_DMA = True
 
 FLOPS = 2 * TOK * C * 2 * C + 2 * TOK * 32 * 32 * D
 
@@ -39,286 +40,346 @@ def tile_differentialattention_pa_kernel(tc, x, Wq, Wk, lq1, lq2, lk1, lk2, out)
     with ExitStack() as ctx:
         const = ctx.enter_context(tc.tile_pool(name="const", bufs=1))
         big = ctx.enter_context(tc.tile_pool(name="big", bufs=1))
-        rawp = ctx.enter_context(tc.tile_pool(name="rawp", bufs=3))
-        grp = ctx.enter_context(tc.tile_pool(name="grp", bufs=2))
-        cdp = ctx.enter_context(tc.tile_pool(name="cdp", bufs=2))
-        sm = ctx.enter_context(tc.tile_pool(name="sm", bufs=2))
-        ps_t = ctx.enter_context(tc.psum_pool(name="ps_t", bufs=4))
-        ps_m = ctx.enter_context(tc.psum_pool(name="ps_m", bufs=4))
         ctx.enter_context(tc.manual_schedule())
 
-        raw_of = {}
-        banks_of = {}
-        grouped_of = {}
-        codes_of = {}
-        acc_of = {}
+        q_pad = big.tile([P, TOK * 32], F32, name="q_pad")
+        k_two = big.tile([P, 32 * TOK], F32, name="k_two")
+        k_rows = k_two[:].rearrange("p (c k) -> p c k", c=32)
+        comb = const.tile([P, P], F32, name="comb")
 
-        def load(n):
-            kind, src, m = pairs[n]
-            raw = rawp.tile([P, 2, C], BF16, tag="raw", name="raw")
-            nc.sync.dma_start(
-                out=raw[:],
-                in_=src[256 * m:256 * (m + 1), :].rearrange("(r p) k -> p r k", p=P),
-            )
-            raw_of[n] = raw
+        with ExitStack() as ph1:
+            one = ph1.enter_context(tc.tile_pool(name="one", bufs=1))
+            rawp = ph1.enter_context(tc.tile_pool(name="rawp", bufs=3))
+            grp = ph1.enter_context(tc.tile_pool(name="grp", bufs=2))
+            cdp = ph1.enter_context(tc.tile_pool(name="cdp", bufs=2))
+            ps_t = ph1.enter_context(tc.psum_pool(name="ps_t", bufs=4))
+            ps_m = ph1.enter_context(tc.psum_pool(name="ps_m", bufs=4))
 
-        for n in range(3):
-            load(n)
+            raw_of = {}
+            banks_of = {}
+            grouped_of = {}
+            codes_of = {}
+            acc_of = {}
 
-        ident = const.tile([P, P], F32, name="ident")
-        masks.make_identity(nc, ident[:])
-        perm = const.tile([P, P], F32, name="perm")
-        nc.vector.tensor_copy(
-            out=perm[:].rearrange("p (j d) -> p j d", j=2),
-            in_=ident[:].rearrange("p (d j) -> p j d", j=2),
-        )
-        slot = const.tile([P, 2], F32, name="slot")
-        nc.vector.memset(slot[0:64, 0:1], SCALE)
-        nc.vector.memset(slot[64:128, 0:1], 0.0)
-        nc.vector.memset(slot[0:64, 1:2], 0.0)
-        nc.vector.memset(slot[64:128, 1:2], SCALE)
-        warm = const.tile([P, 2], F32, name="warm")
-        nc.vector.memset(warm[:, 0:1], 0.0)
-        nc.scalar.activation(out=warm[:, 1:2], in_=warm[:, 0:1], func=ACT.Exp)
-
-        x_codes = big.tile([P, PASSES * TOK], U32, name="x_codes", align_bytes=64)
-        x_scales = big.tile([P, PASSES * TOK], U8, name="x_scales", align_bytes=64)
-        q_pad = big.tile([P, NB * 32 * P], F32, name="q_pad")
-        k_two = big.tile([P, NB * 32 * P], F32, name="k_two")
-        att = big.tile([P, P, H], F32, name="att")
-        res = big.tile([P, NB, H, H], F32, name="res")
-        q_rows = q_pad[:].rearrange("p (t i g) -> p t i g", t=NB, i=32)
-        k_rows = k_two[:].rearrange("p (t c g) -> p t c g", t=NB, c=32)
-
-        def transposes(n):
-            kind = pairs[n][0]
-            moving = ident if kind == "x" else perm
-            words = raw_of[n][:].bitcast(F32)
-            banks = []
-            for gp in range(2):
-                for r in range(2):
-                    tb = ps_t.tile([P, 512], F32, tag="tb", name="tb")
-                    for gg in range(2):
-                        for u in range(2):
-                            base = 256 * (2 * gp + gg)
-                            col = 128 * (2 * gg + u)
-                            nc.tensor.transpose(
-                                tb[:, col:col + 128],
-                                words[:, r, base + u:base + 256:2],
-                                moving[:],
-                            )
-                    banks.append((gp, r, tb))
-            banks_of[n] = banks
-
-        def interleave(n):
-            grouped = grp.tile([P, PASSES * 1024], BF16, tag="grouped", name="grouped", align_bytes=64)
-            gw = grouped[:].bitcast(F32).rearrange("p (g c u) -> p g c u", g=PASSES, u=2)
-            for i, (gp, r, tb) in enumerate(banks_of[n]):
-                dst = gw[:, 2 * gp:2 * gp + 2, 128 * r:128 * r + 128, :]
-                src = tb[:].rearrange("p (g u c) -> p g c u", g=2, u=2)
-                if i % 2 == 0:
-                    nc.scalar.copy(out=dst, in_=src)
+            def load(n):
+                kind, src, m = pairs[n]
+                raw = rawp.tile([P, 2, C], BF16, tag="raw", name="raw")
+                rows = src[256 * m:256 * (m + 1), :].rearrange("(r p) k -> p r k", p=P)
+                if n == 0:
+                    for gp in range(2):
+                        for r in range(2):
+                            cols = slice(1024 * gp, 1024 * (gp + 1))
+                            nc.sync.dma_start(out=raw[:, r, cols], in_=rows[:, r, cols])
                 else:
-                    nc.vector.tensor_copy(out=dst, in_=src)
-            grouped_of[n] = grouped
+                    nc.sync.dma_start(out=raw[:], in_=rows)
+                raw_of[n] = raw
 
-        def quantize(n):
-            kind, src, m = pairs[n]
-            grouped = grouped_of[n]
-            if kind == "x":
+            for n in range(3):
+                load(n)
+
+            ident = const.tile([P, P], F32, name="ident")
+            masks.make_identity(nc, ident[:])
+            perm = const.tile([P, P], F32, name="perm")
+            nc.vector.tensor_copy(
+                out=perm[:].rearrange("p (j d) -> p j d", j=2),
+                in_=ident[:].rearrange("p (d j) -> p j d", j=2),
+            )
+            slot = const.tile([P, 2], F32, name="slot")
+            nc.vector.memset(slot[0:64, 0:1], SCALE)
+            nc.vector.memset(slot[64:128, 0:1], 0.0)
+            nc.vector.memset(slot[0:64, 1:2], 0.0)
+            nc.vector.memset(slot[64:128, 1:2], SCALE)
+            warm = const.tile([P, 2], F32, name="warm")
+            nc.vector.memset(warm[:, 0:1], 0.0)
+            nc.scalar.activation(out=warm[:, 1:2], in_=warm[:, 0:1], func=ACT.Exp)
+            nc.vector.memset(comb[:], 0.0)
+
+            x_codes = one.tile([P, PASSES * TOK], U32, name="x_codes", align_bytes=64)
+            x_scales = one.tile([P, PASSES * TOK], U8, name="x_scales", align_bytes=64)
+            q_nat = one.tile([P, H * TOK], F32, name="q_nat")
+
+            def windows(n):
+                kind = pairs[n][0]
+                if kind == "q":
+                    return (0, 128)
+                if SWAP_DMA and n < n_pairs - 1:
+                    return (0, 128)
+                return (0, 64, 128, 192)
+
+            def transposes(n):
+                kind = pairs[n][0]
+                moving = ident if kind == "x" else perm
+                words = raw_of[n][:].bitcast(F32)
+                banks = []
+                for gp in range(2):
+                    for r in range(2):
+                        tb = ps_t.tile([P, 512], F32, tag="tb", name="tb")
+                        for gg in range(2):
+                            for u in range(2):
+                                base = 256 * (2 * gp + gg)
+                                col = 128 * (2 * gg + u)
+                                nc.tensor.transpose(
+                                    tb[:, col:col + 128],
+                                    words[:, r, base + u:base + 256:2],
+                                    moving[:],
+                                )
+                        banks.append((gp, r, tb))
+                banks_of[n] = banks
+
+            def interleave(n):
+                kind = pairs[n][0]
+                on_vector = (3,) if kind == "k" else (1, 3)
+                grouped = grp.tile([P, PASSES * 1024], BF16, tag="grouped", name="grouped", align_bytes=64)
+                gw = grouped[:].bitcast(F32).rearrange("p (g c u) -> p g c u", g=PASSES, u=2)
+                for i, (gp, r, tb) in enumerate(banks_of[n]):
+                    dst = gw[:, 2 * gp:2 * gp + 2, 128 * r:128 * r + 128, :]
+                    src = tb[:].rearrange("p (g u c) -> p g c u", g=2, u=2)
+                    if i in on_vector:
+                        nc.vector.tensor_copy(out=dst, in_=src)
+                    else:
+                        nc.scalar.copy(out=dst, in_=src)
+                grouped_of[n] = grouped
+
+            def quantize(n):
+                kind, src, m = pairs[n]
+                grouped = grouped_of[n]
+                if kind == "x":
+                    for g in range(PASSES):
+                        cols = slice(TOK * g + 256 * m, TOK * g + 256 * m + 256)
+                        nc.vector.quantize_mx(
+                            out=x_codes[:, cols].bitcast(E5M2),
+                            scales=x_scales[:, cols],
+                            in_=grouped[:, 1024 * g:1024 * (g + 1)],
+                        )
+                    return
+                codes = cdp.tile([P, PASSES * CW], U32, tag="codes", name="codes", align_bytes=64)
+                scales = cdp.tile([P, PASSES * CW], U8, tag="scales", name="scales", align_bytes=64)
                 for g in range(PASSES):
-                    cols = slice(TOK * g + 256 * m, TOK * g + 256 * m + 256)
-                    nc.vector.quantize_mx(
-                        out=x_codes[:, cols].bitcast(E5M2),
-                        scales=x_scales[:, cols],
-                        in_=grouped[:, 1024 * g:1024 * (g + 1)],
-                    )
-                return
-            codes = cdp.tile([P, PASSES * CW], U32, tag="codes", name="codes", align_bytes=64)
-            scales = cdp.tile([P, PASSES * CW], U8, tag="scales", name="scales", align_bytes=64)
-            for g in range(PASSES):
-                cols = slice(CW * g, CW * g + 256)
-                nc.vector.quantize_mx(
-                    out=codes[:, cols].bitcast(E4M3),
-                    scales=scales[:, cols],
-                    in_=grouped[:, 1024 * g:1024 * (g + 1)],
-                )
-            if kind == "k":
-                for g in range(PASSES):
-                    cols = slice(CW * g + 256, CW * g + 320)
+                    cols = slice(CW * g, CW * g + 256)
                     nc.vector.quantize_mx(
                         out=codes[:, cols].bitcast(E4M3),
                         scales=scales[:, cols],
-                        in_=grouped[:, 1024 * g:1024 * g + 256],
+                        in_=grouped[:, 1024 * g:1024 * (g + 1)],
                     )
-            codes_of[n] = (codes, scales)
+                if len(windows(n)) == 4:
+                    for g in range(PASSES):
+                        cols = slice(CW * g + 256, CW * g + 320)
+                        nc.vector.quantize_mx(
+                            out=codes[:, cols].bitcast(E4M3),
+                            scales=scales[:, cols],
+                            in_=grouped[:, 1024 * g:1024 * g + 256],
+                        )
+                codes_of[n] = (codes, scales)
 
-        def project(n):
-            kind = pairs[n][0]
-            codes, scales = codes_of[n]
-            starts = (0, 128) if kind == "q" else (0, 64, 128, 192)
-            accs = []
-            for w in starts:
-                acc = ps_m.tile([P, TOK], F32, tag="acc", name="acc")
-                for g in range(PASSES):
-                    cols = slice(CW * g + w, CW * g + w + 128)
-                    toks = slice(TOK * g, TOK * (g + 1))
-                    nc.tensor.matmul_mx(
-                        out=acc[:],
-                        lhsT=codes[:, cols].bitcast(E4M3),
-                        lhsT_scale=scales[:, cols],
-                        rhs=x_codes[:, toks].bitcast(E5M2),
-                        rhs_scale=x_scales[:, toks],
-                        start=(g == 0),
-                        stop=(g == PASSES - 1),
-                    )
-                accs.append(acc)
-            acc_of[n] = accs
+            def project(n):
+                codes, scales = codes_of[n]
+                accs = []
+                for w in windows(n):
+                    acc = ps_m.tile([P, TOK], F32, tag="acc", name="acc")
+                    for g in range(PASSES):
+                        cols = slice(CW * g + w, CW * g + w + 128)
+                        toks = slice(TOK * g, TOK * (g + 1))
+                        nc.tensor.matmul_mx(
+                            out=acc[:],
+                            lhsT=codes[:, cols].bitcast(E4M3),
+                            lhsT_scale=scales[:, cols],
+                            rhs=x_codes[:, toks].bitcast(E5M2),
+                            rhs_scale=x_scales[:, toks],
+                            start=(g == 0),
+                            stop=(g == PASSES - 1),
+                        )
+                    accs.append((w, acc))
+                acc_of[n] = accs
 
-        def keep(n):
-            kind, src, m = pairs[n]
-            for i, acc in enumerate(acc_of[n]):
-                view = acc[:].rearrange("p (t g) -> p t g", t=NB)
-                if kind == "q":
-                    h = 2 * m + i
-                    for j in range(2):
-                        dst = q_rows[:, :, H * j + h, :]
+            def keep(n):
+                kind, src, m = pairs[n]
+                for i, (w, acc) in enumerate(acc_of[n]):
+                    head = 2 * m + w // 128
+                    if kind == "q":
+                        dst = q_nat[:, TOK * head:TOK * (head + 1)]
                         if i == 0:
-                            nc.scalar.activation(out=dst, in_=view, func=ACT.Copy, scale=slot[:, j:j + 1])
+                            nc.scalar.copy(out=dst, in_=acc[:])
                         else:
-                            nc.vector.tensor_scalar(
-                                out=dst, in0=view, scalar1=slot[:, j:j + 1], scalar2=None, op0=ALU.mult
-                            )
-                else:
-                    c = (2 * m + i // 2) + H * (i % 2)
-                    dst = k_rows[:, :, c, :]
-                    if i == 3:
-                        nc.vector.tensor_copy(out=dst, in_=view)
+                            nc.vector.tensor_copy(out=dst, in_=acc[:])
                     else:
-                        nc.scalar.copy(out=dst, in_=view)
+                        c = head + H * ((w // 64) % 2)
+                        if len(acc_of[n]) == 4 and i % 2 == 1:
+                            nc.vector.tensor_copy(out=k_rows[:, c, :], in_=acc[:])
+                        else:
+                            nc.scalar.copy(out=k_rows[:, c, :], in_=acc[:])
+                if kind == "k" and len(acc_of[n]) == 2:
+                    lo = slice(2 * m, 2 * m + 2)
+                    hi = slice(H + 2 * m, H + 2 * m + 2)
+                    nc.sync.dma_start(out=k_rows[64:128, hi, :], in_=k_rows[0:64, lo, :])
+                    nc.sync.dma_start(out=k_rows[0:64, hi, :], in_=k_rows[64:128, lo, :])
 
-        transposes(0)
-        load(3)
-        for n in range(n_pairs + 1):
-            if n - 1 >= 2:
-                project(n - 1)
-            if n < n_pairs:
-                interleave(n)
-                quantize(n)
-            if n - 1 >= 2:
-                keep(n - 1)
-            if n + 1 < n_pairs:
-                transposes(n + 1)
-                if n + 4 < n_pairs:
-                    load(n + 4)
+            def pad(piece):
+                hb, j = piece // 2, piece % 2
+                nc.vector.tensor_scalar(
+                    out=q_pad[:].rearrange("p (k i) -> p k i", i=32)[:, :, H * j + 4 * hb:H * j + 4 * hb + 4],
+                    in0=q_nat[:].rearrange("p (h k) -> p k h", k=TOK)[:, :, 4 * hb:4 * hb + 4],
+                    scalar1=slot[:, j:j + 1],
+                    scalar2=None,
+                    op0=ALU.mult,
+                )
 
-        lqk = const.tile([P, 4, D], BF16, name="lqk")
-        for i, v in enumerate((lq1, lq2, lk1, lk2)):
-            nc.sync.dma_start(out=lqk[:, i, :], in_=v.partition_broadcast(P))
-        prod = const.tile([P, 2, D], F32, name="prod")
-        nc.vector.tensor_tensor(out=prod[:], in0=lqk[:, 0:2, :], in1=lqk[:, 2:4, :], op=ALU.mult)
-        dots = const.tile([P, 2, 1], F32, name="dots")
-        nc.vector.tensor_reduce(out=dots[:], in_=prod[:], axis=AX.X, op=ALU.add)
-        expd = const.tile([P, 2, 1], F32, name="expd")
-        nc.scalar.activation(out=expd[:], in_=dots[:], func=ACT.Exp)
-        neg_lam = const.tile([P, 1], F32, name="neg_lam")
-        nc.vector.scalar_tensor_tensor(
-            out=neg_lam[:], in0=expd[:, 1, :], scalar=-LAM_INIT, in1=expd[:, 0, :],
-            op0=ALU.add, op1=ALU.subtract,
-        )
-        comb = const.tile([P, NB * H], F32, name="comb")
-        iv = ident[:].rearrange("p (t j a) -> p t j a", t=NB, j=2)
-        nc.vector.scalar_tensor_tensor(
-            out=comb[:].rearrange("p (t a) -> p t a", t=NB),
-            in0=iv[:, :, 1, :], scalar=neg_lam[:, 0:1], in1=iv[:, :, 0, :],
-            op0=ALU.mult, op1=ALU.add,
-        )
+            lqk = const.tile([P, 4, D], BF16, name="lqk")
 
-        q_cols = q_pad[:].rearrange("p (m g) -> p m g", g=P)
-        k_cols = k_two[:].rearrange("p (m g) -> p m g", g=P)
-        n_chunks = P // CHUNK
-        score_of = {}
-        exp_of = {}
+            def load_lambda():
+                for i, v in enumerate((lq1, lq2, lk1, lk2)):
+                    nc.sync.dma_start(out=lqk[:, i, :], in_=v.partition_broadcast(P))
 
-        def scores(ch):
-            pool, tag = (ps_t, "tb") if ch % 2 == 0 else (ps_m, "acc")
-            banks = []
-            for b in range(CHUNK // 4):
-                sb = pool.tile([P, 512], F32, tag=tag, name="sb")
-                for s in range(4):
-                    g = CHUNK * ch + 4 * b + s
-                    nc.tensor.matmul(
-                        out=sb[:, 128 * s:128 * s + 128],
-                        lhsT=q_cols[:, :, g],
-                        rhs=k_cols[:, :, g],
-                        start=True,
-                        stop=True,
-                    )
-                banks.append(sb)
-            score_of[ch] = banks
+            def make_comb():
+                prod = const.tile([P, 2, D], F32, name="prod")
+                nc.vector.tensor_tensor(out=prod[:], in0=lqk[:, 0:2, :], in1=lqk[:, 2:4, :], op=ALU.mult)
+                dots = const.tile([P, 2, 1], F32, name="dots")
+                nc.vector.tensor_reduce(out=dots[:], in_=prod[:], axis=AX.X, op=ALU.add)
+                expd = const.tile([P, 2, 1], F32, name="expd")
+                nc.scalar.activation(out=expd[:], in_=dots[:], func=ACT.Exp)
+                neg_lam = const.tile([P, 1], F32, name="neg_lam")
+                nc.vector.scalar_tensor_tensor(
+                    out=neg_lam[:], in0=expd[:, 1, :], scalar=-LAM_INIT, in1=expd[:, 0, :],
+                    op0=ALU.add, op1=ALU.subtract,
+                )
+                iv = ident[:].rearrange("p (t j a) -> p t j a", t=GT, j=2)
+                nc.vector.scalar_tensor_tensor(
+                    out=comb[:, 0:GT * H].rearrange("p (t a) -> p t a", t=GT),
+                    in0=iv[:, :, 1, :], scalar=neg_lam[:, 0:1], in1=iv[:, :, 0, :],
+                    op0=ALU.mult, op1=ALU.add,
+                )
 
-        def soft_front(ch):
-            sc = sm.tile([P, CHUNK, 32], F32, tag="sc", name="sc")
-            for b, sb in enumerate(score_of[ch]):
-                view = sb[:].rearrange("p (s m) -> p s m", s=4)
-                for t in range(NB):
+            transposes(0)
+            load(3)
+            for n in range(n_pairs + 1):
+                if n - 1 >= 2:
+                    project(n - 1)
+                if n < n_pairs:
+                    interleave(n)
+                    quantize(n)
+                if n - 1 >= 2:
+                    keep(n - 1)
+                if 10 <= n < 18:
+                    pad(n - 10)
+                if n + 1 < n_pairs:
+                    transposes(n + 1)
+                    if n + 4 < n_pairs:
+                        load(n + 4)
+                    if n + 4 == n_pairs:
+                        load_lambda()
+                if n == 16:
+                    make_comb()
+
+        with ExitStack() as ph2:
+            sm = ph2.enter_context(tc.tile_pool(name="sm", bufs=2))
+            ps_s = ph2.enter_context(tc.psum_pool(name="ps_s", bufs=6))
+            ps_f = ph2.enter_context(tc.psum_pool(name="ps_f", bufs=2))
+
+            q_cols = q_pad[:].rearrange("p (g m) -> p g m", m=P)
+            k_cols = k_two[:].rearrange("p (c g t) -> p g c t", c=32, t=GT)
+            out_v = out.rearrange("b n a h -> (b n) a h").rearrange("(g t) a h -> (t a) g h", t=GT)
+            n_banks = P // 4
+            first = [sum(SIZES[:i]) for i in range(len(SIZES))]
+            bank_of = {}
+            exp_of = {}
+            emitted = [0]
+            CH = max(SIZES)
+
+            def score_banks(upto):
+                while emitted[0] < min(upto, n_banks):
+                    b = emitted[0]
+                    sb = ps_s.tile([P, 512], F32, tag="sb", name="sb")
+                    for s in range(4):
+                        g = 4 * b + s
+                        nc.tensor.matmul(
+                            out=sb[:, 128 * s:128 * s + 128].rearrange("p (c t) -> p c t", t=GT),
+                            lhsT=q_cols[:, g, :],
+                            rhs=k_cols[:, g, :, :],
+                            start=True,
+                            stop=True,
+                        )
+                    bank_of[b] = sb
+                    emitted[0] = b + 1
+
+            sc_of = {}
+            sd_of = {}
+            fin_of = {}
+
+            def leave_bank(ch, i):
+                b = first[ch] // 4 + i
+                view = bank_of[b][:].rearrange("p (s c t) -> p s c t", s=4, t=GT)
+                for t in range(GT):
                     rows = slice(32 * t, 32 * t + 32)
-                    dst = sc[rows, 4 * b:4 * b + 4, :]
-                    src = view[rows, :, 32 * t:32 * t + 32]
-                    if b % 2 == 0:
+                    dst = sc_of[ch][rows, 4 * i:4 * i + 4, :]
+                    src = view[rows, :, :, t]
+                    if i % 2 == 0:
                         nc.scalar.copy(out=dst, in_=src)
                     else:
                         nc.vector.tensor_copy(out=dst, in_=src)
-            top = sm.tile([P, CHUNK, 1], F32, tag="top", name="top")
-            nc.vector.tensor_reduce(out=top[:], in_=sc[:], axis=AX.X, op=ALU.max)
-            sd = sm.tile([P, CHUNK, 32], F32, tag="sd", name="sd")
-            nc.vector.tensor_tensor(
-                out=sd[:], in0=sc[:], in1=top[:].to_broadcast([P, CHUNK, 32]), op=ALU.subtract
-            )
-            ex = sm.tile([P, CHUNK, 32], F32, tag="ex", name="ex")
-            nc.scalar.activation(out=ex[:], in_=sd[:], func=ACT.Exp)
-            exp_of[ch] = ex
 
-        def soft_back(ch):
-            ex = exp_of[ch]
-            tot = sm.tile([P, CHUNK, 1], F32, tag="tot", name="tot")
-            nc.vector.tensor_reduce(out=tot[:], in_=ex[:], axis=AX.X, op=ALU.add)
-            rec = sm.tile([P, CHUNK, 1], F32, tag="rec", name="rec")
-            nc.vector.reciprocal(out=rec[:], in_=tot[:])
-            nc.vector.tensor_tensor(
-                out=att[:, CHUNK * ch:CHUNK * (ch + 1), :],
-                in0=ex[:, :, 0:H],
-                in1=rec[:].to_broadcast([P, CHUNK, H]),
-                op=ALU.mult,
-            )
+            def shift(ch):
+                size = SIZES[ch]
+                sc = sc_of[ch]
+                top = sm.tile([P, CH, 1], F32, tag="top", name="top")
+                nc.vector.tensor_reduce(out=top[:, 0:size, :], in_=sc[:, 0:size, :], axis=AX.X, op=ALU.max)
+                sd = sm.tile([P, CH, 32], F32, tag="sd", name="sd")
+                nc.vector.tensor_tensor(
+                    out=sd[:, 0:size, :], in0=sc[:, 0:size, :],
+                    in1=top[:, 0:size, :].to_broadcast([P, size, 32]), op=ALU.subtract,
+                )
+                sd_of[ch] = sd
 
-        scores(0)
-        for ch in range(n_chunks):
-            if ch + 1 < n_chunks:
-                scores(ch + 1)
-            soft_front(ch)
-            if ch >= 1:
-                soft_back(ch - 1)
-        soft_back(n_chunks - 1)
+            def exponent(ch):
+                size = SIZES[ch]
+                ex = sm.tile([P, CH, 32], F32, tag="ex", name="ex")
+                nc.scalar.activation(out=ex[:, 0:size, :], in_=sd_of[ch][:, 0:size, :], func=ACT.Exp)
+                exp_of[ch] = ex
 
-        res_v = res[:].rearrange("p t a h -> p (t a) h")
-        for fb in range(2):
-            fin = ps_t.tile([P, 512], F32, tag="tb", name="fin")
-            for s in range(8):
+            def normalize(ch):
+                size = SIZES[ch]
+                ex = exp_of[ch]
+                tot = sm.tile([P, CH, 1], F32, tag="tot", name="tot")
+                nc.vector.tensor_reduce(out=tot[:, 0:size, :], in_=ex[:, 0:size, :], axis=AX.X, op=ALU.add)
+                rec = sm.tile([P, CH, 1], F32, tag="rec", name="rec")
+                nc.vector.reciprocal(out=rec[:, 0:size, :], in_=tot[:, 0:size, :])
+                att = sm.tile([P, CH, H], F32, tag="att", name="att")
+                nc.vector.tensor_tensor(
+                    out=att[:, 0:size, :],
+                    in0=ex[:, 0:size, 0:H],
+                    in1=rec[:, 0:size, :].to_broadcast([P, size, H]),
+                    op=ALU.mult,
+                )
+                fin = ps_f.tile([P, CH * H], F32, tag="fin", name="fin")
                 nc.tensor.matmul(
-                    out=fin[:, 64 * s:64 * s + 64],
-                    lhsT=att[:, :, 8 * fb + s],
-                    rhs=comb[:],
+                    out=fin[:, 0:size * H],
+                    lhsT=comb[:],
+                    rhs=att[:, 0:size, :].rearrange("p g h -> p (g h)"),
                     start=True,
                     stop=True,
                 )
-            dst = res_v[:, :, 8 * fb:8 * fb + 8]
-            src = fin[:].rearrange("p (s m) -> p m s", s=8)
-            if fb == 0:
-                nc.scalar.copy(out=dst, in_=src)
-            else:
-                nc.vector.tensor_copy(out=dst, in_=src)
-        nc.sync.dma_start(
-            out=out.rearrange("b n a h -> n b (a h)"),
-            in_=res[:].rearrange("p t a h -> p t (a h)"),
-        )
+                fin_of[ch] = fin
+
+            def store(ch):
+                size = SIZES[ch]
+                res = sm.tile([P, CH, H], F32, tag="res", name="res")
+                nc.scalar.copy(
+                    out=res[0:64, 0:size, :].rearrange("p g h -> p (g h)"), in_=fin_of[ch][0:64, 0:size * H]
+                )
+                nc.sync.dma_start(out=out_v[:, first[ch]:first[ch] + size, :], in_=res[0:64, 0:size, :])
+
+            n_chunks = len(SIZES)
+            for ch in range(n_chunks):
+                n_b = SIZES[ch] // 4
+                score_banks(first[ch] // 4 + 6)
+                sc_of[ch] = sm.tile([P, CH, 32], F32, tag="sc", name="sc")
+                for i in range(n_b):
+                    leave_bank(ch, i)
+                    if ch >= 1 and i == 0:
+                        exponent(ch - 1)
+                    if ch >= 1 and i == min(1, n_b - 1):
+                        normalize(ch - 1)
+                if ch >= 1:
+                    store(ch - 1)
+                shift(ch)
+            exponent(n_chunks - 1)
+            normalize(n_chunks - 1)
+            store(n_chunks - 1)

@@ -14,17 +14,18 @@ ACT = mybir.ActivationFunctionType
 AX = mybir.AxisListType
 
 P = 128
+HALF = 64
 C = 2048
 H = 16
 D = 64
 TOK = 512
-GT = 4
+TA = 256
 PASSES = 4
 SCALE = 0.125
 LAM_INIT = 0.8 - 0.6 * 2.718281828459045 ** (-3.6)
 CW = 320
 SIZES = [16] * 7 + [8, 4, 4]
-SWAP_DMA = True
+GB = 8
 
 FLOPS = 2 * TOK * C * 2 * C + 2 * TOK * 32 * 32 * D
 
@@ -42,16 +43,18 @@ def tile_differentialattention_pa_kernel(tc, x, Wq, Wk, lq1, lq2, lk1, lk2, out)
         big = ctx.enter_context(tc.tile_pool(name="big", bufs=1))
         ctx.enter_context(tc.manual_schedule())
 
-        q_pad = big.tile([P, TOK * 32], F32, name="q_pad")
-        k_two = big.tile([P, 32 * TOK], F32, name="k_two")
-        k_rows = k_two[:].rearrange("p (c k) -> p c k", c=32)
+        q_pad = big.tile([P, TA * 64], F32, name="q_pad")
+        k_st = big.tile([P, 32 * TA], F32, name="k_st")
+        k_rows = k_st[:].rearrange("p (m a) -> p m a", m=32)
         comb = const.tile([P, P], F32, name="comb")
+        pick = const.tile([P, 2], F32, name="pick")
 
         with ExitStack() as ph1:
             one = ph1.enter_context(tc.tile_pool(name="one", bufs=1))
             rawp = ph1.enter_context(tc.tile_pool(name="rawp", bufs=3))
             grp = ph1.enter_context(tc.tile_pool(name="grp", bufs=2))
             cdp = ph1.enter_context(tc.tile_pool(name="cdp", bufs=2))
+            stp = ph1.enter_context(tc.tile_pool(name="stp", bufs=3))
             ps_t = ph1.enter_context(tc.psum_pool(name="ps_t", bufs=4))
             ps_m = ph1.enter_context(tc.psum_pool(name="ps_m", bufs=4))
 
@@ -93,18 +96,21 @@ def tile_differentialattention_pa_kernel(tc, x, Wq, Wk, lq1, lq2, lk1, lk2, out)
             nc.vector.memset(warm[:, 0:1], 0.0)
             nc.scalar.activation(out=warm[:, 1:2], in_=warm[:, 0:1], func=ACT.Exp)
             nc.vector.memset(comb[:], 0.0)
+            by_row = ident[:].rearrange("p (x j a) -> p x j a", j=2, a=H)
+            for j in range(2):
+                nc.vector.tensor_reduce(out=pick[:, j:j + 1], in_=by_row[:, :, j, :], axis=AX.XY, op=ALU.add)
 
             x_codes = one.tile([P, PASSES * TOK], U32, name="x_codes", align_bytes=64)
             x_scales = one.tile([P, PASSES * TOK], U8, name="x_scales", align_bytes=64)
             q_nat = one.tile([P, H * TOK], F32, name="q_nat")
+            q_x = one.tile([P, H * TA], F32, name="q_x")
+            q_nat_rows = q_nat[:].rearrange("p (h k) -> p h k", h=H)
+            q_x_rows = q_x[:].rearrange("p (h a) -> p h a", h=H)
 
             def windows(n):
-                kind = pairs[n][0]
-                if kind == "q":
-                    return (0, 128)
-                if SWAP_DMA and n < n_pairs - 1:
-                    return (0, 128)
-                return (0, 64, 128, 192)
+                if n == n_pairs - 1:
+                    return (0, 64, 128, 192)
+                return (0, 128)
 
             def transposes(n):
                 kind = pairs[n][0]
@@ -127,8 +133,7 @@ def tile_differentialattention_pa_kernel(tc, x, Wq, Wk, lq1, lq2, lk1, lk2, out)
                 banks_of[n] = banks
 
             def interleave(n):
-                kind = pairs[n][0]
-                on_vector = (3,) if kind == "k" else (1, 3)
+                on_vector = (1, 3) if n < 6 else (3,)
                 grouped = grp.tile([P, PASSES * 1024], BF16, tag="grouped", name="grouped", align_bytes=64)
                 gw = grouped[:].bitcast(F32).rearrange("p (g c u) -> p g c u", g=PASSES, u=2)
                 for i, (gp, r, tb) in enumerate(banks_of[n]):
@@ -191,37 +196,69 @@ def tile_differentialattention_pa_kernel(tc, x, Wq, Wk, lq1, lq2, lk1, lk2, out)
                     accs.append((w, acc))
                 acc_of[n] = accs
 
-            def keep(n):
-                kind, src, m = pairs[n]
-                for i, (w, acc) in enumerate(acc_of[n]):
-                    head = 2 * m + w // 128
-                    if kind == "q":
-                        dst = q_nat[:, TOK * head:TOK * (head + 1)]
-                        if i == 0:
-                            nc.scalar.copy(out=dst, in_=acc[:])
-                        else:
-                            nc.vector.tensor_copy(out=dst, in_=acc[:])
+            UP = slice(0, HALF)
+            LOW = slice(HALF, P)
+            A_TOK = slice(0, TA)
+            B_TOK = slice(TA, TOK)
+
+            def keep_q(n):
+                m = pairs[n][2]
+                for w, acc in acc_of[n]:
+                    nc.scalar.copy(out=q_nat_rows[:, 2 * m + w // 128, :], in_=acc[:])
+                heads = slice(2 * m, 2 * m + 2)
+                nc.sync.dma_start(out=q_x_rows[LOW, heads, :], in_=q_nat_rows[UP, heads, B_TOK])
+                nc.sync.dma_start(out=q_x_rows[UP, heads, :], in_=q_nat_rows[LOW, heads, A_TOK])
+
+            def keep_k(n):
+                m = pairs[n][2]
+                moves = []
+                if len(acc_of[n]) == 2:
+                    stage = stp.tile([P, 2, TA], F32, tag="stage", name="stage")
+                    for r, (w, acc) in enumerate(acc_of[n]):
+                        h = 2 * m + r
+                        moves.append((k_rows[UP, h, :], acc[UP, A_TOK]))
+                        moves.append((stage[UP, r, :], acc[UP, B_TOK]))
+                        moves.append((k_rows[LOW, H + h, :], acc[LOW, B_TOK]))
+                        moves.append((stage[LOW, r, :], acc[LOW, A_TOK]))
+                else:
+                    stage = None
+                    h0, h1 = 2 * m, 2 * m + 1
+                    tops = (h0, H + h0, h1, H + h1)
+                    lows = (H + h0, h1, H + h1, h0)
+                    for i, (w, acc) in enumerate(acc_of[n]):
+                        moves.append((k_rows[UP, tops[i], :], acc[UP, A_TOK]))
+                        moves.append((k_rows[LOW, lows[i], :], acc[LOW, B_TOK]))
+                for e, (dst, src) in enumerate(moves):
+                    if e in (5, 7):
+                        nc.vector.tensor_copy(out=dst, in_=src)
                     else:
-                        c = head + H * ((w // 64) % 2)
-                        if len(acc_of[n]) == 4 and i % 2 == 1:
-                            nc.vector.tensor_copy(out=k_rows[:, c, :], in_=acc[:])
-                        else:
-                            nc.scalar.copy(out=k_rows[:, c, :], in_=acc[:])
-                if kind == "k" and len(acc_of[n]) == 2:
-                    lo = slice(2 * m, 2 * m + 2)
-                    hi = slice(H + 2 * m, H + 2 * m + 2)
-                    nc.sync.dma_start(out=k_rows[64:128, hi, :], in_=k_rows[0:64, lo, :])
-                    nc.sync.dma_start(out=k_rows[0:64, hi, :], in_=k_rows[64:128, lo, :])
+                        nc.scalar.copy(out=dst, in_=src)
+                if stage is not None:
+                    nc.sync.dma_start(out=k_rows[LOW, 2 * m:2 * m + 2, :], in_=stage[UP, :, :])
+                    nc.sync.dma_start(out=k_rows[UP, H + 2 * m:H + 2 * m + 2, :], in_=stage[LOW, :, :])
+
+            pad_view = q_pad[:].rearrange("p (a s i) -> p a s i", s=2, i=32)
+            nat_view = q_nat[:].rearrange("p (h k) -> p k h", h=H)
+            x_view = q_x[:].rearrange("p (h a) -> p a h", h=H)
 
             def pad(piece):
-                hb, j = piece // 2, piece % 2
+                hb, s, j = piece // 4, (piece // 2) % 2, piece % 2
+                heads = slice(4 * hb, 4 * hb + 4)
+                if j == s:
+                    src = nat_view[:, TA * s:TA * (s + 1), heads]
+                else:
+                    src = x_view[:, :, heads]
                 nc.vector.tensor_scalar(
-                    out=q_pad[:].rearrange("p (k i) -> p k i", i=32)[:, :, H * j + 4 * hb:H * j + 4 * hb + 4],
-                    in0=q_nat[:].rearrange("p (h k) -> p k h", k=TOK)[:, :, 4 * hb:4 * hb + 4],
-                    scalar1=slot[:, j:j + 1],
+                    out=pad_view[:, :, s, H * j + 4 * hb:H * j + 4 * hb + 4],
+                    in0=src,
+                    scalar1=slot[:, s:s + 1],
                     scalar2=None,
                     op0=ALU.mult,
                 )
+
+            pads_at = {6: (0, 1), 7: (2, 3), 8: (4, 5), 9: (6, 7)}
+            for i in range(8):
+                pads_at[10 + i] = (8 + i,)
 
             lqk = const.tile([P, 4, D], BF16, name="lqk")
 
@@ -241,12 +278,14 @@ def tile_differentialattention_pa_kernel(tc, x, Wq, Wk, lq1, lq2, lk1, lk2, out)
                     out=neg_lam[:], in0=expd[:, 1, :], scalar=-LAM_INIT, in1=expd[:, 0, :],
                     op0=ALU.add, op1=ALU.subtract,
                 )
-                iv = ident[:].rearrange("p (t j a) -> p t j a", t=GT, j=2)
-                nc.vector.scalar_tensor_tensor(
-                    out=comb[:, 0:GT * H].rearrange("p (t a) -> p t a", t=GT),
-                    in0=iv[:, :, 1, :], scalar=neg_lam[:, 0:1], in1=iv[:, :, 0, :],
-                    op0=ALU.mult, op1=ALU.add,
-                )
+                iv = ident[:].rearrange("p (e s j a) -> p e s j a", e=2, s=2, j=2)
+                cv = comb[:, 0:HALF].rearrange("p (s e a) -> p e s a", s=2, e=2)
+                for e in range(2):
+                    nc.vector.scalar_tensor_tensor(
+                        out=cv[:, e, :, :],
+                        in0=iv[:, e, :, 1, :], scalar=neg_lam[:, 0:1], in1=iv[:, e, :, 0, :],
+                        op0=ALU.mult, op1=ALU.add,
+                    )
 
             transposes(0)
             load(3)
@@ -257,9 +296,12 @@ def tile_differentialattention_pa_kernel(tc, x, Wq, Wk, lq1, lq2, lk1, lk2, out)
                     interleave(n)
                     quantize(n)
                 if n - 1 >= 2:
-                    keep(n - 1)
-                if 10 <= n < 18:
-                    pad(n - 10)
+                    if pairs[n - 1][0] == "q":
+                        keep_q(n - 1)
+                    else:
+                        keep_k(n - 1)
+                for piece in pads_at.get(n, ()):
+                    pad(piece)
                 if n + 1 < n_pairs:
                     transposes(n + 1)
                     if n + 4 < n_pairs:
@@ -275,23 +317,34 @@ def tile_differentialattention_pa_kernel(tc, x, Wq, Wk, lq1, lq2, lk1, lk2, out)
             ps_f = ph2.enter_context(tc.psum_pool(name="ps_f", bufs=2))
 
             q_cols = q_pad[:].rearrange("p (g m) -> p g m", m=P)
-            k_cols = k_two[:].rearrange("p (c g t) -> p g c t", c=32, t=GT)
-            out_v = out.rearrange("b n a h -> (b n) a h").rearrange("(g t) a h -> (t a) g h", t=GT)
-            n_banks = P // 4
-            first = [sum(SIZES[:i]) for i in range(len(SIZES))]
-            bank_of = {}
-            exp_of = {}
-            emitted = [0]
+            k_cols = k_st[:].rearrange("p (m g e) -> p g m e", m=32, e=2)
+            out_v = out.rearrange("b n a h -> (b n) a h").rearrange("(s g e) a h -> s (e a) g h", s=2, e=2)
+            n_chunks = len(SIZES)
+            first = [sum(SIZES[:i]) for i in range(n_chunks)]
+            plan = []
+            for ch in range(n_chunks):
+                for lo in range(0, SIZES[ch], GB):
+                    plan.append((ch, lo, min(GB, SIZES[ch] - lo)))
+            n_banks = len(plan)
+            first_bank = [min(b for b in range(n_banks) if plan[b][0] == ch) for ch in range(n_chunks)]
             CH = max(SIZES)
+            bank_of = {}
+            sc_of = {}
+            sd_of = {}
+            exp_of = {}
+            low_of = {}
+            fin_of = {}
+            emitted = [0]
 
             def score_banks(upto):
                 while emitted[0] < min(upto, n_banks):
                     b = emitted[0]
+                    ch, lo, count = plan[b]
                     sb = ps_s.tile([P, 512], F32, tag="sb", name="sb")
-                    for s in range(4):
-                        g = 4 * b + s
+                    for s in range(count):
+                        g = first[ch] + lo + s
                         nc.tensor.matmul(
-                            out=sb[:, 128 * s:128 * s + 128].rearrange("p (c t) -> p c t", t=GT),
+                            out=sb[:, 64 * s:64 * s + 64].rearrange("p (m e) -> p m e", e=2),
                             lhsT=q_cols[:, g, :],
                             rhs=k_cols[:, g, :, :],
                             start=True,
@@ -300,21 +353,17 @@ def tile_differentialattention_pa_kernel(tc, x, Wq, Wk, lq1, lq2, lk1, lk2, out)
                     bank_of[b] = sb
                     emitted[0] = b + 1
 
-            sc_of = {}
-            sd_of = {}
-            fin_of = {}
-
-            def leave_bank(ch, i):
-                b = first[ch] // 4 + i
-                view = bank_of[b][:].rearrange("p (s c t) -> p s c t", s=4, t=GT)
-                for t in range(GT):
-                    rows = slice(32 * t, 32 * t + 32)
-                    dst = sc_of[ch][rows, 4 * i:4 * i + 4, :]
-                    src = view[rows, :, :, t]
-                    if i % 2 == 0:
-                        nc.scalar.copy(out=dst, in_=src)
-                    else:
-                        nc.vector.tensor_copy(out=dst, in_=src)
+            def leave(ch):
+                sc = sm.tile([P, CH, 32], F32, tag="sc", name="sc")
+                for b in range(n_banks):
+                    if plan[b][0] != ch:
+                        continue
+                    lo, count = plan[b][1], plan[b][2]
+                    view = bank_of[b][:].rearrange("p (s m e) -> p s m e", s=GB, e=2)
+                    for e in range(2):
+                        rows = slice(HALF * e, HALF * (e + 1))
+                        nc.scalar.copy(out=sc[rows, lo:lo + count, :], in_=view[rows, 0:count, :, e])
+                sc_of[ch] = sc
 
             def shift(ch):
                 size = SIZES[ch]
@@ -332,7 +381,12 @@ def tile_differentialattention_pa_kernel(tc, x, Wq, Wk, lq1, lq2, lk1, lk2, out)
                 size = SIZES[ch]
                 ex = sm.tile([P, CH, 32], F32, tag="ex", name="ex")
                 nc.scalar.activation(out=ex[:, 0:size, :], in_=sd_of[ch][:, 0:size, :], func=ACT.Exp)
+                low = sm.tile([P, CH, H], F32, tag="low", name="low")
+                nc.scalar.activation(
+                    out=low[:, 0:size, :], in_=ex[:, 0:size, 0:H], func=ACT.Copy, scale=pick[:, 0:1]
+                )
                 exp_of[ch] = ex
+                low_of[ch] = low
 
             def normalize(ch):
                 size = SIZES[ch]
@@ -341,10 +395,15 @@ def tile_differentialattention_pa_kernel(tc, x, Wq, Wk, lq1, lq2, lk1, lk2, out)
                 nc.vector.tensor_reduce(out=tot[:, 0:size, :], in_=ex[:, 0:size, :], axis=AX.X, op=ALU.add)
                 rec = sm.tile([P, CH, 1], F32, tag="rec", name="rec")
                 nc.vector.reciprocal(out=rec[:, 0:size, :], in_=tot[:, 0:size, :])
+                own = sm.tile([P, CH, H], F32, tag="own", name="own")
+                nc.vector.scalar_tensor_tensor(
+                    out=own[:, 0:size, :], in0=ex[:, 0:size, H:32], scalar=pick[:, 1:2],
+                    in1=low_of[ch][:, 0:size, :], op0=ALU.mult, op1=ALU.add,
+                )
                 att = sm.tile([P, CH, H], F32, tag="att", name="att")
                 nc.vector.tensor_tensor(
                     out=att[:, 0:size, :],
-                    in0=ex[:, 0:size, 0:H],
+                    in0=own[:, 0:size, :],
                     in1=rec[:, 0:size, :].to_broadcast([P, size, H]),
                     op=ALU.mult,
                 )
@@ -362,24 +421,23 @@ def tile_differentialattention_pa_kernel(tc, x, Wq, Wk, lq1, lq2, lk1, lk2, out)
                 size = SIZES[ch]
                 res = sm.tile([P, CH, H], F32, tag="res", name="res")
                 nc.scalar.copy(
-                    out=res[0:64, 0:size, :].rearrange("p g h -> p (g h)"), in_=fin_of[ch][0:64, 0:size * H]
+                    out=res[0:HALF, 0:size, :].rearrange("p g h -> p (g h)"), in_=fin_of[ch][0:HALF, 0:size * H]
                 )
-                nc.sync.dma_start(out=out_v[:, first[ch]:first[ch] + size, :], in_=res[0:64, 0:size, :])
+                for s in range(2):
+                    nc.sync.dma_start(
+                        out=out_v[s, :, first[ch]:first[ch] + size, :],
+                        in_=res[32 * s:32 * (s + 1), 0:size, :],
+                    )
 
-            n_chunks = len(SIZES)
-            for ch in range(n_chunks):
-                n_b = SIZES[ch] // 4
-                score_banks(first[ch] // 4 + 6)
-                sc_of[ch] = sm.tile([P, CH, 32], F32, tag="sc", name="sc")
-                for i in range(n_b):
-                    leave_bank(ch, i)
-                    if ch >= 1 and i == 0:
-                        exponent(ch - 1)
-                    if ch >= 1 and i == min(1, n_b - 1):
-                        normalize(ch - 1)
-                if ch >= 1:
-                    store(ch - 1)
-                shift(ch)
-            exponent(n_chunks - 1)
-            normalize(n_chunks - 1)
-            store(n_chunks - 1)
+            for ch in range(n_chunks + 2):
+                if ch < n_chunks:
+                    score_banks(first_bank[ch] + 6)
+                    leave(ch)
+                if 1 <= ch <= n_chunks:
+                    exponent(ch - 1)
+                if ch >= 2:
+                    store(ch - 2)
+                if ch < n_chunks:
+                    shift(ch)
+                if 1 <= ch <= n_chunks:
+                    normalize(ch - 1)

@@ -32,8 +32,8 @@ FLOPS = 2 * TOK * C * 2 * C + 2 * TOK * 32 * 32 * D
 
 def tile_differentialattention_pa_kernel(tc, x, Wq, Wk, lq1, lq2, lk1, lk2, out):
     nc = tc.nc
-    x_rows = x.flatten_outer_dims()
-    pairs = [("x", x_rows, m) for m in range(2)]
+    x_by_parity = x.flatten_outer_dims().rearrange("(a s) k -> s a k", s=2)
+    pairs = [("x", x_by_parity[s], 0) for s in range(2)]
     pairs += [("q", Wq, m) for m in range(8)]
     pairs += [("k", Wk, m) for m in range(8)]
     n_pairs = len(pairs)
@@ -133,7 +133,7 @@ def tile_differentialattention_pa_kernel(tc, x, Wq, Wk, lq1, lq2, lk1, lk2, out)
                 banks_of[n] = banks
 
             def interleave(n):
-                on_vector = (1, 3) if n < 6 else (3,)
+                on_vector = (1, 3) if n < 6 or n == n_pairs - 1 else (3,)
                 grouped = grp.tile([P, PASSES * 1024], BF16, tag="grouped", name="grouped", align_bytes=64)
                 gw = grouped[:].bitcast(F32).rearrange("p (g c u) -> p g c u", g=PASSES, u=2)
                 for i, (gp, r, tb) in enumerate(banks_of[n]):
@@ -150,7 +150,7 @@ def tile_differentialattention_pa_kernel(tc, x, Wq, Wk, lq1, lq2, lk1, lk2, out)
                 grouped = grouped_of[n]
                 if kind == "x":
                     for g in range(PASSES):
-                        cols = slice(TOK * g + 256 * m, TOK * g + 256 * m + 256)
+                        cols = slice(TOK * g + TA * n, TOK * g + TA * (n + 1))
                         nc.vector.quantize_mx(
                             out=x_codes[:, cols].bitcast(E5M2),
                             scales=x_scales[:, cols],
@@ -266,26 +266,26 @@ def tile_differentialattention_pa_kernel(tc, x, Wq, Wk, lq1, lq2, lk1, lk2, out)
                 for i, v in enumerate((lq1, lq2, lk1, lk2)):
                     nc.sync.dma_start(out=lqk[:, i, :], in_=v.partition_broadcast(P))
 
-            def make_comb():
+            expd = const.tile([P, 2, 1], F32, name="expd")
+
+            def exp_dots():
                 prod = const.tile([P, 2, D], F32, name="prod")
                 nc.vector.tensor_tensor(out=prod[:], in0=lqk[:, 0:2, :], in1=lqk[:, 2:4, :], op=ALU.mult)
                 dots = const.tile([P, 2, 1], F32, name="dots")
                 nc.vector.tensor_reduce(out=dots[:], in_=prod[:], axis=AX.X, op=ALU.add)
-                expd = const.tile([P, 2, 1], F32, name="expd")
                 nc.scalar.activation(out=expd[:], in_=dots[:], func=ACT.Exp)
+
+            def make_comb():
                 neg_lam = const.tile([P, 1], F32, name="neg_lam")
                 nc.vector.scalar_tensor_tensor(
                     out=neg_lam[:], in0=expd[:, 1, :], scalar=-LAM_INIT, in1=expd[:, 0, :],
                     op0=ALU.add, op1=ALU.subtract,
                 )
-                iv = ident[:].rearrange("p (e s j a) -> p e s j a", e=2, s=2, j=2)
-                cv = comb[:, 0:HALF].rearrange("p (s e a) -> p e s a", s=2, e=2)
-                for e in range(2):
-                    nc.vector.scalar_tensor_tensor(
-                        out=cv[:, e, :, :],
-                        in0=iv[:, e, :, 1, :], scalar=neg_lam[:, 0:1], in1=iv[:, e, :, 0, :],
-                        op0=ALU.mult, op1=ALU.add,
-                    )
+                nc.vector.scalar_tensor_tensor(
+                    out=comb[:, 0:HALF].rearrange("p (t a) -> p t a", a=H),
+                    in0=by_row[:, :, 1, :], scalar=neg_lam[:, 0:1], in1=by_row[:, :, 0, :],
+                    op0=ALU.mult, op1=ALU.add,
+                )
 
             transposes(0)
             load(3)
@@ -306,9 +306,11 @@ def tile_differentialattention_pa_kernel(tc, x, Wq, Wk, lq1, lq2, lk1, lk2, out)
                     transposes(n + 1)
                     if n + 4 < n_pairs:
                         load(n + 4)
-                    if n + 4 == n_pairs:
+                    if n == 3:
                         load_lambda()
-                if n == 16:
+                if n == 5:
+                    exp_dots()
+                if n == 6:
                     make_comb()
 
         with ExitStack() as ph2:
@@ -318,7 +320,7 @@ def tile_differentialattention_pa_kernel(tc, x, Wq, Wk, lq1, lq2, lk1, lk2, out)
 
             q_cols = q_pad[:].rearrange("p (g m) -> p g m", m=P)
             k_cols = k_st[:].rearrange("p (m g e) -> p g m e", m=32, e=2)
-            out_v = out.rearrange("b n a h -> (b n) a h").rearrange("(s g e) a h -> s (e a) g h", s=2, e=2)
+            out_v = out.rearrange("b n a h -> (b n) a h").rearrange("(g t) a h -> (t a) g h", t=4)
             n_chunks = len(SIZES)
             first = [sum(SIZES[:i]) for i in range(n_chunks)]
             plan = []
@@ -423,11 +425,7 @@ def tile_differentialattention_pa_kernel(tc, x, Wq, Wk, lq1, lq2, lk1, lk2, out)
                 nc.scalar.copy(
                     out=res[0:HALF, 0:size, :].rearrange("p g h -> p (g h)"), in_=fin_of[ch][0:HALF, 0:size * H]
                 )
-                for s in range(2):
-                    nc.sync.dma_start(
-                        out=out_v[s, :, first[ch]:first[ch] + size, :],
-                        in_=res[32 * s:32 * (s + 1), 0:size, :],
-                    )
+                nc.sync.dma_start(out=out_v[:, first[ch]:first[ch] + size, :], in_=res[0:HALF, 0:size, :])
 
             for ch in range(n_chunks + 2):
                 if ch < n_chunks:

@@ -26,6 +26,11 @@ LAM_INIT = 0.8 - 0.6 * 2.718281828459045 ** (-3.6)
 CW = 320
 SIZES = [16] * 7 + [8, 4, 4]
 GB = 8
+UNIT = 16
+UA = 2 * UNIT
+N_UNITS = 8
+DEI = True
+EARLY_UNITS = 1
 
 FLOPS = 2 * TOK * C * 2 * C + 2 * TOK * 32 * 32 * D
 
@@ -41,24 +46,54 @@ def tile_differentialattention_pa_kernel(tc, x, Wq, Wk, lq1, lq2, lk1, lk2, out)
     with ExitStack() as ctx:
         const = ctx.enter_context(tc.tile_pool(name="const", bufs=1))
         big = ctx.enter_context(tc.tile_pool(name="big", bufs=1))
+        padp = ctx.enter_context(tc.tile_pool(name="padp", bufs=4))
         ctx.enter_context(tc.manual_schedule())
 
-        q_pad = big.tile([P, TA * 64], F32, name="q_pad")
         k_st = big.tile([P, 32 * TA], F32, name="k_st")
         k_rows = k_st[:].rearrange("p (m a) -> p m a", m=32)
+        q_nat = big.tile([P, H * TOK], F32, name="q_nat")
+        q_x = big.tile([P, H * TA], F32, name="q_x")
+        q_nat_rows = q_nat[:].rearrange("p (h k) -> p h k", h=H)
+        q_x_rows = q_x[:].rearrange("p (h a) -> p h a", h=H)
         comb = const.tile([P, P], F32, name="comb")
         pick = const.tile([P, 2], F32, name="pick")
+        slot = const.tile([P, 2], F32, name="slot")
+
+        nat_blocks = q_nat[:].rearrange("p (b h k) -> p b k h", b=4, h=4)
+        x_blocks = q_x[:].rearrange("p (b h a) -> p b a h", b=4, h=4)
+        padded_of = {}
+
+        def pad_piece(u, s, j):
+            if u not in padded_of:
+                padded_of[u] = padp.tile([P, UA * 64], F32, tag="padded", name="padded")
+            dst = padded_of[u][:].rearrange("p (a s j b h) -> p s j b a h", s=2, j=2, b=4, h=4)
+            if j == s:
+                src = nat_blocks[:, :, TA * s + UA * u:TA * s + UA * (u + 1), :]
+            else:
+                src = x_blocks[:, :, UA * u:UA * (u + 1), :]
+            nc.vector.tensor_scalar(
+                out=dst[:, s, j], in0=src, scalar1=slot[:, s:s + 1], scalar2=None, op0=ALU.mult,
+            )
+
+        PIECES = ((0, 0), (1, 1), (0, 1), (1, 0))
+
+        def prepare(u):
+            for s, j in PIECES:
+                pad_piece(u, s, j)
 
         with ExitStack() as ph1:
             one = ph1.enter_context(tc.tile_pool(name="one", bufs=1))
-            rawp = ph1.enter_context(tc.tile_pool(name="rawp", bufs=3))
+            rawp = ph1.enter_context(tc.tile_pool(name="rawp", bufs=4))
             grp = ph1.enter_context(tc.tile_pool(name="grp", bufs=2))
+            deip = ph1.enter_context(tc.tile_pool(name="deip", bufs=2)) if DEI else None
             cdp = ph1.enter_context(tc.tile_pool(name="cdp", bufs=2))
             stp = ph1.enter_context(tc.tile_pool(name="stp", bufs=3))
             ps_t = ph1.enter_context(tc.psum_pool(name="ps_t", bufs=4))
             ps_m = ph1.enter_context(tc.psum_pool(name="ps_m", bufs=4))
 
             raw_of = {}
+            dei_of = {}
+            stage_of = {}
             banks_of = {}
             grouped_of = {}
             codes_of = {}
@@ -77,7 +112,7 @@ def tile_differentialattention_pa_kernel(tc, x, Wq, Wk, lq1, lq2, lk1, lk2, out)
                     nc.sync.dma_start(out=raw[:], in_=rows)
                 raw_of[n] = raw
 
-            for n in range(3):
+            for n in range(4):
                 load(n)
 
             ident = const.tile([P, P], F32, name="ident")
@@ -87,7 +122,6 @@ def tile_differentialattention_pa_kernel(tc, x, Wq, Wk, lq1, lq2, lk1, lk2, out)
                 out=perm[:].rearrange("p (j d) -> p j d", j=2),
                 in_=ident[:].rearrange("p (d j) -> p j d", j=2),
             )
-            slot = const.tile([P, 2], F32, name="slot")
             nc.vector.memset(slot[0:64, 0:1], SCALE)
             nc.vector.memset(slot[64:128, 0:1], 0.0)
             nc.vector.memset(slot[0:64, 1:2], 0.0)
@@ -102,15 +136,25 @@ def tile_differentialattention_pa_kernel(tc, x, Wq, Wk, lq1, lq2, lk1, lk2, out)
 
             x_codes = one.tile([P, PASSES * TOK], U32, name="x_codes", align_bytes=64)
             x_scales = one.tile([P, PASSES * TOK], U8, name="x_scales", align_bytes=64)
-            q_nat = one.tile([P, H * TOK], F32, name="q_nat")
-            q_x = one.tile([P, H * TA], F32, name="q_x")
-            q_nat_rows = q_nat[:].rearrange("p (h k) -> p h k", h=H)
-            q_x_rows = q_x[:].rearrange("p (h a) -> p h a", h=H)
 
             def windows(n):
                 if n == n_pairs - 1:
                     return (0, 64, 128, 192)
                 return (0, 128)
+
+            def deinterleave(n):
+                words = raw_of[n][:].bitcast(F32)
+                dei = deip.tile([P, 2, C // 2], F32, tag="dei", name="dei")
+                parts = 2 if n == 0 else 1
+                width = (C // 2) // parts
+                for part in range(parts):
+                    for r in range(2):
+                        cols = slice(width * part, width * (part + 1))
+                        nc.vector.tensor_copy(
+                            out=dei[:, r, cols].rearrange("p (g u c) -> p g u c", u=2, c=P),
+                            in_=words[:, r, cols].rearrange("p (g c u) -> p g u c", u=2, c=P),
+                        )
+                dei_of[n] = dei
 
             def transposes(n):
                 kind = pairs[n][0]
@@ -124,16 +168,21 @@ def tile_differentialattention_pa_kernel(tc, x, Wq, Wk, lq1, lq2, lk1, lk2, out)
                             for u in range(2):
                                 base = 256 * (2 * gp + gg)
                                 col = 128 * (2 * gg + u)
-                                nc.tensor.transpose(
-                                    tb[:, col:col + 128],
-                                    words[:, r, base + u:base + 256:2],
-                                    moving[:],
-                                )
+                                if DEI:
+                                    turned = dei_of[n][:, r, base + 128 * u:base + 128 * (u + 1)]
+                                else:
+                                    turned = words[:, r, base + u:base + 256:2]
+                                nc.tensor.transpose(tb[:, col:col + 128], turned, moving[:])
                         banks.append((gp, r, tb))
                 banks_of[n] = banks
 
             def interleave(n):
-                on_vector = (1, 3) if n < 6 or n == n_pairs - 1 else (3,)
+                if n == n_pairs - 1:
+                    on_vector = (1, 3)
+                elif n >= 11:
+                    on_vector = ()
+                else:
+                    on_vector = (3,)
                 grouped = grp.tile([P, PASSES * 1024], BF16, tag="grouped", name="grouped", align_bytes=64)
                 gw = grouped[:].bitcast(F32).rearrange("p (g c u) -> p g c u", g=PASSES, u=2)
                 for i, (gp, r, tb) in enumerate(banks_of[n]):
@@ -213,13 +262,10 @@ def tile_differentialattention_pa_kernel(tc, x, Wq, Wk, lq1, lq2, lk1, lk2, out)
                 m = pairs[n][2]
                 moves = []
                 if len(acc_of[n]) == 2:
-                    stage = stp.tile([P, 2, TA], F32, tag="stage", name="stage")
+                    stage = stp.tile([P, 2, TOK], F32, tag="stage", name="stage")
                     for r, (w, acc) in enumerate(acc_of[n]):
-                        h = 2 * m + r
-                        moves.append((k_rows[UP, h, :], acc[UP, A_TOK]))
-                        moves.append((stage[UP, r, :], acc[UP, B_TOK]))
-                        moves.append((k_rows[LOW, H + h, :], acc[LOW, B_TOK]))
-                        moves.append((stage[LOW, r, :], acc[LOW, A_TOK]))
+                        nc.scalar.copy(out=stage[:, r, :], in_=acc[:])
+                    stage_of[n] = stage
                 else:
                     stage = None
                     h0, h1 = 2 * m, 2 * m + 1
@@ -234,31 +280,20 @@ def tile_differentialattention_pa_kernel(tc, x, Wq, Wk, lq1, lq2, lk1, lk2, out)
                     else:
                         nc.scalar.copy(out=dst, in_=src)
                 if stage is not None:
-                    nc.sync.dma_start(out=k_rows[LOW, 2 * m:2 * m + 2, :], in_=stage[UP, :, :])
-                    nc.sync.dma_start(out=k_rows[UP, H + 2 * m:H + 2 * m + 2, :], in_=stage[LOW, :, :])
+                    nc.sync.dma_start(out=k_rows[LOW, 2 * m:2 * m + 2, :], in_=stage[UP, :, B_TOK])
+                    nc.sync.dma_start(out=k_rows[UP, H + 2 * m:H + 2 * m + 2, :], in_=stage[LOW, :, A_TOK])
 
-            pad_view = q_pad[:].rearrange("p (a s i) -> p a s i", s=2, i=32)
-            nat_view = q_nat[:].rearrange("p (h k) -> p k h", h=H)
-            x_view = q_x[:].rearrange("p (h a) -> p a h", h=H)
+            def settle_k(n):
+                m = pairs[n][2]
+                stage = stage_of[n]
+                nc.vector.tensor_copy(out=k_rows[UP, 2 * m:2 * m + 2, :], in_=stage[UP, :, A_TOK])
+                nc.vector.tensor_copy(out=k_rows[LOW, H + 2 * m:H + 2 * m + 2, :], in_=stage[LOW, :, B_TOK])
 
-            def pad(piece):
-                hb, s, j = piece // 4, (piece // 2) % 2, piece % 2
-                heads = slice(4 * hb, 4 * hb + 4)
-                if j == s:
-                    src = nat_view[:, TA * s:TA * (s + 1), heads]
-                else:
-                    src = x_view[:, :, heads]
-                nc.vector.tensor_scalar(
-                    out=pad_view[:, :, s, H * j + 4 * hb:H * j + 4 * hb + 4],
-                    in0=src,
-                    scalar1=slot[:, s:s + 1],
-                    scalar2=None,
-                    op0=ALU.mult,
-                )
-
-            pads_at = {6: (0, 1), 7: (2, 3), 8: (4, 5), 9: (6, 7)}
-            for i in range(8):
-                pads_at[10 + i] = (8 + i,)
+            early = [(u, sj[0], sj[1]) for u in range(EARLY_UNITS) for sj in PIECES]
+            per_step = -(-len(early) // 6)
+            pads_at = {}
+            for i, piece in enumerate(early):
+                pads_at.setdefault(12 + i // per_step, []).append(piece)
 
             lqk = const.tile([P, 4, D], BF16, name="lqk")
 
@@ -287,24 +322,34 @@ def tile_differentialattention_pa_kernel(tc, x, Wq, Wk, lq1, lq2, lk1, lk2, out)
                     op0=ALU.mult, op1=ALU.add,
                 )
 
+            if DEI:
+                deinterleave(0)
             transposes(0)
-            load(3)
+            if DEI:
+                deinterleave(1)
+            load(4)
             for n in range(n_pairs + 1):
                 if n - 1 >= 2:
                     project(n - 1)
+                if DEI and n + 5 < n_pairs:
+                    load(n + 5)
                 if n < n_pairs:
                     interleave(n)
+                    if DEI and n + 2 < n_pairs:
+                        deinterleave(n + 2)
                     quantize(n)
+                if n - 2 in stage_of:
+                    settle_k(n - 2)
                 if n - 1 >= 2:
                     if pairs[n - 1][0] == "q":
                         keep_q(n - 1)
                     else:
                         keep_k(n - 1)
-                for piece in pads_at.get(n, ()):
-                    pad(piece)
+                for u, sp, jp in pads_at.get(n, ()):
+                    pad_piece(u, sp, jp)
                 if n + 1 < n_pairs:
                     transposes(n + 1)
-                    if n + 4 < n_pairs:
+                    if not DEI and n + 4 < n_pairs:
                         load(n + 4)
                     if n == 3:
                         load_lambda()
@@ -318,7 +363,6 @@ def tile_differentialattention_pa_kernel(tc, x, Wq, Wk, lq1, lq2, lk1, lk2, out)
             ps_s = ph2.enter_context(tc.psum_pool(name="ps_s", bufs=6))
             ps_f = ph2.enter_context(tc.psum_pool(name="ps_f", bufs=2))
 
-            q_cols = q_pad[:].rearrange("p (g m) -> p g m", m=P)
             k_cols = k_st[:].rearrange("p (m g e) -> p g m e", m=32, e=2)
             out_v = out.rearrange("b n a h -> (b n) a h").rearrange("(g t) a h -> (t a) g h", t=4)
             n_chunks = len(SIZES)
@@ -347,7 +391,7 @@ def tile_differentialattention_pa_kernel(tc, x, Wq, Wk, lq1, lq2, lk1, lk2, out)
                         g = first[ch] + lo + s
                         nc.tensor.matmul(
                             out=sb[:, 64 * s:64 * s + 64].rearrange("p (m e) -> p m e", e=2),
-                            lhsT=q_cols[:, g, :],
+                            lhsT=padded_of[g // UNIT][:, P * (g % UNIT):P * (g % UNIT + 1)],
                             rhs=k_cols[:, g, :, :],
                             start=True,
                             stop=True,
@@ -427,6 +471,8 @@ def tile_differentialattention_pa_kernel(tc, x, Wq, Wk, lq1, lq2, lk1, lk2, out)
                 )
                 nc.sync.dma_start(out=out_v[:, first[ch]:first[ch] + size, :], in_=res[0:HALF, 0:size, :])
 
+            for u in range(EARLY_UNITS, 4):
+                prepare(u)
             for ch in range(n_chunks + 2):
                 if ch < n_chunks:
                     score_banks(first_bank[ch] + 6)
@@ -439,3 +485,5 @@ def tile_differentialattention_pa_kernel(tc, x, Wq, Wk, lq1, lq2, lk1, lk2, out)
                     shift(ch)
                 if 1 <= ch <= n_chunks:
                     normalize(ch - 1)
+                if ch + 4 < N_UNITS:
+                    prepare(ch + 4)

@@ -23,7 +23,7 @@ TA = 256
 PASSES = 4
 SCALE = 0.125
 LAM_INIT = 0.8 - 0.6 * 2.718281828459045 ** (-3.6)
-CW = 320
+CW = 256
 SIZES = [16] * 7 + [8, 4, 4]
 GB = 8
 UNIT = 16
@@ -117,15 +117,11 @@ def tile_differentialattention_pa_kernel(tc, x, Wq, Wk, lq1, lq2, lk1, lk2, out)
 
             ident = const.tile([P, P], F32, name="ident")
             masks.make_identity(nc, ident[:])
-            perm = const.tile([P, P], F32, name="perm")
-            nc.vector.tensor_copy(
-                out=perm[:].rearrange("p (j d) -> p j d", j=2),
-                in_=ident[:].rearrange("p (d j) -> p j d", j=2),
-            )
-            nc.vector.memset(slot[0:64, 0:1], SCALE)
-            nc.vector.memset(slot[64:128, 0:1], 0.0)
-            nc.vector.memset(slot[0:64, 1:2], 0.0)
-            nc.vector.memset(slot[64:128, 1:2], SCALE)
+            parity = const.tile([P, 2], F32, name="parity")
+            by_parity = ident[:].rearrange("p (d j) -> p j d", j=2)
+            for sp in range(2):
+                nc.vector.tensor_reduce(out=parity[:, sp:sp + 1], in_=by_parity[:, sp, :], axis=AX.X, op=ALU.add)
+            nc.vector.tensor_scalar(out=slot[:], in0=parity[:], scalar1=SCALE, scalar2=None, op0=ALU.mult)
             warm = const.tile([P, 2], F32, name="warm")
             nc.vector.memset(warm[:, 0:1], 0.0)
             nc.scalar.activation(out=warm[:, 1:2], in_=warm[:, 0:1], func=ACT.Exp)
@@ -138,8 +134,6 @@ def tile_differentialattention_pa_kernel(tc, x, Wq, Wk, lq1, lq2, lk1, lk2, out)
             x_scales = one.tile([P, PASSES * TOK], U8, name="x_scales", align_bytes=64)
 
             def windows(n):
-                if n == n_pairs - 1:
-                    return (0, 64, 128, 192)
                 return (0, 128)
 
             def deinterleave(n):
@@ -157,8 +151,7 @@ def tile_differentialattention_pa_kernel(tc, x, Wq, Wk, lq1, lq2, lk1, lk2, out)
                 dei_of[n] = dei
 
             def transposes(n):
-                kind = pairs[n][0]
-                moving = ident if kind == "x" else perm
+                moving = ident
                 words = raw_of[n][:].bitcast(F32)
                 banks = []
                 for gp in range(2):
@@ -215,14 +208,6 @@ def tile_differentialattention_pa_kernel(tc, x, Wq, Wk, lq1, lq2, lk1, lk2, out)
                         scales=scales[:, cols],
                         in_=grouped[:, 1024 * g:1024 * (g + 1)],
                     )
-                if len(windows(n)) == 4:
-                    for g in range(PASSES):
-                        cols = slice(CW * g + 256, CW * g + 320)
-                        nc.vector.quantize_mx(
-                            out=codes[:, cols].bitcast(E4M3),
-                            scales=scales[:, cols],
-                            in_=grouped[:, 1024 * g:1024 * g + 256],
-                        )
                 codes_of[n] = (codes, scales)
 
             def project(n):
@@ -245,8 +230,8 @@ def tile_differentialattention_pa_kernel(tc, x, Wq, Wk, lq1, lq2, lk1, lk2, out)
                     accs.append((w, acc))
                 acc_of[n] = accs
 
-            UP = slice(0, HALF)
-            LOW = slice(HALF, P)
+            EVEN = slice(0, P, 2)
+            ODD = slice(1, P, 2)
             A_TOK = slice(0, TA)
             B_TOK = slice(TA, TOK)
 
@@ -255,39 +240,32 @@ def tile_differentialattention_pa_kernel(tc, x, Wq, Wk, lq1, lq2, lk1, lk2, out)
                 for w, acc in acc_of[n]:
                     nc.scalar.copy(out=q_nat_rows[:, 2 * m + w // 128, :], in_=acc[:])
                 heads = slice(2 * m, 2 * m + 2)
-                nc.sync.dma_start(out=q_x_rows[LOW, heads, :], in_=q_nat_rows[UP, heads, B_TOK])
-                nc.sync.dma_start(out=q_x_rows[UP, heads, :], in_=q_nat_rows[LOW, heads, A_TOK])
+                nc.sync.dma_start(out=q_x_rows[ODD, heads, :], in_=q_nat_rows[EVEN, heads, B_TOK])
+                nc.sync.dma_start(out=q_x_rows[EVEN, heads, :], in_=q_nat_rows[ODD, heads, A_TOK])
 
             def keep_k(n):
-                m = pairs[n][2]
-                moves = []
-                if len(acc_of[n]) == 2:
-                    stage = stp.tile([P, 2, TOK], F32, tag="stage", name="stage")
-                    for r, (w, acc) in enumerate(acc_of[n]):
-                        nc.scalar.copy(out=stage[:, r, :], in_=acc[:])
-                    stage_of[n] = stage
-                else:
-                    stage = None
-                    h0, h1 = 2 * m, 2 * m + 1
-                    tops = (h0, H + h0, h1, H + h1)
-                    lows = (H + h0, h1, H + h1, h0)
-                    for i, (w, acc) in enumerate(acc_of[n]):
-                        moves.append((k_rows[UP, tops[i], :], acc[UP, A_TOK]))
-                        moves.append((k_rows[LOW, lows[i], :], acc[LOW, B_TOK]))
-                for e, (dst, src) in enumerate(moves):
-                    if e in (5, 7):
-                        nc.vector.tensor_copy(out=dst, in_=src)
+                last = n == n_pairs - 1
+                stage = stp.tile([P, 2, TOK], F32, tag="stage", name="stage")
+                for r, (w, acc) in enumerate(acc_of[n]):
+                    if last and r == 1:
+                        nc.vector.tensor_copy(out=stage[:, r, :], in_=acc[:])
                     else:
-                        nc.scalar.copy(out=dst, in_=src)
-                if stage is not None:
-                    nc.sync.dma_start(out=k_rows[LOW, 2 * m:2 * m + 2, :], in_=stage[UP, :, B_TOK])
-                    nc.sync.dma_start(out=k_rows[UP, H + 2 * m:H + 2 * m + 2, :], in_=stage[LOW, :, A_TOK])
+                        nc.scalar.copy(out=stage[:, r, :], in_=acc[:])
+                stage_of[n] = stage
 
             def settle_k(n):
                 m = pairs[n][2]
                 stage = stage_of[n]
-                nc.vector.tensor_copy(out=k_rows[UP, 2 * m:2 * m + 2, :], in_=stage[UP, :, A_TOK])
-                nc.vector.tensor_copy(out=k_rows[LOW, H + 2 * m:H + 2 * m + 2, :], in_=stage[LOW, :, B_TOK])
+                first_map = slice(2 * m, 2 * m + 2)
+                second_map = slice(H + 2 * m, H + 2 * m + 2)
+                if n == n_pairs - 1:
+                    nc.sync.dma_start(out=k_rows[EVEN, first_map, :], in_=stage[EVEN, :, A_TOK])
+                    nc.sync.dma_start(out=k_rows[ODD, second_map, :], in_=stage[ODD, :, B_TOK])
+                else:
+                    nc.vector.tensor_copy(out=k_rows[:, first_map, :], in_=stage[:, :, A_TOK])
+                    nc.vector.tensor_copy(out=k_rows[:, second_map, :], in_=stage[:, :, B_TOK])
+                nc.sync.dma_start(out=k_rows[ODD, first_map, :], in_=stage[EVEN, :, B_TOK])
+                nc.sync.dma_start(out=k_rows[EVEN, second_map, :], in_=stage[ODD, :, A_TOK])
 
             early = [(u, sj[0], sj[1]) for u in range(EARLY_UNITS) for sj in PIECES]
             per_step = -(-len(early) // 6)
@@ -357,6 +335,7 @@ def tile_differentialattention_pa_kernel(tc, x, Wq, Wk, lq1, lq2, lk1, lk2, out)
                     exp_dots()
                 if n == 6:
                     make_comb()
+            settle_k(n_pairs - 1)
 
         with ExitStack() as ph2:
             sm = ph2.enter_context(tc.tile_pool(name="sm", bufs=2))

@@ -58,6 +58,8 @@ def tile_differentialattention_pa_kernel(tc, x, Wq, Wk, lq1, lq2, lk1, lk2, out)
         comb = const.tile([P, P], F32, name="comb")
         pick = const.tile([P, 2], F32, name="pick")
         slot = const.tile([P, 2], F32, name="slot")
+        lam_pick = const.tile([P, 1], F32, name="lam_pick")
+        moved = [const.tile([P, UNIT, H], F32, name="moved%d" % i) for i in range(2)]
 
         nat_blocks = q_nat[:].rearrange("p (b h k) -> p b k h", b=4, h=4)
         x_blocks = q_x[:].rearrange("p (b h a) -> p b a h", b=4, h=4)
@@ -66,7 +68,7 @@ def tile_differentialattention_pa_kernel(tc, x, Wq, Wk, lq1, lq2, lk1, lk2, out)
         def pad_piece(u, s, j):
             if u not in padded_of:
                 padded_of[u] = padp.tile([P, UA * 64], F32, tag="padded", name="padded")
-            dst = padded_of[u][:].rearrange("p (a s j b h) -> p s j b a h", s=2, j=2, b=4, h=4)
+            dst = padded_of[u][:].rearrange("p (a j s b h) -> p s j b a h", s=2, j=2, b=4, h=4)
             if j == s:
                 src = nat_blocks[:, :, TA * s + UA * u:TA * s + UA * (u + 1), :]
             else:
@@ -126,7 +128,9 @@ def tile_differentialattention_pa_kernel(tc, x, Wq, Wk, lq1, lq2, lk1, lk2, out)
             nc.vector.memset(warm[:, 0:1], 0.0)
             nc.scalar.activation(out=warm[:, 1:2], in_=warm[:, 0:1], func=ACT.Exp)
             nc.vector.memset(comb[:], 0.0)
-            by_row = ident[:].rearrange("p (x j a) -> p x j a", j=2, a=H)
+            for i in range(2):
+                nc.gpsimd.memset(moved[i][:], 0.0)
+            by_row = ident[:].rearrange("p (e j q) -> p e j q", j=2, q=32)
             for j in range(2):
                 nc.vector.tensor_reduce(out=pick[:, j:j + 1], in_=by_row[:, :, j, :], axis=AX.XY, op=ALU.add)
 
@@ -294,10 +298,10 @@ def tile_differentialattention_pa_kernel(tc, x, Wq, Wk, lq1, lq2, lk1, lk2, out)
                     out=neg_lam[:], in0=expd[:, 1, :], scalar=-LAM_INIT, in1=expd[:, 0, :],
                     op0=ALU.add, op1=ALU.subtract,
                 )
-                nc.vector.scalar_tensor_tensor(
-                    out=comb[:, 0:HALF].rearrange("p (t a) -> p t a", a=H),
-                    in0=by_row[:, :, 1, :], scalar=neg_lam[:, 0:1], in1=by_row[:, :, 0, :],
-                    op0=ALU.mult, op1=ALU.add,
+                nc.vector.tensor_tensor(out=lam_pick[:], in0=pick[:, 1:2], in1=neg_lam[:], op=ALU.mult)
+                nc.vector.tensor_tensor(
+                    out=comb[:, 0:HALF].rearrange("p (e q) -> p e q", q=32),
+                    in0=by_row[:, :, 1, :], in1=by_row[:, :, 0, :], op=ALU.add,
                 )
 
             if DEI:
@@ -344,6 +348,8 @@ def tile_differentialattention_pa_kernel(tc, x, Wq, Wk, lq1, lq2, lk1, lk2, out)
 
             k_cols = k_st[:].rearrange("p (m g e) -> p g m e", m=32, e=2)
             out_v = out.rearrange("b n a h -> (b n) a h").rearrange("(g t) a h -> (t a) g h", t=4)
+            out_half = out.rearrange("b n a h -> (b n) a h").rearrange("(g e t) a h -> e (t a) g h", e=2, t=2)
+            att_of = {}
             n_chunks = len(SIZES)
             first = [sum(SIZES[:i]) for i in range(n_chunks)]
             plan = []
@@ -360,6 +366,9 @@ def tile_differentialattention_pa_kernel(tc, x, Wq, Wk, lq1, lq2, lk1, lk2, out)
             low_of = {}
             fin_of = {}
             emitted = [0]
+
+            def by_dma(ch):
+                return SIZES[ch] == UNIT
 
             def score_banks(upto):
                 while emitted[0] < min(upto, n_banks):
@@ -422,7 +431,7 @@ def tile_differentialattention_pa_kernel(tc, x, Wq, Wk, lq1, lq2, lk1, lk2, out)
                 nc.vector.reciprocal(out=rec[:, 0:size, :], in_=tot[:, 0:size, :])
                 own = sm.tile([P, CH, H], F32, tag="own", name="own")
                 nc.vector.scalar_tensor_tensor(
-                    out=own[:, 0:size, :], in0=ex[:, 0:size, H:32], scalar=pick[:, 1:2],
+                    out=own[:, 0:size, :], in0=ex[:, 0:size, H:32], scalar=lam_pick[:, 0:1],
                     in1=low_of[ch][:, 0:size, :], op0=ALU.mult, op1=ALU.add,
                 )
                 att = sm.tile([P, CH, H], F32, tag="att", name="att")
@@ -432,6 +441,14 @@ def tile_differentialattention_pa_kernel(tc, x, Wq, Wk, lq1, lq2, lk1, lk2, out)
                     in1=rec[:, 0:size, :].to_broadcast([P, size, H]),
                     op=ALU.mult,
                 )
+                if by_dma(ch):
+                    mv = moved[ch % 2]
+                    for e in range(2):
+                        nc.sync.dma_start(
+                            out=mv[64 * e:64 * e + 32, 0:size, :], in_=att[64 * e + 32:64 * e + 64, 0:size, :]
+                        )
+                    att_of[ch] = att
+                    return
                 fin = ps_f.tile([P, CH * H], F32, tag="fin", name="fin")
                 nc.tensor.matmul(
                     out=fin[:, 0:size * H],
@@ -441,6 +458,17 @@ def tile_differentialattention_pa_kernel(tc, x, Wq, Wk, lq1, lq2, lk1, lk2, out)
                     stop=True,
                 )
                 fin_of[ch] = fin
+
+            def finish(ch):
+                size = SIZES[ch]
+                res = sm.tile([P, CH, H], F32, tag="res", name="res")
+                nc.vector.tensor_tensor(
+                    out=res[:, 0:size, :], in0=att_of[ch][:, 0:size, :], in1=moved[ch % 2][:, 0:size, :], op=ALU.add
+                )
+                for e in range(2):
+                    nc.sync.dma_start(
+                        out=out_half[e][:, first[ch]:first[ch] + size, :], in_=res[64 * e:64 * e + 32, 0:size, :]
+                    )
 
             def store(ch):
                 size = SIZES[ch]
@@ -458,11 +486,13 @@ def tile_differentialattention_pa_kernel(tc, x, Wq, Wk, lq1, lq2, lk1, lk2, out)
                     leave(ch)
                 if 1 <= ch <= n_chunks:
                     exponent(ch - 1)
-                if ch >= 2:
+                if ch >= 2 and not by_dma(ch - 2):
                     store(ch - 2)
                 if ch < n_chunks:
                     shift(ch)
                 if 1 <= ch <= n_chunks:
                     normalize(ch - 1)
+                if ch >= 2 and by_dma(ch - 2):
+                    finish(ch - 2)
                 if ch + 4 < N_UNITS:
                     prepare(ch + 4)

@@ -30,7 +30,7 @@ UNIT = 16
 UA = 2 * UNIT
 N_UNITS = 8
 DEI = True
-EARLY_UNITS = 1
+EARLY_UNITS = 0
 
 FLOPS = 2 * TOK * C * 2 * C + 2 * TOK * 32 * 32 * D
 
@@ -174,12 +174,7 @@ def tile_differentialattention_pa_kernel(tc, x, Wq, Wk, lq1, lq2, lk1, lk2, out)
                 banks_of[n] = banks
 
             def interleave(n):
-                if n == n_pairs - 1:
-                    on_vector = (1, 3)
-                elif n >= 11:
-                    on_vector = ()
-                else:
-                    on_vector = (3,)
+                on_vector = (1, 3) if n == n_pairs - 1 else (3,)
                 grouped = grp.tile([P, PASSES * 1024], BF16, tag="grouped", name="grouped", align_bytes=64)
                 gw = grouped[:].bitcast(F32).rearrange("p (g c u) -> p g c u", g=PASSES, u=2)
                 for i, (gp, r, tb) in enumerate(banks_of[n]):
@@ -205,12 +200,12 @@ def tile_differentialattention_pa_kernel(tc, x, Wq, Wk, lq1, lq2, lk1, lk2, out)
                     return
                 codes = cdp.tile([P, PASSES * CW], U32, tag="codes", name="codes", align_bytes=64)
                 scales = cdp.tile([P, PASSES * CW], U8, tag="scales", name="scales", align_bytes=64)
-                for g in range(PASSES):
-                    cols = slice(CW * g, CW * g + 256)
+                for gp in range(2):
+                    cols = slice(2 * CW * gp, 2 * CW * (gp + 1))
                     nc.vector.quantize_mx(
                         out=codes[:, cols].bitcast(E4M3),
                         scales=scales[:, cols],
-                        in_=grouped[:, 1024 * g:1024 * (g + 1)],
+                        in_=grouped[:, 2048 * gp:2048 * (gp + 1)],
                     )
                 codes_of[n] = (codes, scales)
 
@@ -262,12 +257,8 @@ def tile_differentialattention_pa_kernel(tc, x, Wq, Wk, lq1, lq2, lk1, lk2, out)
                 stage = stage_of[n]
                 first_map = slice(2 * m, 2 * m + 2)
                 second_map = slice(H + 2 * m, H + 2 * m + 2)
-                if n == n_pairs - 1:
-                    nc.sync.dma_start(out=k_rows[EVEN, first_map, :], in_=stage[EVEN, :, A_TOK])
-                    nc.sync.dma_start(out=k_rows[ODD, second_map, :], in_=stage[ODD, :, B_TOK])
-                else:
-                    nc.vector.tensor_copy(out=k_rows[:, first_map, :], in_=stage[:, :, A_TOK])
-                    nc.vector.tensor_copy(out=k_rows[:, second_map, :], in_=stage[:, :, B_TOK])
+                nc.sync.dma_start(out=k_rows[EVEN, first_map, :], in_=stage[EVEN, :, A_TOK])
+                nc.sync.dma_start(out=k_rows[ODD, second_map, :], in_=stage[ODD, :, B_TOK])
                 nc.sync.dma_start(out=k_rows[ODD, first_map, :], in_=stage[EVEN, :, B_TOK])
                 nc.sync.dma_start(out=k_rows[EVEN, second_map, :], in_=stage[ODD, :, A_TOK])
 
@@ -317,29 +308,27 @@ def tile_differentialattention_pa_kernel(tc, x, Wq, Wk, lq1, lq2, lk1, lk2, out)
                     load(n + 5)
                 if n < n_pairs:
                     interleave(n)
+                    quantize(n)
                     if DEI and n + 2 < n_pairs:
                         deinterleave(n + 2)
-                    quantize(n)
-                if n - 2 in stage_of:
-                    settle_k(n - 2)
                 if n - 1 >= 2:
                     if pairs[n - 1][0] == "q":
                         keep_q(n - 1)
                     else:
                         keep_k(n - 1)
+                        settle_k(n - 1)
                 for u, sp, jp in pads_at.get(n, ()):
                     pad_piece(u, sp, jp)
                 if n + 1 < n_pairs:
                     transposes(n + 1)
                     if not DEI and n + 4 < n_pairs:
                         load(n + 4)
-                    if n == 3:
-                        load_lambda()
-                if n == 5:
+                if n == 13:
+                    load_lambda()
+                if n == 15:
                     exp_dots()
-                if n == 6:
+                if n == 16:
                     make_comb()
-            settle_k(n_pairs - 1)
 
         with ExitStack() as ph2:
             sm = ph2.enter_context(tc.tile_pool(name="sm", bufs=2))

@@ -30,6 +30,10 @@ UNIT = 16
 UA = 2 * UNIT
 N_UNITS = 8
 DEI = True
+IDLE_FILL = 12
+HEAD_FILL = 6
+STEP_FILL = 3
+BY_DMA = 6
 EARLY_UNITS = 0
 
 FLOPS = 2 * TOK * C * 2 * C + 2 * TOK * 32 * 32 * D
@@ -116,6 +120,16 @@ def tile_differentialattention_pa_kernel(tc, x, Wq, Wk, lq1, lq2, lk1, lk2, out)
 
             for n in range(4):
                 load(n)
+
+            zeros = const.tile([P, P], F32, name="zeros")
+            nc.gpsimd.memset(zeros[:], 0.0)
+
+            def fill(count):
+                filler = ps_m.tile([P, TOK], F32, tag="acc", name="acc")
+                for i in range(count):
+                    nc.tensor.matmul(out=filler[:, 0:P], lhsT=zeros[:], rhs=zeros[:], start=True, stop=True)
+
+            fill(HEAD_FILL)
 
             ident = const.tile([P, P], F32, name="ident")
             masks.make_identity(nc, ident[:])
@@ -298,12 +312,15 @@ def tile_differentialattention_pa_kernel(tc, x, Wq, Wk, lq1, lq2, lk1, lk2, out)
             if DEI:
                 deinterleave(0)
             transposes(0)
+            fill(STEP_FILL)
             if DEI:
                 deinterleave(1)
             load(4)
             for n in range(n_pairs + 1):
                 if n - 1 >= 2:
                     project(n - 1)
+                if n == n_pairs:
+                    fill(IDLE_FILL)
                 if DEI and n + 5 < n_pairs:
                     load(n + 5)
                 if n < n_pairs:
@@ -321,6 +338,8 @@ def tile_differentialattention_pa_kernel(tc, x, Wq, Wk, lq1, lq2, lk1, lk2, out)
                     pad_piece(u, sp, jp)
                 if n + 1 < n_pairs:
                     transposes(n + 1)
+                    if n < 2:
+                        fill(STEP_FILL)
                     if not DEI and n + 4 < n_pairs:
                         load(n + 4)
                 if n == 13:
@@ -357,7 +376,7 @@ def tile_differentialattention_pa_kernel(tc, x, Wq, Wk, lq1, lq2, lk1, lk2, out)
             emitted = [0]
 
             def by_dma(ch):
-                return SIZES[ch] == UNIT
+                return ch < BY_DMA
 
             def score_banks(upto):
                 while emitted[0] < min(upto, n_banks):

@@ -24,7 +24,7 @@ PASSES = 4
 SCALE = 0.125
 LAM_INIT = 0.8 - 0.6 * 2.718281828459045 ** (-3.6)
 CW = 256
-SIZES = [16] * 7 + [8, 4, 4]
+SIZES = [16] * 7 + [12, 4]
 GB = 8
 UNIT = 16
 UA = 2 * UNIT
@@ -34,6 +34,7 @@ IDLE_FILL = 12
 HEAD_FILL = 6
 STEP_FILL = 3
 BY_DMA = 6
+FINE = 3
 EARLY_UNITS = 0
 
 FLOPS = 2 * TOK * C * 2 * C + 2 * TOK * 32 * 32 * D
@@ -99,7 +100,6 @@ def tile_differentialattention_pa_kernel(tc, x, Wq, Wk, lq1, lq2, lk1, lk2, out)
 
             raw_of = {}
             dei_of = {}
-            stage_of = {}
             banks_of = {}
             grouped_of = {}
             codes_of = {}
@@ -109,7 +109,7 @@ def tile_differentialattention_pa_kernel(tc, x, Wq, Wk, lq1, lq2, lk1, lk2, out)
                 kind, src, m = pairs[n]
                 raw = rawp.tile([P, 2, C], BF16, tag="raw", name="raw")
                 rows = src[256 * m:256 * (m + 1), :].rearrange("(r p) k -> p r k", p=P)
-                if n == 0:
+                if n < FINE:
                     for gp in range(2):
                         for r in range(2):
                             cols = slice(1024 * gp, 1024 * (gp + 1))
@@ -157,7 +157,7 @@ def tile_differentialattention_pa_kernel(tc, x, Wq, Wk, lq1, lq2, lk1, lk2, out)
             def deinterleave(n):
                 words = raw_of[n][:].bitcast(F32)
                 dei = deip.tile([P, 2, C // 2], F32, tag="dei", name="dei")
-                parts = 2 if n == 0 else 1
+                parts = 2 if n < FINE else 1
                 width = (C // 2) // parts
                 for part in range(parts):
                     for r in range(2):
@@ -264,17 +264,19 @@ def tile_differentialattention_pa_kernel(tc, x, Wq, Wk, lq1, lq2, lk1, lk2, out)
                         nc.vector.tensor_copy(out=stage[:, r, :], in_=acc[:])
                     else:
                         nc.scalar.copy(out=stage[:, r, :], in_=acc[:])
-                stage_of[n] = stage
+                    if last:
+                        settle_k(n, stage, slice(r, r + 1))
+                if not last:
+                    settle_k(n, stage, slice(0, 2))
 
-            def settle_k(n):
+            def settle_k(n, stage, heads):
                 m = pairs[n][2]
-                stage = stage_of[n]
-                first_map = slice(2 * m, 2 * m + 2)
-                second_map = slice(H + 2 * m, H + 2 * m + 2)
-                nc.sync.dma_start(out=k_rows[EVEN, first_map, :], in_=stage[EVEN, :, A_TOK])
-                nc.sync.dma_start(out=k_rows[ODD, second_map, :], in_=stage[ODD, :, B_TOK])
-                nc.sync.dma_start(out=k_rows[ODD, first_map, :], in_=stage[EVEN, :, B_TOK])
-                nc.sync.dma_start(out=k_rows[EVEN, second_map, :], in_=stage[ODD, :, A_TOK])
+                first_map = slice(2 * m + heads.start, 2 * m + heads.stop)
+                second_map = slice(H + 2 * m + heads.start, H + 2 * m + heads.stop)
+                nc.sync.dma_start(out=k_rows[EVEN, first_map, :], in_=stage[EVEN, heads, A_TOK])
+                nc.sync.dma_start(out=k_rows[ODD, second_map, :], in_=stage[ODD, heads, B_TOK])
+                nc.sync.dma_start(out=k_rows[ODD, first_map, :], in_=stage[EVEN, heads, B_TOK])
+                nc.sync.dma_start(out=k_rows[EVEN, second_map, :], in_=stage[ODD, heads, A_TOK])
 
             early = [(u, sj[0], sj[1]) for u in range(EARLY_UNITS) for sj in PIECES]
             per_step = -(-len(early) // 6)
@@ -333,7 +335,6 @@ def tile_differentialattention_pa_kernel(tc, x, Wq, Wk, lq1, lq2, lk1, lk2, out)
                         keep_q(n - 1)
                     else:
                         keep_k(n - 1)
-                        settle_k(n - 1)
                 for u, sp, jp in pads_at.get(n, ()):
                     pad_piece(u, sp, jp)
                 if n + 1 < n_pairs:

@@ -31,8 +31,8 @@ UA = 2 * UNIT
 N_UNITS = 8
 DEI = True
 IDLE_FILL = 12
-HEAD_FILL = 6
-STEP_FILL = 3
+HEAD_FILL = 4
+STEP_FILL = 2
 BY_DMA = 6
 FINE = 3
 EARLY_UNITS = 0
@@ -122,12 +122,18 @@ def tile_differentialattention_pa_kernel(tc, x, Wq, Wk, lq1, lq2, lk1, lk2, out)
                 load(n)
 
             zeros = const.tile([P, P], F32, name="zeros")
+
+            zeros_bf = const.tile([P, TOK], BF16, name="zeros_bf")
+            nc.gpsimd.memset(zeros_bf[:], 0.0)
             nc.gpsimd.memset(zeros[:], 0.0)
 
-            def fill(count):
+            def fill(count, wide=True):
                 filler = ps_m.tile([P, TOK], F32, tag="acc", name="acc")
                 for i in range(count):
-                    nc.tensor.matmul(out=filler[:, 0:P], lhsT=zeros[:], rhs=zeros[:], start=True, stop=True)
+                    if wide:
+                        nc.tensor.matmul(out=filler[:], lhsT=zeros_bf[:, 0:P], rhs=zeros_bf[:], start=True, stop=True)
+                    else:
+                        nc.tensor.matmul(out=filler[:, 0:64], lhsT=zeros[:], rhs=zeros[:, 0:64], start=True, stop=True)
 
             fill(HEAD_FILL)
 
@@ -322,7 +328,7 @@ def tile_differentialattention_pa_kernel(tc, x, Wq, Wk, lq1, lq2, lk1, lk2, out)
                 if n - 1 >= 2:
                     project(n - 1)
                 if n == n_pairs:
-                    fill(IDLE_FILL)
+                    fill(IDLE_FILL, False)
                 if DEI and n + 5 < n_pairs:
                     load(n + 5)
                 if n < n_pairs:

@@ -30,12 +30,14 @@ UNIT = 16
 UA = 2 * UNIT
 N_UNITS = 8
 DEI = True
-IDLE_FILL = 12
+IDLE_FILL = 0
 HEAD_FILL = 4
 STEP_FILL = 2
+SCALAR_FROM = 6
 BY_DMA = 6
-FINE = 3
+FINE = 5
 EARLY_UNITS = 0
+DEI_FROM = 4
 
 FLOPS = 2 * TOK * C * 2 * C + 2 * TOK * 32 * 32 * D
 
@@ -64,6 +66,8 @@ def tile_differentialattention_pa_kernel(tc, x, Wq, Wk, lq1, lq2, lk1, lk2, out)
         pick = const.tile([P, 2], F32, name="pick")
         slot = const.tile([P, 2], F32, name="slot")
         lam_pick = const.tile([P, 1], F32, name="lam_pick")
+        swap = const.tile([P, P], F32, name="swap")
+        parity = const.tile([P, 2], F32, name="parity")
         moved = [const.tile([P, UNIT, H], F32, name="moved%d" % i) for i in range(2)]
 
         nat_blocks = q_nat[:].rearrange("p (b h k) -> p b k h", b=4, h=4)
@@ -90,8 +94,8 @@ def tile_differentialattention_pa_kernel(tc, x, Wq, Wk, lq1, lq2, lk1, lk2, out)
 
         with ExitStack() as ph1:
             one = ph1.enter_context(tc.tile_pool(name="one", bufs=1))
-            rawp = ph1.enter_context(tc.tile_pool(name="rawp", bufs=4))
-            grp = ph1.enter_context(tc.tile_pool(name="grp", bufs=2))
+            rawp = ph1.enter_context(tc.tile_pool(name="rawp", bufs=5))
+            grp = ph1.enter_context(tc.tile_pool(name="grp", bufs=4))
             deip = ph1.enter_context(tc.tile_pool(name="deip", bufs=2)) if DEI else None
             cdp = ph1.enter_context(tc.tile_pool(name="cdp", bufs=2))
             stp = ph1.enter_context(tc.tile_pool(name="stp", bufs=3))
@@ -105,21 +109,23 @@ def tile_differentialattention_pa_kernel(tc, x, Wq, Wk, lq1, lq2, lk1, lk2, out)
             codes_of = {}
             acc_of = {}
 
-            def load(n):
+            def load(n, gps=(0, 1)):
                 kind, src, m = pairs[n]
-                raw = rawp.tile([P, 2, C], BF16, tag="raw", name="raw")
+                if n not in raw_of:
+                    raw_of[n] = rawp.tile([P, 2, C], BF16, tag="raw", name="raw")
+                raw = raw_of[n]
                 rows = src[256 * m:256 * (m + 1), :].rearrange("(r p) k -> p r k", p=P)
                 if n < FINE:
-                    for gp in range(2):
+                    for gp in gps:
                         for r in range(2):
                             cols = slice(1024 * gp, 1024 * (gp + 1))
                             nc.sync.dma_start(out=raw[:, r, cols], in_=rows[:, r, cols])
                 else:
                     nc.sync.dma_start(out=raw[:], in_=rows)
-                raw_of[n] = raw
 
-            for n in range(4):
-                load(n)
+            for n, gp in ((0, 0), (1, 0), (2, 0), (0, 1), (1, 1), (2, 1), (3, 0), (3, 1)):
+                load(n, (gp,))
+            load(4)
 
             zeros = const.tile([P, P], F32, name="zeros")
 
@@ -139,7 +145,6 @@ def tile_differentialattention_pa_kernel(tc, x, Wq, Wk, lq1, lq2, lk1, lk2, out)
 
             ident = const.tile([P, P], F32, name="ident")
             masks.make_identity(nc, ident[:])
-            parity = const.tile([P, 2], F32, name="parity")
             by_parity = ident[:].rearrange("p (d j) -> p j d", j=2)
             for sp in range(2):
                 nc.vector.tensor_reduce(out=parity[:, sp:sp + 1], in_=by_parity[:, sp, :], axis=AX.X, op=ALU.add)
@@ -160,94 +165,101 @@ def tile_differentialattention_pa_kernel(tc, x, Wq, Wk, lq1, lq2, lk1, lk2, out)
             def windows(n):
                 return (0, 128)
 
-            def deinterleave(n):
+            def deinterleave(n, gps=(0, 1)):
+                if n < DEI_FROM:
+                    return
                 words = raw_of[n][:].bitcast(F32)
-                dei = deip.tile([P, 2, C // 2], F32, tag="dei", name="dei")
-                parts = 2 if n < FINE else 1
-                width = (C // 2) // parts
-                for part in range(parts):
+                if n not in dei_of:
+                    dei_of[n] = deip.tile([P, 2, C // 2], F32, tag="dei", name="dei")
+                dei = dei_of[n]
+                spans = [slice(512 * gp, 512 * (gp + 1)) for gp in gps] if n < FINE else [slice(0, C // 2)]
+                for cols in spans:
                     for r in range(2):
-                        cols = slice(width * part, width * (part + 1))
                         nc.vector.tensor_copy(
                             out=dei[:, r, cols].rearrange("p (g u c) -> p g u c", u=2, c=P),
                             in_=words[:, r, cols].rearrange("p (g c u) -> p g u c", u=2, c=P),
                         )
-                dei_of[n] = dei
 
-            def transposes(n):
-                moving = ident
+            def transposes(n, gps=(0, 1)):
                 words = raw_of[n][:].bitcast(F32)
-                banks = []
-                for gp in range(2):
+                banks = banks_of.setdefault(n, [])
+                for gp in gps:
                     for r in range(2):
                         tb = ps_t.tile([P, 512], F32, tag="tb", name="tb")
                         for gg in range(2):
                             for u in range(2):
                                 base = 256 * (2 * gp + gg)
                                 col = 128 * (2 * gg + u)
-                                if DEI:
+                                if n >= DEI_FROM:
                                     turned = dei_of[n][:, r, base + 128 * u:base + 128 * (u + 1)]
                                 else:
                                     turned = words[:, r, base + u:base + 256:2]
-                                nc.tensor.transpose(tb[:, col:col + 128], turned, moving[:])
+                                nc.tensor.transpose(tb[:, col:col + 128], turned, ident[:])
                         banks.append((gp, r, tb))
-                banks_of[n] = banks
 
-            def interleave(n):
+            def interleave(n, gps=(0, 1)):
                 on_vector = (1, 3) if n == n_pairs - 1 else (3,)
-                grouped = grp.tile([P, PASSES * 1024], BF16, tag="grouped", name="grouped", align_bytes=64)
-                gw = grouped[:].bitcast(F32).rearrange("p (g c u) -> p g c u", g=PASSES, u=2)
-                for i, (gp, r, tb) in enumerate(banks_of[n]):
-                    dst = gw[:, 2 * gp:2 * gp + 2, 128 * r:128 * r + 128, :]
-                    src = tb[:].rearrange("p (g u c) -> p g c u", g=2, u=2)
-                    if i in on_vector:
-                        nc.vector.tensor_copy(out=dst, in_=src)
-                    else:
-                        nc.scalar.copy(out=dst, in_=src)
-                grouped_of[n] = grouped
+                for gp in gps:
+                    grouped = grp.tile([P, 2048], BF16, tag="grouped", name="grouped", align_bytes=64)
+                    gw = grouped[:].bitcast(F32).rearrange("p (g c u) -> p g c u", g=2, u=2)
+                    for bgp, r, tb in banks_of[n]:
+                        if bgp != gp:
+                            continue
+                        dst = gw[:, :, 128 * r:128 * r + 128, :]
+                        src = tb[:].rearrange("p (g u c) -> p g c u", g=2, u=2)
+                        if 2 * gp + r in on_vector:
+                            nc.vector.tensor_copy(out=dst, in_=src)
+                        else:
+                            nc.scalar.copy(out=dst, in_=src)
+                    grouped_of[(n, gp)] = grouped
 
-            def quantize(n):
+            def quantize(n, gps=(0, 1)):
                 kind, src, m = pairs[n]
-                grouped = grouped_of[n]
                 if kind == "x":
-                    for g in range(PASSES):
-                        cols = slice(TOK * g + TA * n, TOK * g + TA * (n + 1))
-                        nc.vector.quantize_mx(
-                            out=x_codes[:, cols].bitcast(E5M2),
-                            scales=x_scales[:, cols],
-                            in_=grouped[:, 1024 * g:1024 * (g + 1)],
-                        )
+                    for gp in gps:
+                        for gg in range(2):
+                            g = 2 * gp + gg
+                            cols = slice(TOK * g + TA * n, TOK * g + TA * (n + 1))
+                            nc.vector.quantize_mx(
+                                out=x_codes[:, cols].bitcast(E5M2),
+                                scales=x_scales[:, cols],
+                                in_=grouped_of[(n, gp)][:, 1024 * gg:1024 * (gg + 1)],
+                            )
                     return
-                codes = cdp.tile([P, PASSES * CW], U32, tag="codes", name="codes", align_bytes=64)
-                scales = cdp.tile([P, PASSES * CW], U8, tag="scales", name="scales", align_bytes=64)
-                for gp in range(2):
+                if n not in codes_of:
+                    codes = cdp.tile([P, PASSES * CW], U32, tag="codes", name="codes", align_bytes=64)
+                    scales = cdp.tile([P, PASSES * CW], U8, tag="scales", name="scales", align_bytes=64)
+                    codes_of[n] = (codes, scales)
+                codes, scales = codes_of[n]
+                for gp in gps:
                     cols = slice(2 * CW * gp, 2 * CW * (gp + 1))
                     nc.vector.quantize_mx(
                         out=codes[:, cols].bitcast(E4M3),
                         scales=scales[:, cols],
-                        in_=grouped[:, 2048 * gp:2048 * (gp + 1)],
+                        in_=grouped_of[(n, gp)][:],
                     )
-                codes_of[n] = (codes, scales)
 
-            def project(n):
+            def project(n, gps=(0, 1)):
                 codes, scales = codes_of[n]
-                accs = []
-                for w in windows(n):
-                    acc = ps_m.tile([P, TOK], F32, tag="acc", name="acc")
-                    for g in range(PASSES):
-                        cols = slice(CW * g + w, CW * g + w + 128)
-                        toks = slice(TOK * g, TOK * (g + 1))
-                        nc.tensor.matmul_mx(
-                            out=acc[:],
-                            lhsT=codes[:, cols].bitcast(E4M3),
-                            lhsT_scale=scales[:, cols],
-                            rhs=x_codes[:, toks].bitcast(E5M2),
-                            rhs_scale=x_scales[:, toks],
-                            start=(g == 0),
-                            stop=(g == PASSES - 1),
-                        )
-                    accs.append((w, acc))
-                acc_of[n] = accs
+                if n not in acc_of:
+                    acc_of[n] = []
+                    for w in windows(n):
+                        acc = ps_m.tile([P, TOK], F32, tag="acc", name="acc")
+                        acc_of[n].append((w, acc))
+                for w, acc in acc_of[n]:
+                    for gp in gps:
+                        for g in (2 * gp, 2 * gp + 1):
+                            cols = slice(CW * g + w, CW * g + w + 128)
+                            toks = slice(TOK * g, TOK * (g + 1))
+                            nc.tensor.matmul_mx(
+                                out=acc[:],
+                                lhsT=codes[:, cols].bitcast(E4M3),
+                                lhsT_scale=scales[:, cols],
+                                rhs=x_codes[:, toks].bitcast(E5M2),
+                                rhs_scale=x_scales[:, toks],
+                                start=(g == 0),
+                                stop=(g == PASSES - 1),
+                            )
 
             EVEN = slice(0, P, 2)
             ODD = slice(1, P, 2)
@@ -267,13 +279,33 @@ def tile_differentialattention_pa_kernel(tc, x, Wq, Wk, lq1, lq2, lk1, lk2, out)
                 stage = stp.tile([P, 2, TOK], F32, tag="stage", name="stage")
                 for r, (w, acc) in enumerate(acc_of[n]):
                     if last and r == 1:
-                        nc.vector.tensor_copy(out=stage[:, r, :], in_=acc[:])
-                    else:
-                        nc.scalar.copy(out=stage[:, r, :], in_=acc[:])
+                        cross_on_tensor(n, stage, acc)
+                        continue
+                    nc.scalar.copy(out=stage[:, r, :], in_=acc[:])
                     if last:
                         settle_k(n, stage, slice(r, r + 1))
                 if not last:
                     settle_k(n, stage, slice(0, 2))
+
+            def cross_on_tensor(n, stage, acc):
+                head = 2 * pairs[n][2] + 1
+                swapped = {}
+                for name, toks in (("a", A_TOK), ("b", B_TOK)):
+                    nc.scalar.copy(out=stage[:, 1, toks], in_=acc[:, toks])
+                    sw = ps_m.tile([P, TOK], F32, tag="acc", name="acc")
+                    nc.tensor.matmul(out=sw[:, 0:TA], lhsT=swap[:], rhs=stage[:, 1, toks], start=True, stop=True)
+                    swapped[name] = sw
+                own = stp.tile([P, 2, TOK], F32, tag="stage", name="stage")
+                nc.scalar.activation(out=own[:, 1, 0:TA], in_=acc[:, B_TOK], func=ACT.Copy, scale=parity[:, 1:2])
+                nc.scalar.activation(out=own[:, 0, 0:TA], in_=acc[:, A_TOK], func=ACT.Copy, scale=parity[:, 0:1])
+                nc.vector.scalar_tensor_tensor(
+                    out=k_rows[:, H + head, :], in0=swapped["a"][:, 0:TA], scalar=parity[:, 0:1], in1=own[:, 1, 0:TA],
+                    op0=ALU.mult, op1=ALU.add,
+                )
+                nc.vector.scalar_tensor_tensor(
+                    out=k_rows[:, head, :], in0=swapped["b"][:, 0:TA], scalar=parity[:, 1:2], in1=own[:, 0, 0:TA],
+                    op0=ALU.mult, op1=ALU.add,
+                )
 
             def settle_k(n, stage, heads):
                 m = pairs[n][2]
@@ -317,18 +349,48 @@ def tile_differentialattention_pa_kernel(tc, x, Wq, Wk, lq1, lq2, lk1, lk2, out)
                     in0=by_row[:, :, 1, :], in1=by_row[:, :, 0, :], op=ALU.add,
                 )
 
-            if DEI:
-                deinterleave(0)
-            transposes(0)
+            LO = (0,)
+            HI = (1,)
+            transposes(0, LO)
+            transposes(1, LO)
             fill(STEP_FILL)
-            if DEI:
-                deinterleave(1)
-            load(4)
-            for n in range(n_pairs + 1):
+            interleave(0, LO)
+            interleave(1, LO)
+            quantize(0, LO)
+            quantize(1, LO)
+            transposes(2, LO)
+            transposes(0, HI)
+            fill(STEP_FILL)
+            load(5)
+            interleave(2, LO)
+            quantize(2, LO)
+            interleave(0, HI)
+            quantize(0, HI)
+            transposes(1, HI)
+            load(6)
+            project(2, LO)
+            interleave(1, HI)
+            quantize(1, HI)
+            transposes(2, HI)
+            load(7)
+            transposes(3, LO)
+            interleave(2, HI)
+            quantize(2, HI)
+            deinterleave(4, LO)
+            interleave(3, LO)
+            quantize(3, LO)
+            project(2, HI)
+            deinterleave(4, HI)
+            keep_q(2)
+            transposes(3, HI)
+            load(8)
+            interleave(3, HI)
+            quantize(3, HI)
+            deinterleave(5)
+            transposes(4)
+            for n in range(4, n_pairs + 1):
                 if n - 1 >= 2:
                     project(n - 1)
-                if n == n_pairs:
-                    fill(IDLE_FILL, False)
                 if DEI and n + 5 < n_pairs:
                     load(n + 5)
                 if n < n_pairs:
@@ -345,12 +407,18 @@ def tile_differentialattention_pa_kernel(tc, x, Wq, Wk, lq1, lq2, lk1, lk2, out)
                     pad_piece(u, sp, jp)
                 if n + 1 < n_pairs:
                     transposes(n + 1)
-                    if n < 2:
-                        fill(STEP_FILL)
                     if not DEI and n + 4 < n_pairs:
                         load(n + 4)
                 if n == 13:
                     load_lambda()
+                if n == 14:
+                    for j in range(2):
+                        nc.vector.tensor_copy(
+                            out=swap[:].rearrange("p (d j) -> p d j", j=2)[:, :, j],
+                            in_=ident[:].rearrange("p (d j) -> p d j", j=2)[:, :, 1 - j],
+                        )
+                if n == n_pairs - 1:
+                    prepare(0)
                 if n == 15:
                     exp_dots()
                 if n == 16:
@@ -377,6 +445,8 @@ def tile_differentialattention_pa_kernel(tc, x, Wq, Wk, lq1, lq2, lk1, lk2, out)
             bank_of = {}
             sc_of = {}
             sd_of = {}
+            neg_of = {}
+            tot_of = {}
             exp_of = {}
             low_of = {}
             fin_of = {}
@@ -419,6 +489,13 @@ def tile_differentialattention_pa_kernel(tc, x, Wq, Wk, lq1, lq2, lk1, lk2, out)
                 sc = sc_of[ch]
                 top = sm.tile([P, CH, 1], F32, tag="top", name="top")
                 nc.vector.tensor_reduce(out=top[:, 0:size, :], in_=sc[:, 0:size, :], axis=AX.X, op=ALU.max)
+                if ch >= SCALAR_FROM:
+                    neg = sm.tile([P, CH, 1], F32, tag="neg", name="neg")
+                    nc.vector.tensor_scalar(
+                        out=neg[:, 0:size, :], in0=top[:, 0:size, :], scalar1=-1.0, scalar2=None, op0=ALU.mult
+                    )
+                    neg_of[ch] = neg
+                    return
                 sd = sm.tile([P, CH, 32], F32, tag="sd", name="sd")
                 nc.vector.tensor_tensor(
                     out=sd[:, 0:size, :], in0=sc[:, 0:size, :],
@@ -429,21 +506,41 @@ def tile_differentialattention_pa_kernel(tc, x, Wq, Wk, lq1, lq2, lk1, lk2, out)
             def exponent(ch):
                 size = SIZES[ch]
                 ex = sm.tile([P, CH, 32], F32, tag="ex", name="ex")
-                nc.scalar.activation(out=ex[:, 0:size, :], in_=sd_of[ch][:, 0:size, :], func=ACT.Exp)
+                if ch >= SCALAR_FROM:
+                    tot = sm.tile([P, CH, 1], F32, tag="tot", name="tot")
+                    for g in range(size):
+                        nc.scalar.activation(
+                            out=ex[:, g, :], in_=sc_of[ch][:, g, :], func=ACT.Exp, bias=neg_of[ch][:, g, :], scale=1.0,
+                            accum_out=tot[:, g, :],
+                        )
+                    tot_of[ch] = tot
+                else:
+                    nc.scalar.activation(out=ex[:, 0:size, :], in_=sd_of[ch][:, 0:size, :], func=ACT.Exp)
+                exp_of[ch] = ex
+                if ch >= SCALAR_FROM:
+                    return
                 low = sm.tile([P, CH, H], F32, tag="low", name="low")
                 nc.scalar.activation(
                     out=low[:, 0:size, :], in_=ex[:, 0:size, 0:H], func=ACT.Copy, scale=pick[:, 0:1]
                 )
-                exp_of[ch] = ex
                 low_of[ch] = low
 
             def normalize(ch):
                 size = SIZES[ch]
                 ex = exp_of[ch]
-                tot = sm.tile([P, CH, 1], F32, tag="tot", name="tot")
-                nc.vector.tensor_reduce(out=tot[:, 0:size, :], in_=ex[:, 0:size, :], axis=AX.X, op=ALU.add)
+                if ch >= SCALAR_FROM:
+                    tot = tot_of[ch]
+                else:
+                    tot = sm.tile([P, CH, 1], F32, tag="tot", name="tot")
+                    nc.vector.tensor_reduce(out=tot[:, 0:size, :], in_=ex[:, 0:size, :], axis=AX.X, op=ALU.add)
                 rec = sm.tile([P, CH, 1], F32, tag="rec", name="rec")
                 nc.vector.reciprocal(out=rec[:, 0:size, :], in_=tot[:, 0:size, :])
+                if ch >= SCALAR_FROM:
+                    low = sm.tile([P, CH, H], F32, tag="low", name="low")
+                    nc.vector.tensor_scalar(
+                        out=low[:, 0:size, :], in0=ex[:, 0:size, 0:H], scalar1=pick[:, 0:1], scalar2=None, op0=ALU.mult
+                    )
+                    low_of[ch] = low
                 own = sm.tile([P, CH, H], F32, tag="own", name="own")
                 nc.vector.scalar_tensor_tensor(
                     out=own[:, 0:size, :], in0=ex[:, 0:size, H:32], scalar=lam_pick[:, 0:1],
@@ -493,7 +590,7 @@ def tile_differentialattention_pa_kernel(tc, x, Wq, Wk, lq1, lq2, lk1, lk2, out)
                 )
                 nc.sync.dma_start(out=out_v[:, first[ch]:first[ch] + size, :], in_=res[0:HALF, 0:size, :])
 
-            for u in range(EARLY_UNITS, 4):
+            for u in range(1, 4):
                 prepare(u)
             for ch in range(n_chunks + 2):
                 if ch < n_chunks:
@@ -501,7 +598,9 @@ def tile_differentialattention_pa_kernel(tc, x, Wq, Wk, lq1, lq2, lk1, lk2, out)
                     leave(ch)
                 if 1 <= ch <= n_chunks:
                     exponent(ch - 1)
-                if ch >= 2 and not by_dma(ch - 2):
+                if ch == n_chunks:
+                    store(ch - 3)
+                if ch >= 2 and not by_dma(ch - 2) and ch != n_chunks - 1:
                     store(ch - 2)
                 if ch < n_chunks:
                     shift(ch)

@@ -593,18 +593,23 @@ def tile_differentialattention_pa_kernel(tc, x, Wq, Wk, lq1, lq2, lk1, lk2, out)
             for u in range(1, 4):
                 prepare(u)
             for ch in range(n_chunks + 2):
+                ahead = ch == n_chunks - 2
                 if ch < n_chunks:
                     score_banks(first_bank[ch] + 6)
-                    leave(ch)
+                    if not ahead:
+                        leave(ch)
                 if 1 <= ch <= n_chunks:
                     exponent(ch - 1)
+                if ahead:
+                    normalize(ch - 1)
+                    leave(ch)
                 if ch == n_chunks:
                     store(ch - 3)
                 if ch >= 2 and not by_dma(ch - 2) and ch != n_chunks - 1:
                     store(ch - 2)
                 if ch < n_chunks:
                     shift(ch)
-                if 1 <= ch <= n_chunks:
+                if 1 <= ch <= n_chunks and not ahead:
                     normalize(ch - 1)
                 if ch >= 2 and by_dma(ch - 2):
                     finish(ch - 2)

@@ -14,54 +14,59 @@ ACT = mybir.ActivationFunctionType
 AX = mybir.AxisListType
 
 P = 128
-HALF = 64
-C = 2048
+HALF_P = 64
+K = 2048
 H = 16
+ROWS = 32
 D = 64
 TOK = 512
 TA = 256
 PASSES = 4
+CW = 256
 SCALE = 0.125
 LAM_INIT = 0.8 - 0.6 * 2.718281828459045 ** (-3.6)
-CW = 256
-SIZES = [16] * 7 + [12, 4]
-GB = 8
-UNIT = 16
-UA = 2 * UNIT
-N_UNITS = 8
-DEI = True
-IDLE_FILL = 0
-HEAD_FILL = 4
-STEP_FILL = 2
-SCALAR_FROM = 6
-BY_DMA = 6
-FINE = 5
-EARLY_UNITS = 0
-DEI_FROM = 4
 
-FLOPS = 2 * TOK * C * 2 * C + 2 * TOK * 32 * 32 * D
+LO = (0,)
+HI = (1,)
+BOTH = (0, 1)
+N_PIECEWISE = 5
+N_STEPPED = 4
+WARM_UP = 4
+KEEP_WARM = 2
+
+GROUPS_IN_BANK = 8
+UNIT = 16
+UNIT_PAIRS = 2 * UNIT
+N_UNITS = 8
+CHUNKS = [16] * 7 + [12, 4]
+BANKS_AHEAD = 6
+N_BY_DMA = 6
+SHORT_EXP_FROM = 5
+
+FLOPS = 2 * TOK * K * 2 * K + 2 * TOK * ROWS * ROWS * D
 
 
 def tile_differentialattention_pa_kernel(tc, x, Wq, Wk, lq1, lq2, lk1, lk2, out):
     nc = tc.nc
     x_by_parity = x.flatten_outer_dims().rearrange("(a s) k -> s a k", s=2)
-    pairs = [("x", x_by_parity[s], 0) for s in range(2)]
-    pairs += [("q", Wq, m) for m in range(8)]
-    pairs += [("k", Wk, m) for m in range(8)]
-    n_pairs = len(pairs)
+    slabs = [("x", x_by_parity[s], 0) for s in range(2)]
+    slabs += [("q", Wq, m) for m in range(8)]
+    slabs += [("k", Wk, m) for m in range(8)]
+    n_slabs = len(slabs)
+    last_slab = n_slabs - 1
 
     with ExitStack() as ctx:
         const = ctx.enter_context(tc.tile_pool(name="const", bufs=1))
-        big = ctx.enter_context(tc.tile_pool(name="big", bufs=1))
-        padp = ctx.enter_context(tc.tile_pool(name="padp", bufs=4))
+        kept = ctx.enter_context(tc.tile_pool(name="kept", bufs=1))
+        pad_pool = ctx.enter_context(tc.tile_pool(name="pad_pool", bufs=4))
         ctx.enter_context(tc.manual_schedule())
 
-        k_st = big.tile([P, 32 * TA], F32, name="k_st")
-        k_rows = k_st[:].rearrange("p (m a) -> p m a", m=32)
-        q_nat = big.tile([P, H * TOK], F32, name="q_nat")
-        q_x = big.tile([P, H * TA], F32, name="q_x")
-        q_nat_rows = q_nat[:].rearrange("p (h k) -> p h k", h=H)
-        q_x_rows = q_x[:].rearrange("p (h a) -> p h a", h=H)
+        k_all = kept.tile([P, ROWS * TA], F32, name="k_all")
+        k_rows = k_all[:].rearrange("p (m a) -> p m a", m=ROWS)
+        q_own = kept.tile([P, H * TOK], F32, name="q_own")
+        q_own_rows = q_own[:].rearrange("p (h tok) -> p h tok", h=H)
+        q_crossed = kept.tile([P, H * TA], F32, name="q_crossed")
+        q_crossed_rows = q_crossed[:].rearrange("p (h a) -> p h a", h=H)
         comb = const.tile([P, P], F32, name="comb")
         pick = const.tile([P, 2], F32, name="pick")
         slot = const.tile([P, 2], F32, name="slot")
@@ -70,84 +75,72 @@ def tile_differentialattention_pa_kernel(tc, x, Wq, Wk, lq1, lq2, lk1, lk2, out)
         parity = const.tile([P, 2], F32, name="parity")
         moved = [const.tile([P, UNIT, H], F32, name="moved%d" % i) for i in range(2)]
 
-        nat_blocks = q_nat[:].rearrange("p (b h k) -> p b k h", b=4, h=4)
-        x_blocks = q_x[:].rearrange("p (b h a) -> p b a h", b=4, h=4)
+        own_blocks = q_own[:].rearrange("p (hb hl tok) -> p hb tok hl", hb=4, hl=4)
+        crossed_blocks = q_crossed[:].rearrange("p (hb hl a) -> p hb a hl", hb=4, hl=4)
         padded_of = {}
 
-        def pad_piece(u, s, j):
-            if u not in padded_of:
-                padded_of[u] = padp.tile([P, UA * 64], F32, tag="padded", name="padded")
-            dst = padded_of[u][:].rearrange("p (a j s b h) -> p s j b a h", s=2, j=2, b=4, h=4)
-            if j == s:
-                src = nat_blocks[:, :, TA * s + UA * u:TA * s + UA * (u + 1), :]
-            else:
-                src = x_blocks[:, :, UA * u:UA * (u + 1), :]
-            nc.vector.tensor_scalar(
-                out=dst[:, s, j], in0=src, scalar1=slot[:, s:s + 1], scalar2=None, op0=ALU.mult,
-            )
+        def prepare(unit):
+            padded_of[unit] = pad_pool.tile([P, UNIT_PAIRS * 64], F32, name="padded")
+            dst = padded_of[unit][:].rearrange("p (a j s hb hl) -> p s j hb a hl", s=2, j=2, hb=4, hl=4)
+            for s, j in ((0, 0), (1, 1), (0, 1), (1, 0)):
+                if j == s:
+                    src = own_blocks[:, :, TA * s + UNIT_PAIRS * unit:TA * s + UNIT_PAIRS * (unit + 1), :]
+                else:
+                    src = crossed_blocks[:, :, UNIT_PAIRS * unit:UNIT_PAIRS * (unit + 1), :]
+                nc.vector.tensor_scalar(
+                    out=dst[:, s, j], in0=src, scalar1=slot[:, s:s + 1], scalar2=None, op0=ALU.mult,
+                )
 
-        PIECES = ((0, 0), (1, 1), (0, 1), (1, 0))
-
-        def prepare(u):
-            for s, j in PIECES:
-                pad_piece(u, s, j)
-
-        with ExitStack() as ph1:
-            one = ph1.enter_context(tc.tile_pool(name="one", bufs=1))
-            rawp = ph1.enter_context(tc.tile_pool(name="rawp", bufs=5))
-            grp = ph1.enter_context(tc.tile_pool(name="grp", bufs=4))
-            deip = ph1.enter_context(tc.tile_pool(name="deip", bufs=2)) if DEI else None
-            cdp = ph1.enter_context(tc.tile_pool(name="cdp", bufs=2))
-            stp = ph1.enter_context(tc.tile_pool(name="stp", bufs=3))
-            ps_t = ph1.enter_context(tc.psum_pool(name="ps_t", bufs=4))
-            ps_m = ph1.enter_context(tc.psum_pool(name="ps_m", bufs=4))
+        with ExitStack() as part1:
+            x_pool = part1.enter_context(tc.tile_pool(name="x_pool", bufs=1))
+            raw_pool = part1.enter_context(tc.tile_pool(name="raw_pool", bufs=5))
+            grouped_pool = part1.enter_context(tc.tile_pool(name="grouped_pool", bufs=4))
+            ordered_pool = part1.enter_context(tc.tile_pool(name="ordered_pool", bufs=2))
+            code_pool = part1.enter_context(tc.tile_pool(name="code_pool", bufs=2))
+            stage_pool = part1.enter_context(tc.tile_pool(name="stage_pool", bufs=3))
+            turn_banks = part1.enter_context(tc.psum_pool(name="turn_banks", bufs=4))
+            sum_banks = part1.enter_context(tc.psum_pool(name="sum_banks", bufs=4))
 
             raw_of = {}
-            dei_of = {}
+            ordered_of = {}
             banks_of = {}
             grouped_of = {}
             codes_of = {}
-            acc_of = {}
+            sums_of = {}
 
-            def load(n, gps=(0, 1)):
-                kind, src, m = pairs[n]
+            def load(n, halves=BOTH):
+                src, m = slabs[n][1], slabs[n][2]
                 if n not in raw_of:
-                    raw_of[n] = rawp.tile([P, 2, C], BF16, tag="raw", name="raw")
+                    raw_of[n] = raw_pool.tile([P, 2, K], BF16, name="raw")
                 raw = raw_of[n]
                 rows = src[256 * m:256 * (m + 1), :].rearrange("(r p) k -> p r k", p=P)
-                if n < FINE:
-                    for gp in gps:
+                if n < N_PIECEWISE:
+                    for half in halves:
                         for r in range(2):
-                            cols = slice(1024 * gp, 1024 * (gp + 1))
+                            cols = slice(1024 * half, 1024 * (half + 1))
                             nc.sync.dma_start(out=raw[:, r, cols], in_=rows[:, r, cols])
                 else:
                     nc.sync.dma_start(out=raw[:], in_=rows)
 
-            for n, gp in ((0, 0), (1, 0), (2, 0), (0, 1), (1, 1), (2, 1), (3, 0), (3, 1)):
-                load(n, (gp,))
+            for n, half in ((0, 0), (1, 0), (2, 0), (0, 1), (1, 1), (2, 1), (3, 0), (3, 1)):
+                load(n, (half,))
             load(4)
 
-            zeros = const.tile([P, P], F32, name="zeros")
-
-            zeros_bf = const.tile([P, TOK], BF16, name="zeros_bf")
-            nc.gpsimd.memset(zeros_bf[:], 0.0)
+            zeros = const.tile([P, TOK], BF16, name="zeros")
             nc.gpsimd.memset(zeros[:], 0.0)
 
-            def fill(count, wide=True):
-                filler = ps_m.tile([P, TOK], F32, tag="acc", name="acc")
+            def matmuls_on_zeros(count):
+                unread = sum_banks.tile([P, TOK], F32, name="sums")
                 for i in range(count):
-                    if wide:
-                        nc.tensor.matmul(out=filler[:], lhsT=zeros_bf[:, 0:P], rhs=zeros_bf[:], start=True, stop=True)
-                    else:
-                        nc.tensor.matmul(out=filler[:, 0:64], lhsT=zeros[:], rhs=zeros[:, 0:64], start=True, stop=True)
+                    nc.tensor.matmul(out=unread[:], lhsT=zeros[:, 0:P], rhs=zeros[:], start=True, stop=True)
 
-            fill(HEAD_FILL)
+            matmuls_on_zeros(WARM_UP)
 
             ident = const.tile([P, P], F32, name="ident")
             masks.make_identity(nc, ident[:])
             by_parity = ident[:].rearrange("p (d j) -> p j d", j=2)
-            for sp in range(2):
-                nc.vector.tensor_reduce(out=parity[:, sp:sp + 1], in_=by_parity[:, sp, :], axis=AX.X, op=ALU.add)
+            for s in range(2):
+                nc.vector.tensor_reduce(out=parity[:, s:s + 1], in_=by_parity[:, s, :], axis=AX.X, op=ALU.add)
             nc.vector.tensor_scalar(out=slot[:], in0=parity[:], scalar1=SCALE, scalar2=None, op0=ALU.mult)
             warm = const.tile([P, 2], F32, name="warm")
             nc.vector.memset(warm[:, 0:1], 0.0)
@@ -159,208 +152,204 @@ def tile_differentialattention_pa_kernel(tc, x, Wq, Wk, lq1, lq2, lk1, lk2, out)
             for j in range(2):
                 nc.vector.tensor_reduce(out=pick[:, j:j + 1], in_=by_row[:, :, j, :], axis=AX.XY, op=ALU.add)
 
-            x_codes = one.tile([P, PASSES * TOK], U32, name="x_codes", align_bytes=64)
-            x_scales = one.tile([P, PASSES * TOK], U8, name="x_scales", align_bytes=64)
+            x_codes = x_pool.tile([P, PASSES * TOK], U32, name="x_codes", align_bytes=64)
+            x_scales = x_pool.tile([P, PASSES * TOK], U8, name="x_scales", align_bytes=64)
 
-            def windows(n):
-                return (0, 128)
-
-            def deinterleave(n, gps=(0, 1)):
-                if n < DEI_FROM:
-                    return
+            def reorder(n, halves=BOTH):
                 words = raw_of[n][:].bitcast(F32)
-                if n not in dei_of:
-                    dei_of[n] = deip.tile([P, 2, C // 2], F32, tag="dei", name="dei")
-                dei = dei_of[n]
-                spans = [slice(512 * gp, 512 * (gp + 1)) for gp in gps] if n < FINE else [slice(0, C // 2)]
+                if n not in ordered_of:
+                    ordered_of[n] = ordered_pool.tile([P, 2, K // 2], F32, name="ordered")
+                ordered = ordered_of[n]
+                if n < N_PIECEWISE:
+                    spans = [slice(512 * half, 512 * (half + 1)) for half in halves]
+                else:
+                    spans = [slice(0, K // 2)]
                 for cols in spans:
                     for r in range(2):
                         nc.vector.tensor_copy(
-                            out=dei[:, r, cols].rearrange("p (g u c) -> p g u c", u=2, c=P),
-                            in_=words[:, r, cols].rearrange("p (g c u) -> p g u c", u=2, c=P),
+                            out=ordered[:, r, cols].rearrange("p (ps u c) -> p ps u c", u=2, c=P),
+                            in_=words[:, r, cols].rearrange("p (ps c u) -> p ps u c", u=2, c=P),
                         )
 
-            def transposes(n, gps=(0, 1)):
+            def transposes(n, halves=BOTH):
                 words = raw_of[n][:].bitcast(F32)
                 banks = banks_of.setdefault(n, [])
-                for gp in gps:
+                for half in halves:
                     for r in range(2):
-                        tb = ps_t.tile([P, 512], F32, tag="tb", name="tb")
-                        for gg in range(2):
+                        bank = turn_banks.tile([P, 512], F32, name="turned")
+                        for in_half in range(2):
                             for u in range(2):
-                                base = 256 * (2 * gp + gg)
-                                col = 128 * (2 * gg + u)
-                                if n >= DEI_FROM:
-                                    turned = dei_of[n][:, r, base + 128 * u:base + 128 * (u + 1)]
+                                base = 256 * (2 * half + in_half)
+                                col = 128 * (2 * in_half + u)
+                                if n >= N_STEPPED:
+                                    rows_in = ordered_of[n][:, r, base + 128 * u:base + 128 * (u + 1)]
                                 else:
-                                    turned = words[:, r, base + u:base + 256:2]
-                                nc.tensor.transpose(tb[:, col:col + 128], turned, ident[:])
-                        banks.append((gp, r, tb))
+                                    rows_in = words[:, r, base + u:base + 256:2]
+                                nc.tensor.transpose(bank[:, col:col + 128], rows_in, ident[:])
+                        banks.append((half, r, bank))
 
-            def interleave(n, gps=(0, 1)):
-                on_vector = (1, 3) if n == n_pairs - 1 else (3,)
-                for gp in gps:
-                    grouped = grp.tile([P, 2048], BF16, tag="grouped", name="grouped", align_bytes=64)
-                    gw = grouped[:].bitcast(F32).rearrange("p (g c u) -> p g c u", g=2, u=2)
-                    for bgp, r, tb in banks_of[n]:
-                        if bgp != gp:
+            def interleave(n, halves=BOTH):
+                on_vector = (1, 3) if n == last_slab else (3,)
+                for half in halves:
+                    grouped = grouped_pool.tile([P, 2048], BF16, name="grouped", align_bytes=64)
+                    grouped_words = grouped[:].bitcast(F32).rearrange("p (ps c u) -> p ps c u", ps=2, u=2)
+                    for bank_half, r, bank in banks_of[n]:
+                        if bank_half != half:
                             continue
-                        dst = gw[:, :, 128 * r:128 * r + 128, :]
-                        src = tb[:].rearrange("p (g u c) -> p g c u", g=2, u=2)
-                        if 2 * gp + r in on_vector:
+                        dst = grouped_words[:, :, 128 * r:128 * r + 128, :]
+                        src = bank[:].rearrange("p (ps u c) -> p ps c u", ps=2, u=2)
+                        if 2 * half + r in on_vector:
                             nc.vector.tensor_copy(out=dst, in_=src)
                         else:
                             nc.scalar.copy(out=dst, in_=src)
-                    grouped_of[(n, gp)] = grouped
+                    grouped_of[(n, half)] = grouped
 
-            def quantize(n, gps=(0, 1)):
-                kind, src, m = pairs[n]
-                if kind == "x":
-                    for gp in gps:
-                        for gg in range(2):
-                            g = 2 * gp + gg
-                            cols = slice(TOK * g + TA * n, TOK * g + TA * (n + 1))
+            def quantize(n, halves=BOTH):
+                if slabs[n][0] == "x":
+                    for half in halves:
+                        for in_half in range(2):
+                            ps = 2 * half + in_half
+                            cols = slice(TOK * ps + TA * n, TOK * ps + TA * (n + 1))
                             nc.vector.quantize_mx(
                                 out=x_codes[:, cols].bitcast(E5M2),
                                 scales=x_scales[:, cols],
-                                in_=grouped_of[(n, gp)][:, 1024 * gg:1024 * (gg + 1)],
+                                in_=grouped_of[(n, half)][:, 1024 * in_half:1024 * (in_half + 1)],
                             )
                     return
                 if n not in codes_of:
-                    codes = cdp.tile([P, PASSES * CW], U32, tag="codes", name="codes", align_bytes=64)
-                    scales = cdp.tile([P, PASSES * CW], U8, tag="scales", name="scales", align_bytes=64)
-                    codes_of[n] = (codes, scales)
-                codes, scales = codes_of[n]
-                for gp in gps:
-                    cols = slice(2 * CW * gp, 2 * CW * (gp + 1))
+                    w_codes = code_pool.tile([P, PASSES * CW], U32, name="w_codes", align_bytes=64)
+                    w_scales = code_pool.tile([P, PASSES * CW], U8, name="w_scales", align_bytes=64)
+                    codes_of[n] = (w_codes, w_scales)
+                w_codes, w_scales = codes_of[n]
+                for half in halves:
+                    cols = slice(2 * CW * half, 2 * CW * (half + 1))
                     nc.vector.quantize_mx(
-                        out=codes[:, cols].bitcast(E4M3),
-                        scales=scales[:, cols],
-                        in_=grouped_of[(n, gp)][:],
+                        out=w_codes[:, cols].bitcast(E4M3),
+                        scales=w_scales[:, cols],
+                        in_=grouped_of[(n, half)][:],
                     )
 
-            def project(n, gps=(0, 1)):
-                codes, scales = codes_of[n]
-                if n not in acc_of:
-                    acc_of[n] = []
-                    for w in windows(n):
-                        acc = ps_m.tile([P, TOK], F32, tag="acc", name="acc")
-                        acc_of[n].append((w, acc))
-                for w, acc in acc_of[n]:
-                    for gp in gps:
-                        for g in (2 * gp, 2 * gp + 1):
-                            cols = slice(CW * g + w, CW * g + w + 128)
-                            toks = slice(TOK * g, TOK * (g + 1))
+            def project(n, halves=BOTH):
+                w_codes, w_scales = codes_of[n]
+                if n not in sums_of:
+                    sums_of[n] = []
+                    for r in range(2):
+                        sums = sum_banks.tile([P, TOK], F32, name="sums")
+                        sums_of[n].append(sums)
+                for r, sums in enumerate(sums_of[n]):
+                    for half in halves:
+                        for ps in (2 * half, 2 * half + 1):
+                            cols = slice(CW * ps + 128 * r, CW * ps + 128 * r + 128)
+                            toks = slice(TOK * ps, TOK * (ps + 1))
                             nc.tensor.matmul_mx(
-                                out=acc[:],
-                                lhsT=codes[:, cols].bitcast(E4M3),
-                                lhsT_scale=scales[:, cols],
+                                out=sums[:],
+                                lhsT=w_codes[:, cols].bitcast(E4M3),
+                                lhsT_scale=w_scales[:, cols],
                                 rhs=x_codes[:, toks].bitcast(E5M2),
                                 rhs_scale=x_scales[:, toks],
-                                start=(g == 0),
-                                stop=(g == PASSES - 1),
+                                start=(ps == 0),
+                                stop=(ps == PASSES - 1),
                             )
 
             EVEN = slice(0, P, 2)
             ODD = slice(1, P, 2)
-            A_TOK = slice(0, TA)
-            B_TOK = slice(TA, TOK)
+            EVEN_TOK = slice(0, TA)
+            ODD_TOK = slice(TA, TOK)
 
             def keep_q(n):
-                m = pairs[n][2]
-                for w, acc in acc_of[n]:
-                    nc.scalar.copy(out=q_nat_rows[:, 2 * m + w // 128, :], in_=acc[:])
+                m = slabs[n][2]
+                for r, sums in enumerate(sums_of[n]):
+                    nc.scalar.copy(out=q_own_rows[:, 2 * m + r, :], in_=sums[:])
                 heads = slice(2 * m, 2 * m + 2)
-                nc.sync.dma_start(out=q_x_rows[ODD, heads, :], in_=q_nat_rows[EVEN, heads, B_TOK])
-                nc.sync.dma_start(out=q_x_rows[EVEN, heads, :], in_=q_nat_rows[ODD, heads, A_TOK])
+                nc.sync.dma_start(out=q_crossed_rows[ODD, heads, :], in_=q_own_rows[EVEN, heads, ODD_TOK])
+                nc.sync.dma_start(out=q_crossed_rows[EVEN, heads, :], in_=q_own_rows[ODD, heads, EVEN_TOK])
 
             def keep_k(n):
-                last = n == n_pairs - 1
-                stage = stp.tile([P, 2, TOK], F32, tag="stage", name="stage")
-                for r, (w, acc) in enumerate(acc_of[n]):
-                    if last and r == 1:
-                        cross_on_tensor(n, stage, acc)
+                stage = stage_pool.tile([P, 2, TOK], F32, name="stage")
+                for r, sums in enumerate(sums_of[n]):
+                    if n == last_slab and r == 1:
+                        settle_on_engines(n, stage, sums)
                         continue
-                    nc.scalar.copy(out=stage[:, r, :], in_=acc[:])
-                    if last:
-                        settle_k(n, stage, slice(r, r + 1))
-                if not last:
-                    settle_k(n, stage, slice(0, 2))
+                    nc.scalar.copy(out=stage[:, r, :], in_=sums[:])
+                    if n == last_slab:
+                        settle_by_dma(n, stage, slice(r, r + 1))
+                if n != last_slab:
+                    settle_by_dma(n, stage, slice(0, 2))
 
-            def cross_on_tensor(n, stage, acc):
-                head = 2 * pairs[n][2] + 1
+            def settle_on_engines(n, stage, sums):
+                head = 2 * slabs[n][2] + 1
                 swapped = {}
-                for name, toks in (("a", A_TOK), ("b", B_TOK)):
-                    nc.scalar.copy(out=stage[:, 1, toks], in_=acc[:, toks])
-                    sw = ps_m.tile([P, TOK], F32, tag="acc", name="acc")
-                    nc.tensor.matmul(out=sw[:, 0:TA], lhsT=swap[:], rhs=stage[:, 1, toks], start=True, stop=True)
-                    swapped[name] = sw
-                own = stp.tile([P, 2, TOK], F32, tag="stage", name="stage")
-                nc.scalar.activation(out=own[:, 1, 0:TA], in_=acc[:, B_TOK], func=ACT.Copy, scale=parity[:, 1:2])
-                nc.scalar.activation(out=own[:, 0, 0:TA], in_=acc[:, A_TOK], func=ACT.Copy, scale=parity[:, 0:1])
+                for name, toks in (("even", EVEN_TOK), ("odd", ODD_TOK)):
+                    nc.scalar.copy(out=stage[:, 1, toks], in_=sums[:, toks])
+                    bank = sum_banks.tile([P, TOK], F32, name="sums")
+                    nc.tensor.matmul(out=bank[:, 0:TA], lhsT=swap[:], rhs=stage[:, 1, toks], start=True, stop=True)
+                    swapped[name] = bank
+                own = stage_pool.tile([P, 2, TOK], F32, name="stage")
+                nc.scalar.activation(out=own[:, 1, 0:TA], in_=sums[:, ODD_TOK], func=ACT.Copy, scale=parity[:, 1:2])
+                nc.scalar.activation(out=own[:, 0, 0:TA], in_=sums[:, EVEN_TOK], func=ACT.Copy, scale=parity[:, 0:1])
                 nc.vector.scalar_tensor_tensor(
-                    out=k_rows[:, H + head, :], in0=swapped["a"][:, 0:TA], scalar=parity[:, 0:1], in1=own[:, 1, 0:TA],
-                    op0=ALU.mult, op1=ALU.add,
+                    out=k_rows[:, H + head, :], in0=swapped["even"][:, 0:TA], scalar=parity[:, 0:1],
+                    in1=own[:, 1, 0:TA], op0=ALU.mult, op1=ALU.add,
                 )
                 nc.vector.scalar_tensor_tensor(
-                    out=k_rows[:, head, :], in0=swapped["b"][:, 0:TA], scalar=parity[:, 1:2], in1=own[:, 0, 0:TA],
-                    op0=ALU.mult, op1=ALU.add,
+                    out=k_rows[:, head, :], in0=swapped["odd"][:, 0:TA], scalar=parity[:, 1:2],
+                    in1=own[:, 0, 0:TA], op0=ALU.mult, op1=ALU.add,
                 )
 
-            def settle_k(n, stage, heads):
-                m = pairs[n][2]
+            def settle_by_dma(n, stage, heads):
+                m = slabs[n][2]
                 first_map = slice(2 * m + heads.start, 2 * m + heads.stop)
                 second_map = slice(H + 2 * m + heads.start, H + 2 * m + heads.stop)
-                nc.sync.dma_start(out=k_rows[EVEN, first_map, :], in_=stage[EVEN, heads, A_TOK])
-                nc.sync.dma_start(out=k_rows[ODD, second_map, :], in_=stage[ODD, heads, B_TOK])
-                nc.sync.dma_start(out=k_rows[ODD, first_map, :], in_=stage[EVEN, heads, B_TOK])
-                nc.sync.dma_start(out=k_rows[EVEN, second_map, :], in_=stage[ODD, heads, A_TOK])
+                nc.sync.dma_start(out=k_rows[EVEN, first_map, :], in_=stage[EVEN, heads, EVEN_TOK])
+                nc.sync.dma_start(out=k_rows[ODD, second_map, :], in_=stage[ODD, heads, ODD_TOK])
+                nc.sync.dma_start(out=k_rows[ODD, first_map, :], in_=stage[EVEN, heads, ODD_TOK])
+                nc.sync.dma_start(out=k_rows[EVEN, second_map, :], in_=stage[ODD, heads, EVEN_TOK])
 
-            early = [(u, sj[0], sj[1]) for u in range(EARLY_UNITS) for sj in PIECES]
-            per_step = -(-len(early) // 6)
-            pads_at = {}
-            for i, piece in enumerate(early):
-                pads_at.setdefault(12 + i // per_step, []).append(piece)
-
-            lqk = const.tile([P, 4, D], BF16, name="lqk")
+            lam_vectors = const.tile([P, 4, D], BF16, name="lam_vectors")
+            exp_of_dots = const.tile([P, 2, 1], F32, name="exp_of_dots")
 
             def load_lambda():
                 for i, v in enumerate((lq1, lq2, lk1, lk2)):
-                    nc.sync.dma_start(out=lqk[:, i, :], in_=v.partition_broadcast(P))
+                    nc.sync.dma_start(out=lam_vectors[:, i, :], in_=v.partition_broadcast(P))
 
-            expd = const.tile([P, 2, 1], F32, name="expd")
+            def make_swap():
+                for j in range(2):
+                    nc.vector.tensor_copy(
+                        out=swap[:].rearrange("p (d j) -> p d j", j=2)[:, :, j],
+                        in_=ident[:].rearrange("p (d j) -> p d j", j=2)[:, :, 1 - j],
+                    )
 
             def exp_dots():
-                prod = const.tile([P, 2, D], F32, name="prod")
-                nc.vector.tensor_tensor(out=prod[:], in0=lqk[:, 0:2, :], in1=lqk[:, 2:4, :], op=ALU.mult)
+                products = const.tile([P, 2, D], F32, name="products")
+                nc.vector.tensor_tensor(
+                    out=products[:], in0=lam_vectors[:, 0:2, :], in1=lam_vectors[:, 2:4, :], op=ALU.mult
+                )
                 dots = const.tile([P, 2, 1], F32, name="dots")
-                nc.vector.tensor_reduce(out=dots[:], in_=prod[:], axis=AX.X, op=ALU.add)
-                nc.scalar.activation(out=expd[:], in_=dots[:], func=ACT.Exp)
+                nc.vector.tensor_reduce(out=dots[:], in_=products[:], axis=AX.X, op=ALU.add)
+                nc.scalar.activation(out=exp_of_dots[:], in_=dots[:], func=ACT.Exp)
 
-            def make_comb():
+            def make_lambda_and_comb():
                 neg_lam = const.tile([P, 1], F32, name="neg_lam")
                 nc.vector.scalar_tensor_tensor(
-                    out=neg_lam[:], in0=expd[:, 1, :], scalar=-LAM_INIT, in1=expd[:, 0, :],
+                    out=neg_lam[:], in0=exp_of_dots[:, 1, :], scalar=-LAM_INIT, in1=exp_of_dots[:, 0, :],
                     op0=ALU.add, op1=ALU.subtract,
                 )
                 nc.vector.tensor_tensor(out=lam_pick[:], in0=pick[:, 1:2], in1=neg_lam[:], op=ALU.mult)
                 nc.vector.tensor_tensor(
-                    out=comb[:, 0:HALF].rearrange("p (e q) -> p e q", q=32),
+                    out=comb[:, 0:HALF_P].rearrange("p (e q) -> p e q", q=32),
                     in0=by_row[:, :, 1, :], in1=by_row[:, :, 0, :], op=ALU.add,
                 )
 
-            LO = (0,)
-            HI = (1,)
             transposes(0, LO)
             transposes(1, LO)
-            fill(STEP_FILL)
+            matmuls_on_zeros(KEEP_WARM)
             interleave(0, LO)
             interleave(1, LO)
             quantize(0, LO)
             quantize(1, LO)
             transposes(2, LO)
             transposes(0, HI)
-            fill(STEP_FILL)
+            matmuls_on_zeros(KEEP_WARM)
             load(5)
             interleave(2, LO)
             quantize(2, LO)
@@ -376,177 +365,170 @@ def tile_differentialattention_pa_kernel(tc, x, Wq, Wk, lq1, lq2, lk1, lk2, out)
             transposes(3, LO)
             interleave(2, HI)
             quantize(2, HI)
-            deinterleave(4, LO)
+            reorder(4, LO)
             interleave(3, LO)
             quantize(3, LO)
             project(2, HI)
-            deinterleave(4, HI)
+            reorder(4, HI)
             keep_q(2)
             transposes(3, HI)
             load(8)
             interleave(3, HI)
             quantize(3, HI)
-            deinterleave(5)
+            reorder(5)
             transposes(4)
-            for n in range(4, n_pairs + 1):
-                if n - 1 >= 2:
-                    project(n - 1)
-                if DEI and n + 5 < n_pairs:
+
+            for n in range(4, n_slabs + 1):
+                project(n - 1)
+                if n + 5 < n_slabs:
                     load(n + 5)
-                if n < n_pairs:
+                if n < n_slabs:
                     interleave(n)
                     quantize(n)
-                    if DEI and n + 2 < n_pairs:
-                        deinterleave(n + 2)
-                if n - 1 >= 2:
-                    if pairs[n - 1][0] == "q":
-                        keep_q(n - 1)
-                    else:
-                        keep_k(n - 1)
-                for u, sp, jp in pads_at.get(n, ()):
-                    pad_piece(u, sp, jp)
-                if n + 1 < n_pairs:
+                    if n + 2 < n_slabs:
+                        reorder(n + 2)
+                if slabs[n - 1][0] == "q":
+                    keep_q(n - 1)
+                else:
+                    keep_k(n - 1)
+                if n + 1 < n_slabs:
                     transposes(n + 1)
-                    if not DEI and n + 4 < n_pairs:
-                        load(n + 4)
-                if n == 13:
+                if n == last_slab - 4:
                     load_lambda()
-                if n == 14:
-                    for j in range(2):
-                        nc.vector.tensor_copy(
-                            out=swap[:].rearrange("p (d j) -> p d j", j=2)[:, :, j],
-                            in_=ident[:].rearrange("p (d j) -> p d j", j=2)[:, :, 1 - j],
-                        )
-                if n == n_pairs - 1:
+                if n == last_slab - 3:
+                    make_swap()
+                if n == last_slab:
                     prepare(0)
-                if n == 15:
+                if n == last_slab - 2:
                     exp_dots()
-                if n == 16:
-                    make_comb()
+                if n == last_slab - 1:
+                    make_lambda_and_comb()
 
-        with ExitStack() as ph2:
-            sm = ph2.enter_context(tc.tile_pool(name="sm", bufs=2))
-            ps_s = ph2.enter_context(tc.psum_pool(name="ps_s", bufs=6))
-            ps_f = ph2.enter_context(tc.psum_pool(name="ps_f", bufs=2))
+        with ExitStack() as part2:
+            soft = part2.enter_context(tc.tile_pool(name="soft", bufs=2))
+            score_banks = part2.enter_context(tc.psum_pool(name="score_banks", bufs=BANKS_AHEAD))
+            comb_banks = part2.enter_context(tc.psum_pool(name="comb_banks", bufs=2))
 
-            k_cols = k_st[:].rearrange("p (m g e) -> p g m e", m=32, e=2)
-            out_v = out.rearrange("b n a h -> (b n) a h").rearrange("(g t) a h -> (t a) g h", t=4)
-            out_half = out.rearrange("b n a h -> (b n) a h").rearrange("(g e t) a h -> e (t a) g h", e=2, t=2)
-            att_of = {}
-            n_chunks = len(SIZES)
-            first = [sum(SIZES[:i]) for i in range(n_chunks)]
+            k_cols = k_all[:].rearrange("p (m g e) -> p g m e", m=ROWS, e=2)
+            out_rows = out.rearrange("batch pos hq h -> (batch pos) hq h")
+            out_by_group = out_rows.rearrange("(g e s) hq h -> (e s hq) g h", e=2, s=2)
+            out_by_pair = out_rows.rearrange("(g e s) hq h -> e (s hq) g h", e=2, s=2)
+            n_chunks = len(CHUNKS)
+            first = [sum(CHUNKS[:i]) for i in range(n_chunks)]
             plan = []
             for ch in range(n_chunks):
-                for lo in range(0, SIZES[ch], GB):
-                    plan.append((ch, lo, min(GB, SIZES[ch] - lo)))
+                for lo in range(0, CHUNKS[ch], GROUPS_IN_BANK):
+                    plan.append((ch, lo, min(GROUPS_IN_BANK, CHUNKS[ch] - lo)))
             n_banks = len(plan)
             first_bank = [min(b for b in range(n_banks) if plan[b][0] == ch) for ch in range(n_chunks)]
-            CH = max(SIZES)
+            WIDEST = max(CHUNKS)
             bank_of = {}
-            sc_of = {}
-            sd_of = {}
-            neg_of = {}
-            tot_of = {}
+            scores_of = {}
+            shifted_of = {}
+            neg_top_of = {}
+            total_of = {}
             exp_of = {}
             low_of = {}
-            fin_of = {}
+            att_of = {}
+            combined_of = {}
             emitted = [0]
 
             def by_dma(ch):
-                return ch < BY_DMA
+                return ch < N_BY_DMA
 
-            def score_banks(upto):
+            def short_exp(ch):
+                return ch >= SHORT_EXP_FROM
+
+            def score_matmuls(upto):
                 while emitted[0] < min(upto, n_banks):
                     b = emitted[0]
                     ch, lo, count = plan[b]
-                    sb = ps_s.tile([P, 512], F32, tag="sb", name="sb")
-                    for s in range(count):
-                        g = first[ch] + lo + s
+                    bank = score_banks.tile([P, 512], F32, name="scores_bank")
+                    for in_bank in range(count):
+                        g = first[ch] + lo + in_bank
                         nc.tensor.matmul(
-                            out=sb[:, 64 * s:64 * s + 64].rearrange("p (m e) -> p m e", e=2),
+                            out=bank[:, 64 * in_bank:64 * in_bank + 64].rearrange("p (m e) -> p m e", e=2),
                             lhsT=padded_of[g // UNIT][:, P * (g % UNIT):P * (g % UNIT + 1)],
                             rhs=k_cols[:, g, :, :],
                             start=True,
                             stop=True,
                         )
-                    bank_of[b] = sb
+                    bank_of[b] = bank
                     emitted[0] = b + 1
 
             def leave(ch):
-                sc = sm.tile([P, CH, 32], F32, tag="sc", name="sc")
+                scores = soft.tile([P, WIDEST, ROWS], F32, name="scores")
                 for b in range(n_banks):
                     if plan[b][0] != ch:
                         continue
                     lo, count = plan[b][1], plan[b][2]
-                    view = bank_of[b][:].rearrange("p (s m e) -> p s m e", s=GB, e=2)
+                    view = bank_of[b][:].rearrange("p (g m e) -> p g m e", g=GROUPS_IN_BANK, e=2)
                     for e in range(2):
-                        rows = slice(HALF * e, HALF * (e + 1))
-                        nc.scalar.copy(out=sc[rows, lo:lo + count, :], in_=view[rows, 0:count, :, e])
-                sc_of[ch] = sc
+                        rows = slice(HALF_P * e, HALF_P * (e + 1))
+                        nc.scalar.copy(out=scores[rows, lo:lo + count, :], in_=view[rows, 0:count, :, e])
+                scores_of[ch] = scores
 
             def shift(ch):
-                size = SIZES[ch]
-                sc = sc_of[ch]
-                top = sm.tile([P, CH, 1], F32, tag="top", name="top")
-                nc.vector.tensor_reduce(out=top[:, 0:size, :], in_=sc[:, 0:size, :], axis=AX.X, op=ALU.max)
-                if ch >= SCALAR_FROM:
-                    neg = sm.tile([P, CH, 1], F32, tag="neg", name="neg")
+                size = CHUNKS[ch]
+                scores = scores_of[ch]
+                top = soft.tile([P, WIDEST, 1], F32, name="top")
+                nc.vector.tensor_reduce(out=top[:, 0:size, :], in_=scores[:, 0:size, :], axis=AX.X, op=ALU.max)
+                if short_exp(ch):
+                    neg_top = soft.tile([P, WIDEST, 1], F32, name="neg_top")
                     nc.vector.tensor_scalar(
-                        out=neg[:, 0:size, :], in0=top[:, 0:size, :], scalar1=-1.0, scalar2=None, op0=ALU.mult
+                        out=neg_top[:, 0:size, :], in0=top[:, 0:size, :], scalar1=-1.0, scalar2=None, op0=ALU.mult
                     )
-                    neg_of[ch] = neg
+                    neg_top_of[ch] = neg_top
                     return
-                sd = sm.tile([P, CH, 32], F32, tag="sd", name="sd")
+                shifted = soft.tile([P, WIDEST, ROWS], F32, name="shifted")
                 nc.vector.tensor_tensor(
-                    out=sd[:, 0:size, :], in0=sc[:, 0:size, :],
-                    in1=top[:, 0:size, :].to_broadcast([P, size, 32]), op=ALU.subtract,
+                    out=shifted[:, 0:size, :], in0=scores[:, 0:size, :],
+                    in1=top[:, 0:size, :].to_broadcast([P, size, ROWS]), op=ALU.subtract,
                 )
-                sd_of[ch] = sd
+                shifted_of[ch] = shifted
 
             def exponent(ch):
-                size = SIZES[ch]
-                ex = sm.tile([P, CH, 32], F32, tag="ex", name="ex")
-                if ch >= SCALAR_FROM:
-                    tot = sm.tile([P, CH, 1], F32, tag="tot", name="tot")
-                    for g in range(size):
-                        nc.scalar.activation(
-                            out=ex[:, g, :], in_=sc_of[ch][:, g, :], func=ACT.Exp, bias=neg_of[ch][:, g, :], scale=1.0,
-                            accum_out=tot[:, g, :],
-                        )
-                    tot_of[ch] = tot
-                else:
-                    nc.scalar.activation(out=ex[:, 0:size, :], in_=sd_of[ch][:, 0:size, :], func=ACT.Exp)
+                size = CHUNKS[ch]
+                ex = soft.tile([P, WIDEST, ROWS], F32, name="ex")
                 exp_of[ch] = ex
-                if ch >= SCALAR_FROM:
+                if short_exp(ch):
+                    total = soft.tile([P, WIDEST, 1], F32, name="total")
+                    for in_chunk in range(size):
+                        nc.scalar.activation(
+                            out=ex[:, in_chunk, :], in_=scores_of[ch][:, in_chunk, :], func=ACT.Exp,
+                            bias=neg_top_of[ch][:, in_chunk, :], scale=1.0, accum_out=total[:, in_chunk, :],
+                        )
+                    total_of[ch] = total
                     return
-                low = sm.tile([P, CH, H], F32, tag="low", name="low")
+                nc.scalar.activation(out=ex[:, 0:size, :], in_=shifted_of[ch][:, 0:size, :], func=ACT.Exp)
+                low = soft.tile([P, WIDEST, H], F32, name="low")
                 nc.scalar.activation(
                     out=low[:, 0:size, :], in_=ex[:, 0:size, 0:H], func=ACT.Copy, scale=pick[:, 0:1]
                 )
                 low_of[ch] = low
 
             def normalize(ch):
-                size = SIZES[ch]
+                size = CHUNKS[ch]
                 ex = exp_of[ch]
-                if ch >= SCALAR_FROM:
-                    tot = tot_of[ch]
+                if short_exp(ch):
+                    total = total_of[ch]
                 else:
-                    tot = sm.tile([P, CH, 1], F32, tag="tot", name="tot")
-                    nc.vector.tensor_reduce(out=tot[:, 0:size, :], in_=ex[:, 0:size, :], axis=AX.X, op=ALU.add)
-                rec = sm.tile([P, CH, 1], F32, tag="rec", name="rec")
-                nc.vector.reciprocal(out=rec[:, 0:size, :], in_=tot[:, 0:size, :])
-                if ch >= SCALAR_FROM:
-                    low = sm.tile([P, CH, H], F32, tag="low", name="low")
+                    total = soft.tile([P, WIDEST, 1], F32, name="total")
+                    nc.vector.tensor_reduce(out=total[:, 0:size, :], in_=ex[:, 0:size, :], axis=AX.X, op=ALU.add)
+                rec = soft.tile([P, WIDEST, 1], F32, name="rec")
+                nc.vector.reciprocal(out=rec[:, 0:size, :], in_=total[:, 0:size, :])
+                if short_exp(ch):
+                    low = soft.tile([P, WIDEST, H], F32, name="low")
                     nc.vector.tensor_scalar(
                         out=low[:, 0:size, :], in0=ex[:, 0:size, 0:H], scalar1=pick[:, 0:1], scalar2=None, op0=ALU.mult
                     )
                     low_of[ch] = low
-                own = sm.tile([P, CH, H], F32, tag="own", name="own")
+                own = soft.tile([P, WIDEST, H], F32, name="own")
                 nc.vector.scalar_tensor_tensor(
-                    out=own[:, 0:size, :], in0=ex[:, 0:size, H:32], scalar=lam_pick[:, 0:1],
+                    out=own[:, 0:size, :], in0=ex[:, 0:size, H:ROWS], scalar=lam_pick[:, 0:1],
                     in1=low_of[ch][:, 0:size, :], op0=ALU.mult, op1=ALU.add,
                 )
-                att = sm.tile([P, CH, H], F32, tag="att", name="att")
+                att = soft.tile([P, WIDEST, H], F32, name="att")
                 nc.vector.tensor_tensor(
                     out=att[:, 0:size, :],
                     in0=own[:, 0:size, :],
@@ -554,53 +536,52 @@ def tile_differentialattention_pa_kernel(tc, x, Wq, Wk, lq1, lq2, lk1, lk2, out)
                     op=ALU.mult,
                 )
                 if by_dma(ch):
-                    mv = moved[ch % 2]
                     for e in range(2):
                         nc.sync.dma_start(
-                            out=mv[64 * e:64 * e + 32, 0:size, :], in_=att[64 * e + 32:64 * e + 64, 0:size, :]
+                            out=moved[ch % 2][64 * e:64 * e + 32, 0:size, :], in_=att[64 * e + 32:64 * e + 64, 0:size, :]
                         )
                     att_of[ch] = att
                     return
-                fin = ps_f.tile([P, CH * H], F32, tag="fin", name="fin")
+                combined = comb_banks.tile([P, WIDEST * H], F32, name="combined")
                 nc.tensor.matmul(
-                    out=fin[:, 0:size * H],
+                    out=combined[:, 0:size * H],
                     lhsT=comb[:],
                     rhs=att[:, 0:size, :].rearrange("p g h -> p (g h)"),
                     start=True,
                     stop=True,
                 )
-                fin_of[ch] = fin
+                combined_of[ch] = combined
 
             def finish(ch):
-                size = SIZES[ch]
-                res = sm.tile([P, CH, H], F32, tag="res", name="res")
+                size = CHUNKS[ch]
+                res = soft.tile([P, WIDEST, H], F32, name="res")
                 nc.vector.tensor_tensor(
                     out=res[:, 0:size, :], in0=att_of[ch][:, 0:size, :], in1=moved[ch % 2][:, 0:size, :], op=ALU.add
                 )
                 for e in range(2):
                     nc.sync.dma_start(
-                        out=out_half[e][:, first[ch]:first[ch] + size, :], in_=res[64 * e:64 * e + 32, 0:size, :]
+                        out=out_by_pair[e][:, first[ch]:first[ch] + size, :], in_=res[64 * e:64 * e + 32, 0:size, :]
                     )
 
             def store(ch):
-                size = SIZES[ch]
-                res = sm.tile([P, CH, H], F32, tag="res", name="res")
+                size = CHUNKS[ch]
+                res = soft.tile([P, WIDEST, H], F32, name="res")
                 nc.scalar.copy(
-                    out=res[0:HALF, 0:size, :].rearrange("p g h -> p (g h)"), in_=fin_of[ch][0:HALF, 0:size * H]
+                    out=res[0:HALF_P, 0:size, :].rearrange("p g h -> p (g h)"), in_=combined_of[ch][0:HALF_P, 0:size * H]
                 )
-                nc.sync.dma_start(out=out_v[:, first[ch]:first[ch] + size, :], in_=res[0:HALF, 0:size, :])
+                nc.sync.dma_start(out=out_by_group[:, first[ch]:first[ch] + size, :], in_=res[0:HALF_P, 0:size, :])
 
-            for u in range(1, 4):
-                prepare(u)
+            for unit in range(1, 4):
+                prepare(unit)
             for ch in range(n_chunks + 2):
-                ahead = ch == n_chunks - 2
+                older_first = SHORT_EXP_FROM < ch <= n_chunks - 2
                 if ch < n_chunks:
-                    score_banks(first_bank[ch] + 6)
-                    if not ahead:
+                    score_matmuls(first_bank[ch] + BANKS_AHEAD)
+                    if not older_first:
                         leave(ch)
                 if 1 <= ch <= n_chunks:
                     exponent(ch - 1)
-                if ahead:
+                if older_first:
                     normalize(ch - 1)
                     leave(ch)
                 if ch == n_chunks:
@@ -609,7 +590,7 @@ def tile_differentialattention_pa_kernel(tc, x, Wq, Wk, lq1, lq2, lk1, lk2, out)
                     store(ch - 2)
                 if ch < n_chunks:
                     shift(ch)
-                if 1 <= ch <= n_chunks and not ahead:
+                if 1 <= ch <= n_chunks and not older_first:
                     normalize(ch - 1)
                 if ch >= 2 and by_dma(ch - 2):
                     finish(ch - 2)

@@ -41,7 +41,7 @@ N_UNITS = 8
 CHUNKS = [16] * 7 + [12, 4]
 BANKS_AHEAD = 6
 N_BY_DMA = 6
-SHORT_EXP_FROM = 5
+SHORT_EXP_FROM = 6
 
 FLOPS = 2 * TOK * K * 2 * K + 2 * TOK * ROWS * ROWS * D
 

@@ -67,7 +67,8 @@ def tile_differentialattention_pa_kernel(tc, x, Wq, Wk, lq1, lq2, lk1, lk2, out)
         q_own_rows = q_own[:].rearrange("p (h tok) -> p h tok", h=H)
         q_crossed = kept.tile([P, H * TA], F32, name="q_crossed")
         q_crossed_rows = q_crossed[:].rearrange("p (h a) -> p h a", h=H)
-        comb = const.tile([P, P], F32, name="comb")
+        comb_first = const.tile([P, P], F32, name="comb_first")
+        comb_second = const.tile([P, P], F32, name="comb_second")
         pick = const.tile([P, 2], F32, name="pick")
         slot = const.tile([P, 2], F32, name="slot")
         lam_pick = const.tile([P, 1], F32, name="lam_pick")
@@ -145,7 +146,8 @@ def tile_differentialattention_pa_kernel(tc, x, Wq, Wk, lq1, lq2, lk1, lk2, out)
             warm = const.tile([P, 2], F32, name="warm")
             nc.vector.memset(warm[:, 0:1], 0.0)
             nc.scalar.activation(out=warm[:, 1:2], in_=warm[:, 0:1], func=ACT.Exp)
-            nc.vector.memset(comb[:], 0.0)
+            nc.vector.memset(comb_first[:], 0.0)
+            nc.vector.memset(comb_second[:], 0.0)
             for i in range(2):
                 nc.gpsimd.memset(moved[i][:], 0.0)
             by_row = ident[:].rearrange("p (e j q) -> p e j q", j=2, q=32)
@@ -335,9 +337,10 @@ def tile_differentialattention_pa_kernel(tc, x, Wq, Wk, lq1, lq2, lk1, lk2, out)
                     op0=ALU.add, op1=ALU.subtract,
                 )
                 nc.vector.tensor_tensor(out=lam_pick[:], in0=pick[:, 1:2], in1=neg_lam[:], op=ALU.mult)
-                nc.vector.tensor_tensor(
-                    out=comb[:, 0:HALF_P].rearrange("p (e q) -> p e q", q=32),
-                    in0=by_row[:, :, 1, :], in1=by_row[:, :, 0, :], op=ALU.add,
+                nc.vector.tensor_copy(out=comb_first[:, 0:HALF_P].rearrange("p (e q) -> p e q", q=32), in_=by_row[:, :, 0, :])
+                nc.vector.tensor_scalar(
+                    out=comb_second[:, 0:HALF_P].rearrange("p (e q) -> p e q", q=32), in0=by_row[:, :, 1, :],
+                    scalar1=neg_lam[:, 0:1], scalar2=None, op0=ALU.mult,
                 )
 
             transposes(0, LO)
@@ -471,15 +474,15 @@ def tile_differentialattention_pa_kernel(tc, x, Wq, Wk, lq1, lq2, lk1, lk2, out)
             def shift(ch):
                 size = CHUNKS[ch]
                 scores = scores_of[ch]
-                top = soft.tile([P, WIDEST, 1], F32, name="top")
-                nc.vector.tensor_reduce(out=top[:, 0:size, :], in_=scores[:, 0:size, :], axis=AX.X, op=ALU.max)
                 if short_exp(ch):
                     neg_top = soft.tile([P, WIDEST, 1], F32, name="neg_top")
-                    nc.vector.tensor_scalar(
-                        out=neg_top[:, 0:size, :], in0=top[:, 0:size, :], scalar1=-1.0, scalar2=None, op0=ALU.mult
+                    nc.vector.tensor_reduce(
+                        out=neg_top[:, 0:size, :], in_=scores[:, 0:size, :], axis=AX.X, op=ALU.max, negate=True
                     )
                     neg_top_of[ch] = neg_top
                     return
+                top = soft.tile([P, WIDEST, 1], F32, name="top")
+                nc.vector.tensor_reduce(out=top[:, 0:size, :], in_=scores[:, 0:size, :], axis=AX.X, op=ALU.max)
                 shifted = soft.tile([P, WIDEST, ROWS], F32, name="shifted")
                 nc.vector.tensor_tensor(
                     out=shifted[:, 0:size, :], in0=scores[:, 0:size, :],
@@ -517,12 +520,25 @@ def tile_differentialattention_pa_kernel(tc, x, Wq, Wk, lq1, lq2, lk1, lk2, out)
                     nc.vector.tensor_reduce(out=total[:, 0:size, :], in_=ex[:, 0:size, :], axis=AX.X, op=ALU.add)
                 rec = soft.tile([P, WIDEST, 1], F32, name="rec")
                 nc.vector.reciprocal(out=rec[:, 0:size, :], in_=total[:, 0:size, :])
-                if short_exp(ch):
-                    low = soft.tile([P, WIDEST, H], F32, name="low")
-                    nc.vector.tensor_scalar(
-                        out=low[:, 0:size, :], in0=ex[:, 0:size, 0:H], scalar1=pick[:, 0:1], scalar2=None, op0=ALU.mult
+                if not by_dma(ch):
+                    whole = soft.tile([P, WIDEST, ROWS], F32, name="whole")
+                    nc.vector.tensor_tensor(
+                        out=whole[:, 0:size, :],
+                        in0=ex[:, 0:size, :],
+                        in1=rec[:, 0:size, :].to_broadcast([P, size, ROWS]),
+                        op=ALU.mult,
                     )
-                    low_of[ch] = low
+                    combined = comb_banks.tile([P, WIDEST * H], F32, name="combined")
+                    for j, matrix in enumerate((comb_first, comb_second)):
+                        nc.tensor.matmul(
+                            out=combined[:, 0:size * H].rearrange("p (g h) -> p g h", h=H),
+                            lhsT=matrix[:],
+                            rhs=whole[:, 0:size, H * j:H * (j + 1)],
+                            start=(j == 0),
+                            stop=(j == 1),
+                        )
+                    combined_of[ch] = combined
+                    return
                 own = soft.tile([P, WIDEST, H], F32, name="own")
                 nc.vector.scalar_tensor_tensor(
                     out=own[:, 0:size, :], in0=ex[:, 0:size, H:ROWS], scalar=lam_pick[:, 0:1],
@@ -541,16 +557,6 @@ def tile_differentialattention_pa_kernel(tc, x, Wq, Wk, lq1, lq2, lk1, lk2, out)
                             out=moved[ch % 2][64 * e:64 * e + 32, 0:size, :], in_=att[64 * e + 32:64 * e + 64, 0:size, :]
                         )
                     att_of[ch] = att
-                    return
-                combined = comb_banks.tile([P, WIDEST * H], F32, name="combined")
-                nc.tensor.matmul(
-                    out=combined[:, 0:size * H],
-                    lhsT=comb[:],
-                    rhs=att[:, 0:size, :].rearrange("p g h -> p (g h)"),
-                    start=True,
-                    stop=True,
-                )
-                combined_of[ch] = combined
 
             def finish(ch):
                 size = CHUNKS[ch]
@@ -565,7 +571,7 @@ def tile_differentialattention_pa_kernel(tc, x, Wq, Wk, lq1, lq2, lk1, lk2, out)
 
             def store(ch):
                 size = CHUNKS[ch]
-                res = soft.tile([P, WIDEST, H], F32, name="res")
+                res = soft.tile([P, WIDEST, H], F32, name="res_of_chunk_%d" % ch)
                 nc.scalar.copy(
                     out=res[0:HALF_P, 0:size, :].rearrange("p g h -> p (g h)"), in_=combined_of[ch][0:HALF_P, 0:size * H]
                 )

@@ -40,6 +40,7 @@ UNIT_PAIRS = 2 * UNIT
 N_UNITS = 8
 CHUNKS = [16] * 7 + [12, 4]
 BANKS_AHEAD = 6
+FIRST = 32
 N_BY_DMA = 6
 SHORT_EXP_FROM = 6
 
@@ -231,14 +232,15 @@ def tile_differentialattention_pa_kernel(tc, x, Wq, Wk, lq1, lq2, lk1, lk2, out)
                         in_=grouped_of[(n, half)][:],
                     )
 
-            def project(n, halves=BOTH):
+            def project(n, halves=BOTH, heads=BOTH):
                 w_codes, w_scales = codes_of[n]
                 if n not in sums_of:
                     sums_of[n] = []
                     for r in range(2):
                         sums = sum_banks.tile([P, TOK], F32, name="sums")
                         sums_of[n].append(sums)
-                for r, sums in enumerate(sums_of[n]):
+                for r in heads:
+                    sums = sums_of[n][r]
                     for half in halves:
                         for ps in (2 * half, 2 * half + 1):
                             cols = slice(CW * ps + 128 * r, CW * ps + 128 * r + 128)
@@ -269,43 +271,62 @@ def tile_differentialattention_pa_kernel(tc, x, Wq, Wk, lq1, lq2, lk1, lk2, out)
             def keep_k(n):
                 stage = stage_pool.tile([P, 2, TOK], F32, name="stage")
                 for r, sums in enumerate(sums_of[n]):
-                    if n == last_slab and r == 1:
-                        settle_on_engines(n, stage, sums)
-                        continue
                     nc.scalar.copy(out=stage[:, r, :], in_=sums[:])
-                    if n == last_slab:
-                        settle_by_dma(n, stage, slice(r, r + 1))
-                if n != last_slab:
-                    settle_by_dma(n, stage, slice(0, 2))
+                settle_by_dma(n, stage, slice(0, 2))
 
-            def settle_on_engines(n, stage, sums):
-                head = 2 * slabs[n][2] + 1
-                swapped = {}
-                for name, toks in (("even", EVEN_TOK), ("odd", ODD_TOK)):
-                    nc.scalar.copy(out=stage[:, 1, toks], in_=sums[:, toks])
-                    bank = sum_banks.tile([P, TOK], F32, name="sums")
-                    nc.tensor.matmul(out=bank[:, 0:TA], lhsT=swap[:], rhs=stage[:, 1, toks], start=True, stop=True)
-                    swapped[name] = bank
-                own = stage_pool.tile([P, 2, TOK], F32, name="stage")
-                nc.scalar.activation(out=own[:, 1, 0:TA], in_=sums[:, ODD_TOK], func=ACT.Copy, scale=parity[:, 1:2])
-                nc.scalar.activation(out=own[:, 0, 0:TA], in_=sums[:, EVEN_TOK], func=ACT.Copy, scale=parity[:, 0:1])
+            small_of = {}
+            own_of = {}
+            swapped_of = {}
+            last_stage = {}
+
+            def leave_last(r):
+                n = last_slab
+                by_token = sums_of[n][r][:].rearrange("p (s a) -> p s a", s=2)
+                small = stage_pool.tile([P, 2, FIRST], F32, name="small")
+                nc.scalar.copy(out=small[:], in_=by_token[:, :, 0:FIRST])
+                own = stage_pool.tile([P, 2, FIRST], F32, name="own")
+                for s in range(2):
+                    nc.scalar.activation(
+                        out=own[:, s, :], in_=by_token[:, s, 0:FIRST], func=ACT.Copy, scale=parity[:, s:s + 1]
+                    )
+                small_of[r] = small
+                own_of[r] = own
+                if r == 0:
+                    last_stage[0] = stage_pool.tile([P, 2, TOK], F32, name="stage")
+                stage = last_stage[0]
+                nc.scalar.copy(out=stage[:, r, :], in_=sums_of[n][r][:])
+                settle_by_dma(n, stage, slice(r, r + 1), FIRST)
+
+            def swap_first(r):
+                bank = sum_banks.tile([P, TOK], F32, name="sums")
+                nc.tensor.matmul(
+                    out=bank[:, 0:2 * FIRST], lhsT=swap[:], rhs=small_of[r][:].rearrange("p s a -> p (s a)"),
+                    start=True, stop=True,
+                )
+                swapped_of[r] = bank
+
+            def pick_first(r):
+                head = 2 * slabs[last_slab][2] + r
+                swapped = swapped_of[r][:, 0:2 * FIRST].rearrange("p (s a) -> p s a", s=2)
                 nc.vector.scalar_tensor_tensor(
-                    out=k_rows[:, H + head, :], in0=swapped["even"][:, 0:TA], scalar=parity[:, 0:1],
-                    in1=own[:, 1, 0:TA], op0=ALU.mult, op1=ALU.add,
+                    out=k_rows[:, H + head, 0:FIRST], in0=swapped[:, 0, :], scalar=parity[:, 0:1],
+                    in1=own_of[r][:, 1, :], op0=ALU.mult, op1=ALU.add,
                 )
                 nc.vector.scalar_tensor_tensor(
-                    out=k_rows[:, head, :], in0=swapped["odd"][:, 0:TA], scalar=parity[:, 1:2],
-                    in1=own[:, 0, 0:TA], op0=ALU.mult, op1=ALU.add,
+                    out=k_rows[:, head, 0:FIRST], in0=swapped[:, 1, :], scalar=parity[:, 1:2],
+                    in1=own_of[r][:, 0, :], op0=ALU.mult, op1=ALU.add,
                 )
 
-            def settle_by_dma(n, stage, heads):
+            def settle_by_dma(n, stage, heads, lo=0):
                 m = slabs[n][2]
                 first_map = slice(2 * m + heads.start, 2 * m + heads.stop)
                 second_map = slice(H + 2 * m + heads.start, H + 2 * m + heads.stop)
-                nc.sync.dma_start(out=k_rows[EVEN, first_map, :], in_=stage[EVEN, heads, EVEN_TOK])
-                nc.sync.dma_start(out=k_rows[ODD, second_map, :], in_=stage[ODD, heads, ODD_TOK])
-                nc.sync.dma_start(out=k_rows[ODD, first_map, :], in_=stage[EVEN, heads, ODD_TOK])
-                nc.sync.dma_start(out=k_rows[EVEN, second_map, :], in_=stage[ODD, heads, EVEN_TOK])
+                even_tok = slice(lo, TA)
+                odd_tok = slice(TA + lo, TOK)
+                nc.sync.dma_start(out=k_rows[EVEN, first_map, lo:TA], in_=stage[EVEN, heads, even_tok])
+                nc.sync.dma_start(out=k_rows[ODD, second_map, lo:TA], in_=stage[ODD, heads, odd_tok])
+                nc.sync.dma_start(out=k_rows[ODD, first_map, lo:TA], in_=stage[EVEN, heads, odd_tok])
+                nc.sync.dma_start(out=k_rows[EVEN, second_map, lo:TA], in_=stage[ODD, heads, even_tok])
 
             lam_vectors = const.tile([P, 4, D], BF16, name="lam_vectors")
             exp_of_dots = const.tile([P, 2, 1], F32, name="exp_of_dots")
@@ -382,6 +403,17 @@ def tile_differentialattention_pa_kernel(tc, x, Wq, Wk, lq1, lq2, lk1, lk2, out)
             transposes(4)
 
             for n in range(4, n_slabs + 1):
+                if n == n_slabs:
+                    project(last_slab, BOTH, (0,))
+                    leave_last(0)
+                    project(last_slab, BOTH, (1,))
+                    swap_first(0)
+                    pick_first(0)
+                    leave_last(1)
+                    swap_first(1)
+                    matmuls_on_zeros(2)
+                    pick_first(1)
+                    break
                 project(n - 1)
                 if n + 5 < n_slabs:
                     load(n + 5)

@@ -177,6 +177,20 @@ def tile_differentialattention_pa_kernel(tc, x, Wq, Wk, lq1, lq2, lk1, lk2, out)
             def transposes(n, halves=BOTH):
                 words = raw_of[n][:].bitcast(F32)
                 banks = banks_of.setdefault(n, [])
+                if n > N_STEPPED:
+                    for half in halves:
+                        for r in range(2):
+                            bank = turn_banks.tile([P, 512], F32, name="turned")
+                            banks.append((half, r, bank))
+                    for in_half in range(2):
+                        for u in range(2):
+                            for half, r, bank in banks:
+                                base = 256 * (2 * half + in_half)
+                                col = 128 * (2 * in_half + u)
+                                nc.tensor.transpose(
+                                    bank[:, col:col + 128], ordered_of[n][:, r, base + 128 * u:base + 128 * (u + 1)], ident[:]
+                                )
+                    return
                 for half in halves:
                     for r in range(2):
                         bank = turn_banks.tile([P, 512], F32, name="turned")

@@ -163,6 +163,17 @@ def tile_differentialattention_pa_kernel(tc, x, Wq, Wk, lq1, lq2, lk1, lk2, out)
                 if n not in ordered_of:
                     ordered_of[n] = ordered_pool.tile([P, 2, K // 2], F32, name="ordered")
                 ordered = ordered_of[n]
+                if n > N_STEPPED:
+                    in_order = ordered[:].rearrange("p r w -> p (r w)").rearrange(
+                        "p (ih u half r c) -> p half r ih u c", ih=2, u=2, half=2, r=2
+                    )
+                    for half in halves:
+                        for r in range(2):
+                            nc.vector.tensor_copy(
+                                out=in_order[:, half, r],
+                                in_=words[:, r, 512 * half:512 * (half + 1)].rearrange("p (ih c u) -> p ih u c", u=2, c=P),
+                            )
+                    return
                 if n < N_PIECEWISE:
                     spans = [slice(512 * half, 512 * (half + 1)) for half in halves]
                 else:
@@ -182,14 +193,14 @@ def tile_differentialattention_pa_kernel(tc, x, Wq, Wk, lq1, lq2, lk1, lk2, out)
                         for r in range(2):
                             bank = turn_banks.tile([P, 512], F32, name="turned")
                             banks.append((half, r, bank))
+                    runs = ordered_of[n][:].rearrange("p r w -> p (r w)")
+                    place = 0
                     for in_half in range(2):
                         for u in range(2):
                             for half, r, bank in banks:
-                                base = 256 * (2 * half + in_half)
                                 col = 128 * (2 * in_half + u)
-                                nc.tensor.transpose(
-                                    bank[:, col:col + 128], ordered_of[n][:, r, base + 128 * u:base + 128 * (u + 1)], ident[:]
-                                )
+                                nc.tensor.transpose(bank[:, col:col + 128], runs[:, 128 * place:128 * (place + 1)], ident[:])
+                                place += 1
                     return
                 for half in halves:
                     for r in range(2):

@@ -453,7 +453,7 @@ def tile_differentialattention_pa_kernel(tc, x, Wq, Wk, lq1, lq2, lk1, lk2, out)
                     keep_k(n - 1)
                 if n + 1 < n_slabs:
                     transposes(n + 1)
-                if n == last_slab - 4:
+                if n == last_slab - 8:
                     load_lambda()
                 if n == last_slab - 3:
                     make_swap()

@@ -99,7 +99,8 @@ def tile_differentialattention_pa_kernel(tc, x, Wq, Wk, lq1, lq2, lk1, lk2, out)
             grouped_pool = part1.enter_context(tc.tile_pool(name="grouped_pool", bufs=4))
             ordered_pool = part1.enter_context(tc.tile_pool(name="ordered_pool", bufs=2))
             code_pool = part1.enter_context(tc.tile_pool(name="code_pool", bufs=2))
-            stage_pool = part1.enter_context(tc.tile_pool(name="stage_pool", bufs=3))
+            stage_pool = part1.enter_context(tc.tile_pool(name="stage_pool", bufs=2))
+            pair_pool = part1.enter_context(tc.tile_pool(name="pair_pool", bufs=2))
             turn_banks = part1.enter_context(tc.psum_pool(name="turn_banks", bufs=4))
             sum_banks = part1.enter_context(tc.psum_pool(name="sum_banks", bufs=4))
 
@@ -289,15 +290,28 @@ def tile_differentialattention_pa_kernel(tc, x, Wq, Wk, lq1, lq2, lk1, lk2, out)
                 m = slabs[n][2]
                 for r, sums in enumerate(sums_of[n]):
                     nc.scalar.copy(out=q_own_rows[:, 2 * m + r, :], in_=sums[:])
-                heads = slice(2 * m, 2 * m + 2)
+                if m % 2 == 0:
+                    return
+                heads = slice(2 * m - 2, 2 * m + 2)
                 nc.sync.dma_start(out=q_crossed_rows[ODD, heads, :], in_=q_own_rows[EVEN, heads, ODD_TOK])
                 nc.sync.dma_start(out=q_crossed_rows[EVEN, heads, :], in_=q_own_rows[ODD, heads, EVEN_TOK])
 
+            pair_stage = {}
+
             def keep_k(n):
-                stage = stage_pool.tile([P, 2, TOK], F32, name="stage")
+                m = slabs[n][2]
+                if n == last_slab - 1:
+                    stage = stage_pool.tile([P, 2, TOK], F32, name="stage")
+                    for r, sums in enumerate(sums_of[n]):
+                        nc.scalar.copy(out=stage[:, r, :], in_=sums[:])
+                    settle_by_dma(n, stage, slice(0, 2))
+                    return
+                if m % 2 == 0:
+                    pair_stage[0] = pair_pool.tile([P, 4, TOK], F32, name="pair_stage")
                 for r, sums in enumerate(sums_of[n]):
-                    nc.scalar.copy(out=stage[:, r, :], in_=sums[:])
-                settle_by_dma(n, stage, slice(0, 2))
+                    nc.scalar.copy(out=pair_stage[0][:, 2 * (m % 2) + r, :], in_=sums[:])
+                if m % 2 == 1:
+                    settle_by_dma(n - 1, pair_stage[0], slice(0, 4))
 
             small_of = {}
             own_of = {}

@@ -65,7 +65,7 @@ def tile_differentialattention_pa_kernel(tc, x, Wq, Wk, lq1, lq2, lk1, lk2, out)
         k_all = kept.tile([P, ROWS * TA], F32, name="k_all")
         k_rows = k_all[:].rearrange("p (m a) -> p m a", m=ROWS)
         q_own = kept.tile([P, H * TOK], F32, name="q_own")
-        q_own_rows = q_own[:].rearrange("p (h tok) -> p h tok", h=H)
+        q_own_rows = q_own[:].rearrange("p (s h a) -> p s h a", s=2, h=H)
         q_crossed = kept.tile([P, H * TA], F32, name="q_crossed")
         q_crossed_rows = q_crossed[:].rearrange("p (h a) -> p h a", h=H)
         comb_first = const.tile([P, P], F32, name="comb_first")
@@ -77,7 +77,7 @@ def tile_differentialattention_pa_kernel(tc, x, Wq, Wk, lq1, lq2, lk1, lk2, out)
         parity = const.tile([P, 2], F32, name="parity")
         moved = [const.tile([P, UNIT, H], F32, name="moved%d" % i) for i in range(2)]
 
-        own_blocks = q_own[:].rearrange("p (hb hl tok) -> p hb tok hl", hb=4, hl=4)
+        own_blocks = q_own[:].rearrange("p (s hb hl a) -> p s hb a hl", s=2, hb=4, hl=4)
         crossed_blocks = q_crossed[:].rearrange("p (hb hl a) -> p hb a hl", hb=4, hl=4)
         padded_of = {}
 
@@ -86,7 +86,7 @@ def tile_differentialattention_pa_kernel(tc, x, Wq, Wk, lq1, lq2, lk1, lk2, out)
             dst = padded_of[unit][:].rearrange("p (a j s hb hl) -> p s j hb a hl", s=2, j=2, hb=4, hl=4)
             for s, j in ((0, 0), (1, 1), (0, 1), (1, 0)):
                 if j == s:
-                    src = own_blocks[:, :, TA * s + UNIT_PAIRS * unit:TA * s + UNIT_PAIRS * (unit + 1), :]
+                    src = own_blocks[:, s, :, UNIT_PAIRS * unit:UNIT_PAIRS * (unit + 1), :]
                 else:
                     src = crossed_blocks[:, :, UNIT_PAIRS * unit:UNIT_PAIRS * (unit + 1), :]
                 nc.vector.tensor_scalar(
@@ -283,33 +283,33 @@ def tile_differentialattention_pa_kernel(tc, x, Wq, Wk, lq1, lq2, lk1, lk2, out)
 
             EVEN = slice(0, P, 2)
             ODD = slice(1, P, 2)
-            EVEN_TOK = slice(0, TA)
-            ODD_TOK = slice(TA, TOK)
 
             def keep_q(n):
                 m = slabs[n][2]
                 for r, sums in enumerate(sums_of[n]):
-                    nc.scalar.copy(out=q_own_rows[:, 2 * m + r, :], in_=sums[:])
+                    nc.scalar.copy(out=q_own_rows[:, :, 2 * m + r, :], in_=sums[:].rearrange("p (s a) -> p s a", s=2))
                 if m % 2 == 0:
                     return
                 heads = slice(2 * m - 2, 2 * m + 2)
-                nc.sync.dma_start(out=q_crossed_rows[ODD, heads, :], in_=q_own_rows[EVEN, heads, ODD_TOK])
-                nc.sync.dma_start(out=q_crossed_rows[EVEN, heads, :], in_=q_own_rows[ODD, heads, EVEN_TOK])
+                nc.sync.dma_start(out=q_crossed_rows[ODD, heads, :], in_=q_own_rows[EVEN, 1, heads, :])
+                nc.sync.dma_start(out=q_crossed_rows[EVEN, heads, :], in_=q_own_rows[ODD, 0, heads, :])
 
             pair_stage = {}
 
             def keep_k(n):
                 m = slabs[n][2]
                 if n == last_slab - 1:
-                    stage = stage_pool.tile([P, 2, TOK], F32, name="stage")
+                    stage = stage_pool.tile([P, 2, 2, TA], F32, name="stage")
                     for r, sums in enumerate(sums_of[n]):
-                        nc.scalar.copy(out=stage[:, r, :], in_=sums[:])
+                        nc.scalar.copy(out=stage[:, :, r, :], in_=sums[:].rearrange("p (s a) -> p s a", s=2))
                     settle_by_dma(n, stage, slice(0, 2))
                     return
                 if m % 2 == 0:
-                    pair_stage[0] = pair_pool.tile([P, 4, TOK], F32, name="pair_stage")
+                    pair_stage[0] = pair_pool.tile([P, 2, 4, TA], F32, name="pair_stage")
                 for r, sums in enumerate(sums_of[n]):
-                    nc.scalar.copy(out=pair_stage[0][:, 2 * (m % 2) + r, :], in_=sums[:])
+                    nc.scalar.copy(
+                        out=pair_stage[0][:, :, 2 * (m % 2) + r, :], in_=sums[:].rearrange("p (s a) -> p s a", s=2)
+                    )
                 if m % 2 == 1:
                     settle_by_dma(n - 1, pair_stage[0], slice(0, 4))
 
@@ -331,9 +331,9 @@ def tile_differentialattention_pa_kernel(tc, x, Wq, Wk, lq1, lq2, lk1, lk2, out)
                 small_of[r] = small
                 own_of[r] = own
                 if r == 0:
-                    last_stage[0] = stage_pool.tile([P, 2, TOK], F32, name="stage")
+                    last_stage[0] = stage_pool.tile([P, 2, 2, TA], F32, name="stage")
                 stage = last_stage[0]
-                nc.scalar.copy(out=stage[:, r, :], in_=sums_of[n][r][:])
+                nc.scalar.copy(out=stage[:, :, r, :], in_=by_token)
                 settle_by_dma(n, stage, slice(r, r + 1), FIRST)
 
             def swap_first(r):
@@ -360,12 +360,10 @@ def tile_differentialattention_pa_kernel(tc, x, Wq, Wk, lq1, lq2, lk1, lk2, out)
                 m = slabs[n][2]
                 first_map = slice(2 * m + heads.start, 2 * m + heads.stop)
                 second_map = slice(H + 2 * m + heads.start, H + 2 * m + heads.stop)
-                even_tok = slice(lo, TA)
-                odd_tok = slice(TA + lo, TOK)
-                nc.sync.dma_start(out=k_rows[EVEN, first_map, lo:TA], in_=stage[EVEN, heads, even_tok])
-                nc.sync.dma_start(out=k_rows[ODD, second_map, lo:TA], in_=stage[ODD, heads, odd_tok])
-                nc.sync.dma_start(out=k_rows[ODD, first_map, lo:TA], in_=stage[EVEN, heads, odd_tok])
-                nc.sync.dma_start(out=k_rows[EVEN, second_map, lo:TA], in_=stage[ODD, heads, even_tok])
+                nc.sync.dma_start(out=k_rows[EVEN, first_map, lo:TA], in_=stage[EVEN, 0, heads, lo:TA])
+                nc.sync.dma_start(out=k_rows[ODD, second_map, lo:TA], in_=stage[ODD, 1, heads, lo:TA])
+                nc.sync.dma_start(out=k_rows[ODD, first_map, lo:TA], in_=stage[EVEN, 1, heads, lo:TA])
+                nc.sync.dma_start(out=k_rows[EVEN, second_map, lo:TA], in_=stage[ODD, 0, heads, lo:TA])
 
             lam_vectors = const.tile([P, 4, D], BF16, name="lam_vectors")
             exp_of_dots = const.tile([P, 2, 1], F32, name="exp_of_dots")

@@ -302,7 +302,8 @@ def tile_differentialattention_pa_kernel(tc, x, Wq, Wk, lq1, lq2, lk1, lk2, out)
                     stage = stage_pool.tile([P, 2, 2, TA], F32, name="stage")
                     for r, sums in enumerate(sums_of[n]):
                         nc.scalar.copy(out=stage[:, :, r, :], in_=sums[:].rearrange("p (s a) -> p s a", s=2))
-                    settle_by_dma(n, stage, slice(0, 2))
+                    settle_by_dma(n, stage, slice(0, 2), 0, FIRST)
+                    settle_by_dma(n, stage, slice(0, 2), FIRST)
                     return
                 if m % 2 == 0:
                     pair_stage[0] = pair_pool.tile([P, 2, 4, TA], F32, name="pair_stage")
@@ -356,14 +357,14 @@ def tile_differentialattention_pa_kernel(tc, x, Wq, Wk, lq1, lq2, lk1, lk2, out)
                     in1=own_of[r][:, 0, :], op0=ALU.mult, op1=ALU.add,
                 )
 
-            def settle_by_dma(n, stage, heads, lo=0):
+            def settle_by_dma(n, stage, heads, lo=0, hi=TA):
                 m = slabs[n][2]
                 first_map = slice(2 * m + heads.start, 2 * m + heads.stop)
                 second_map = slice(H + 2 * m + heads.start, H + 2 * m + heads.stop)
-                nc.sync.dma_start(out=k_rows[EVEN, first_map, lo:TA], in_=stage[EVEN, 0, heads, lo:TA])
-                nc.sync.dma_start(out=k_rows[ODD, second_map, lo:TA], in_=stage[ODD, 1, heads, lo:TA])
-                nc.sync.dma_start(out=k_rows[ODD, first_map, lo:TA], in_=stage[EVEN, 1, heads, lo:TA])
-                nc.sync.dma_start(out=k_rows[EVEN, second_map, lo:TA], in_=stage[ODD, 0, heads, lo:TA])
+                nc.sync.dma_start(out=k_rows[EVEN, first_map, lo:hi], in_=stage[EVEN, 0, heads, lo:hi])
+                nc.sync.dma_start(out=k_rows[ODD, second_map, lo:hi], in_=stage[ODD, 1, heads, lo:hi])
+                nc.sync.dma_start(out=k_rows[ODD, first_map, lo:hi], in_=stage[EVEN, 1, heads, lo:hi])
+                nc.sync.dma_start(out=k_rows[EVEN, second_map, lo:hi], in_=stage[ODD, 0, heads, lo:hi])
 
             lam_vectors = const.tile([P, 4, D], BF16, name="lam_vectors")
             exp_of_dots = const.tile([P, 2, 1], F32, name="exp_of_dots")

@@ -468,14 +468,12 @@ def tile_differentialattention_pa_kernel(tc, x, Wq, Wk, lq1, lq2, lk1, lk2, out)
                     transposes(n + 1)
                 if n == last_slab - 8:
                     load_lambda()
-                if n == last_slab - 3:
+                if n == last_slab - 1:
+                    exp_dots()
                     make_swap()
+                    make_lambda_and_comb()
                 if n == last_slab:
                     prepare(0)
-                if n == last_slab - 2:
-                    exp_dots()
-                if n == last_slab - 1:
-                    make_lambda_and_comb()
 
         with ExitStack() as part2:
             soft = part2.enter_context(tc.tile_pool(name="soft", bufs=2))

from contextlib import ExitStack

import concourse.masks as masks
import concourse.mybir as mybir

F32 = mybir.dt.float32
BF16 = mybir.dt.bfloat16
U32 = mybir.dt.uint32
U8 = mybir.dt.uint8
E4M3 = mybir.dt.float8_e4m3fn_x4
E5M2 = mybir.dt.float8_e5m2_x4
ALU = mybir.AluOpType
ACT = mybir.ActivationFunctionType
AX = mybir.AxisListType

P = 128
HALF_P = 64
K = 2048
H = 16
ROWS = 32
D = 64
TOK = 512
TA = 256
PASSES = 4
CW = 256
SCALE = 0.125
LAM_INIT = 0.8 - 0.6 * 2.718281828459045 ** (-3.6)

LO = (0,)
HI = (1,)
BOTH = (0, 1)
N_PIECEWISE = 5
N_STEPPED = 4
WARM_UP = 4
KEEP_WARM = 2

GROUPS_IN_BANK = 8
UNIT = 16
UNIT_PAIRS = 2 * UNIT
N_UNITS = 8
CHUNKS = [16] * 7 + [12, 4]
BANKS_AHEAD = 6
FIRST = 32
N_BY_DMA = 6
SHORT_EXP_FROM = 6

FLOPS = 2 * TOK * K * 2 * K + 2 * TOK * ROWS * ROWS * D


def tile_differentialattention_pa_kernel(tc, x, Wq, Wk, lq1, lq2, lk1, lk2, out):
    nc = tc.nc
    x_by_parity = x.flatten_outer_dims().rearrange("(a s) k -> s a k", s=2)
    slabs = [("x", x_by_parity[s], 0) for s in range(2)]
    slabs += [("q", Wq, m) for m in range(8)]
    slabs += [("k", Wk, m) for m in range(8)]
    n_slabs = len(slabs)
    last_slab = n_slabs - 1

    with ExitStack() as ctx:
        const = ctx.enter_context(tc.tile_pool(name="const", bufs=1))
        kept = ctx.enter_context(tc.tile_pool(name="kept", bufs=1))
        pad_pool = ctx.enter_context(tc.tile_pool(name="pad_pool", bufs=4))
        ctx.enter_context(tc.manual_schedule())

        k_all = kept.tile([P, ROWS * TA], F32, name="k_all")
        k_rows = k_all[:].rearrange("p (m a) -> p m a", m=ROWS)
        q_own = kept.tile([P, H * TOK], F32, name="q_own")
        q_own_rows = q_own[:].rearrange("p (s h a) -> p s h a", s=2, h=H)
        q_crossed = kept.tile([P, H * TA], F32, name="q_crossed")
        q_crossed_rows = q_crossed[:].rearrange("p (h a) -> p h a", h=H)
        comb_first = const.tile([P, P], F32, name="comb_first")
        comb_second = const.tile([P, P], F32, name="comb_second")
        pick = const.tile([P, 2], F32, name="pick")
        slot = const.tile([P, 2], F32, name="slot")
        lam_pick = const.tile([P, 1], F32, name="lam_pick")
        swap = const.tile([P, P], F32, name="swap")
        parity = const.tile([P, 2], F32, name="parity")
        moved = [const.tile([P, UNIT, H], F32, name="moved%d" % i) for i in range(2)]

        own_blocks = q_own[:].rearrange("p (s hb hl a) -> p s hb a hl", s=2, hb=4, hl=4)
        crossed_blocks = q_crossed[:].rearrange("p (hb hl a) -> p hb a hl", hb=4, hl=4)
        padded_of = {}

        def prepare(unit):
            padded_of[unit] = pad_pool.tile([P, UNIT_PAIRS * 64], F32, name="padded")
            dst = padded_of[unit][:].rearrange("p (a j s hb hl) -> p s j hb a hl", s=2, j=2, hb=4, hl=4)
            for s, j in ((0, 0), (1, 1), (0, 1), (1, 0)):
                if j == s:
                    src = own_blocks[:, s, :, UNIT_PAIRS * unit:UNIT_PAIRS * (unit + 1), :]
                else:
                    src = crossed_blocks[:, :, UNIT_PAIRS * unit:UNIT_PAIRS * (unit + 1), :]
                nc.vector.tensor_scalar(
                    out=dst[:, s, j], in0=src, scalar1=slot[:, s:s + 1], scalar2=None, op0=ALU.mult,
                )

        with ExitStack() as part1:
            x_pool = part1.enter_context(tc.tile_pool(name="x_pool", bufs=1))
            raw_pool = part1.enter_context(tc.tile_pool(name="raw_pool", bufs=5))
            grouped_pool = part1.enter_context(tc.tile_pool(name="grouped_pool", bufs=4))
            ordered_pool = part1.enter_context(tc.tile_pool(name="ordered_pool", bufs=2))
            code_pool = part1.enter_context(tc.tile_pool(name="code_pool", bufs=2))
            stage_pool = part1.enter_context(tc.tile_pool(name="stage_pool", bufs=2))
            pair_pool = part1.enter_context(tc.tile_pool(name="pair_pool", bufs=2))
            turn_banks = part1.enter_context(tc.psum_pool(name="turn_banks", bufs=4))
            sum_banks = part1.enter_context(tc.psum_pool(name="sum_banks", bufs=4))

            raw_of = {}
            ordered_of = {}
            banks_of = {}
            grouped_of = {}
            codes_of = {}
            sums_of = {}

            def load(n, halves=BOTH):
                src, m = slabs[n][1], slabs[n][2]
                if n not in raw_of:
                    raw_of[n] = raw_pool.tile([P, 2, K], BF16, name="raw")
                raw = raw_of[n]
                rows = src[256 * m:256 * (m + 1), :].rearrange("(r p) k -> p r k", p=P)
                if n < N_PIECEWISE:
                    for half in halves:
                        for r in range(2):
                            cols = slice(1024 * half, 1024 * (half + 1))
                            nc.sync.dma_start(out=raw[:, r, cols], in_=rows[:, r, cols])
                else:
                    nc.sync.dma_start(out=raw[:], in_=rows)

            for n, half in ((0, 0), (1, 0), (2, 0), (0, 1), (1, 1), (2, 1), (3, 0), (3, 1)):
                load(n, (half,))
            load(4)

            zeros = const.tile([P, TOK], BF16, name="zeros")
            nc.gpsimd.memset(zeros[:], 0.0)

            def matmuls_on_zeros(count):
                unread = sum_banks.tile([P, TOK], F32, name="sums")
                for i in range(count):
                    nc.tensor.matmul(out=unread[:], lhsT=zeros[:, 0:P], rhs=zeros[:], start=True, stop=True)

            matmuls_on_zeros(WARM_UP)

            ident = const.tile([P, P], F32, name="ident")
            masks.make_identity(nc, ident[:])
            by_parity = ident[:].rearrange("p (d j) -> p j d", j=2)
            for s in range(2):
                nc.vector.tensor_reduce(out=parity[:, s:s + 1], in_=by_parity[:, s, :], axis=AX.X, op=ALU.add)
            nc.vector.tensor_scalar(out=slot[:], in0=parity[:], scalar1=SCALE, scalar2=None, op0=ALU.mult)
            warm = const.tile([P, 2], F32, name="warm")
            nc.vector.memset(warm[:, 0:1], 0.0)
            nc.scalar.activation(out=warm[:, 1:2], in_=warm[:, 0:1], func=ACT.Exp)
            nc.vector.memset(comb_first[:], 0.0)
            nc.vector.memset(comb_second[:], 0.0)
            for i in range(2):
                nc.gpsimd.memset(moved[i][:], 0.0)
            by_row = ident[:].rearrange("p (e j q) -> p e j q", j=2, q=32)
            for j in range(2):
                nc.vector.tensor_reduce(out=pick[:, j:j + 1], in_=by_row[:, :, j, :], axis=AX.XY, op=ALU.add)

            x_codes = x_pool.tile([P, PASSES * TOK], U32, name="x_codes", align_bytes=64)
            x_scales = x_pool.tile([P, PASSES * TOK], U8, name="x_scales", align_bytes=64)

            def reorder(n, halves=BOTH):
                words = raw_of[n][:].bitcast(F32)
                if n not in ordered_of:
                    ordered_of[n] = ordered_pool.tile([P, 2, K // 2], F32, name="ordered")
                ordered = ordered_of[n]
                if n > N_STEPPED:
                    in_order = ordered[:].rearrange("p r w -> p (r w)").rearrange(
                        "p (ih u half r c) -> p half r ih u c", ih=2, u=2, half=2, r=2
                    )
                    for half in halves:
                        for r in range(2):
                            nc.vector.tensor_copy(
                                out=in_order[:, half, r],
                                in_=words[:, r, 512 * half:512 * (half + 1)].rearrange("p (ih c u) -> p ih u c", u=2, c=P),
                            )
                    return
                if n < N_PIECEWISE:
                    spans = [slice(512 * half, 512 * (half + 1)) for half in halves]
                else:
                    spans = [slice(0, K // 2)]
                for cols in spans:
                    for r in range(2):
                        nc.vector.tensor_copy(
                            out=ordered[:, r, cols].rearrange("p (ps u c) -> p ps u c", u=2, c=P),
                            in_=words[:, r, cols].rearrange("p (ps c u) -> p ps u c", u=2, c=P),
                        )

            def transposes(n, halves=BOTH):
                words = raw_of[n][:].bitcast(F32)
                banks = banks_of.setdefault(n, [])
                if n > N_STEPPED:
                    for half in halves:
                        for r in range(2):
                            bank = turn_banks.tile([P, 512], F32, name="turned")
                            banks.append((half, r, bank))
                    runs = ordered_of[n][:].rearrange("p r w -> p (r w)")
                    place = 0
                    for in_half in range(2):
                        for u in range(2):
                            for half, r, bank in banks:
                                col = 128 * (2 * in_half + u)
                                nc.tensor.transpose(bank[:, col:col + 128], runs[:, 128 * place:128 * (place + 1)], ident[:])
                                place += 1
                    return
                for half in halves:
                    for r in range(2):
                        bank = turn_banks.tile([P, 512], F32, name="turned")
                        for in_half in range(2):
                            for u in range(2):
                                base = 256 * (2 * half + in_half)
                                col = 128 * (2 * in_half + u)
                                if n >= N_STEPPED:
                                    rows_in = ordered_of[n][:, r, base + 128 * u:base + 128 * (u + 1)]
                                else:
                                    rows_in = words[:, r, base + u:base + 256:2]
                                nc.tensor.transpose(bank[:, col:col + 128], rows_in, ident[:])
                        banks.append((half, r, bank))

            def interleave(n, halves=BOTH):
                on_vector = (1, 3) if n == last_slab else (3,)
                for half in halves:
                    grouped = grouped_pool.tile([P, 2048], BF16, name="grouped", align_bytes=64)
                    grouped_words = grouped[:].bitcast(F32).rearrange("p (ps c u) -> p ps c u", ps=2, u=2)
                    for bank_half, r, bank in banks_of[n]:
                        if bank_half != half:
                            continue
                        dst = grouped_words[:, :, 128 * r:128 * r + 128, :]
                        src = bank[:].rearrange("p (ps u c) -> p ps c u", ps=2, u=2)
                        if 2 * half + r in on_vector:
                            nc.vector.tensor_copy(out=dst, in_=src)
                        else:
                            nc.scalar.copy(out=dst, in_=src)
                    grouped_of[(n, half)] = grouped

            def quantize(n, halves=BOTH):
                if slabs[n][0] == "x":
                    for half in halves:
                        for in_half in range(2):
                            ps = 2 * half + in_half
                            cols = slice(TOK * ps + TA * n, TOK * ps + TA * (n + 1))
                            nc.vector.quantize_mx(
                                out=x_codes[:, cols].bitcast(E5M2),
                                scales=x_scales[:, cols],
                                in_=grouped_of[(n, half)][:, 1024 * in_half:1024 * (in_half + 1)],
                            )
                    return
                if n not in codes_of:
                    w_codes = code_pool.tile([P, PASSES * CW], U32, name="w_codes", align_bytes=64)
                    w_scales = code_pool.tile([P, PASSES * CW], U8, name="w_scales", align_bytes=64)
                    codes_of[n] = (w_codes, w_scales)
                w_codes, w_scales = codes_of[n]
                for half in halves:
                    cols = slice(2 * CW * half, 2 * CW * (half + 1))
                    nc.vector.quantize_mx(
                        out=w_codes[:, cols].bitcast(E4M3),
                        scales=w_scales[:, cols],
                        in_=grouped_of[(n, half)][:],
                    )

            def project(n, halves=BOTH, heads=BOTH):
                w_codes, w_scales = codes_of[n]
                if n not in sums_of:
                    sums_of[n] = []
                    for r in range(2):
                        sums = sum_banks.tile([P, TOK], F32, name="sums")
                        sums_of[n].append(sums)
                for r in heads:
                    sums = sums_of[n][r]
                    for half in halves:
                        for ps in (2 * half, 2 * half + 1):
                            cols = slice(CW * ps + 128 * r, CW * ps + 128 * r + 128)
                            toks = slice(TOK * ps, TOK * (ps + 1))
                            nc.tensor.matmul_mx(
                                out=sums[:],
                                lhsT=w_codes[:, cols].bitcast(E4M3),
                                lhsT_scale=w_scales[:, cols],
                                rhs=x_codes[:, toks].bitcast(E5M2),
                                rhs_scale=x_scales[:, toks],
                                start=(ps == 0),
                                stop=(ps == PASSES - 1),
                            )

            EVEN = slice(0, P, 2)
            ODD = slice(1, P, 2)

            def keep_q(n):
                m = slabs[n][2]
                for r, sums in enumerate(sums_of[n]):
                    nc.scalar.copy(out=q_own_rows[:, :, 2 * m + r, :], in_=sums[:].rearrange("p (s a) -> p s a", s=2))
                if m % 2 == 0:
                    return
                heads = slice(2 * m - 2, 2 * m + 2)
                nc.sync.dma_start(out=q_crossed_rows[ODD, heads, :], in_=q_own_rows[EVEN, 1, heads, :])
                nc.sync.dma_start(out=q_crossed_rows[EVEN, heads, :], in_=q_own_rows[ODD, 0, heads, :])

            pair_stage = {}

            def keep_k(n):
                m = slabs[n][2]
                if n == last_slab - 1:
                    stage = stage_pool.tile([P, 2, 2, TA], F32, name="stage")
                    for r, sums in enumerate(sums_of[n]):
                        nc.scalar.copy(out=stage[:, :, r, :], in_=sums[:].rearrange("p (s a) -> p s a", s=2))
                    settle_by_dma(n, stage, slice(0, 2), 0, FIRST)
                    settle_by_dma(n, stage, slice(0, 2), FIRST)
                    return
                if m % 2 == 0:
                    pair_stage[0] = pair_pool.tile([P, 2, 4, TA], F32, name="pair_stage")
                for r, sums in enumerate(sums_of[n]):
                    nc.scalar.copy(
                        out=pair_stage[0][:, :, 2 * (m % 2) + r, :], in_=sums[:].rearrange("p (s a) -> p s a", s=2)
                    )
                if m % 2 == 1:
                    settle_by_dma(n - 1, pair_stage[0], slice(0, 4))

            small_of = {}
            own_of = {}
            swapped_of = {}
            last_stage = {}

            def leave_last(r):
                n = last_slab
                by_token = sums_of[n][r][:].rearrange("p (s a) -> p s a", s=2)
                small = stage_pool.tile([P, 2, FIRST], F32, name="small")
                nc.scalar.copy(out=small[:], in_=by_token[:, :, 0:FIRST])
                own = stage_pool.tile([P, 2, FIRST], F32, name="own")
                for s in range(2):
                    nc.scalar.activation(
                        out=own[:, s, :], in_=by_token[:, s, 0:FIRST], func=ACT.Copy, scale=parity[:, s:s + 1]
                    )
                small_of[r] = small
                own_of[r] = own
                if r == 0:
                    last_stage[0] = stage_pool.tile([P, 2, 2, TA], F32, name="stage")
                stage = last_stage[0]
                nc.scalar.copy(out=stage[:, :, r, :], in_=by_token)
                settle_by_dma(n, stage, slice(r, r + 1), FIRST)

            def swap_first(r):
                bank = sum_banks.tile([P, TOK], F32, name="sums")
                nc.tensor.matmul(
                    out=bank[:, 0:2 * FIRST], lhsT=swap[:], rhs=small_of[r][:].rearrange("p s a -> p (s a)"),
                    start=True, stop=True,
                )
                swapped_of[r] = bank

            def pick_first(r):
                head = 2 * slabs[last_slab][2] + r
                swapped = swapped_of[r][:, 0:2 * FIRST].rearrange("p (s a) -> p s a", s=2)
                nc.vector.scalar_tensor_tensor(
                    out=k_rows[:, H + head, 0:FIRST], in0=swapped[:, 0, :], scalar=parity[:, 0:1],
                    in1=own_of[r][:, 1, :], op0=ALU.mult, op1=ALU.add,
                )
                nc.vector.scalar_tensor_tensor(
                    out=k_rows[:, head, 0:FIRST], in0=swapped[:, 1, :], scalar=parity[:, 1:2],
                    in1=own_of[r][:, 0, :], op0=ALU.mult, op1=ALU.add,
                )

            def settle_by_dma(n, stage, heads, lo=0, hi=TA):
                m = slabs[n][2]
                first_map = slice(2 * m + heads.start, 2 * m + heads.stop)
                second_map = slice(H + 2 * m + heads.start, H + 2 * m + heads.stop)
                nc.sync.dma_start(out=k_rows[EVEN, first_map, lo:hi], in_=stage[EVEN, 0, heads, lo:hi])
                nc.sync.dma_start(out=k_rows[ODD, second_map, lo:hi], in_=stage[ODD, 1, heads, lo:hi])
                nc.sync.dma_start(out=k_rows[ODD, first_map, lo:hi], in_=stage[EVEN, 1, heads, lo:hi])
                nc.sync.dma_start(out=k_rows[EVEN, second_map, lo:hi], in_=stage[ODD, 0, heads, lo:hi])

            lam_vectors = const.tile([P, 4, D], BF16, name="lam_vectors")
            exp_of_dots = const.tile([P, 2, 1], F32, name="exp_of_dots")

            def load_lambda():
                for i, v in enumerate((lq1, lq2, lk1, lk2)):
                    nc.sync.dma_start(out=lam_vectors[:, i, :], in_=v.partition_broadcast(P))

            def make_swap():
                for j in range(2):
                    nc.vector.tensor_copy(
                        out=swap[:].rearrange("p (d j) -> p d j", j=2)[:, :, j],
                        in_=ident[:].rearrange("p (d j) -> p d j", j=2)[:, :, 1 - j],
                    )

            def exp_dots():
                products = const.tile([P, 2, D], F32, name="products")
                nc.vector.tensor_tensor(
                    out=products[:], in0=lam_vectors[:, 0:2, :], in1=lam_vectors[:, 2:4, :], op=ALU.mult
                )
                dots = const.tile([P, 2, 1], F32, name="dots")
                nc.vector.tensor_reduce(out=dots[:], in_=products[:], axis=AX.X, op=ALU.add)
                nc.scalar.activation(out=exp_of_dots[:], in_=dots[:], func=ACT.Exp)

            def make_lambda_and_comb():
                neg_lam = const.tile([P, 1], F32, name="neg_lam")
                nc.vector.scalar_tensor_tensor(
                    out=neg_lam[:], in0=exp_of_dots[:, 1, :], scalar=-LAM_INIT, in1=exp_of_dots[:, 0, :],
                    op0=ALU.add, op1=ALU.subtract,
                )
                nc.vector.tensor_tensor(out=lam_pick[:], in0=pick[:, 1:2], in1=neg_lam[:], op=ALU.mult)
                nc.vector.tensor_copy(out=comb_first[:, 0:HALF_P].rearrange("p (e q) -> p e q", q=32), in_=by_row[:, :, 0, :])
                nc.vector.tensor_scalar(
                    out=comb_second[:, 0:HALF_P].rearrange("p (e q) -> p e q", q=32), in0=by_row[:, :, 1, :],
                    scalar1=neg_lam[:, 0:1], scalar2=None, op0=ALU.mult,
                )

            transposes(0, LO)
            transposes(1, LO)
            matmuls_on_zeros(KEEP_WARM)
            interleave(0, LO)
            interleave(1, LO)
            quantize(0, LO)
            quantize(1, LO)
            transposes(2, LO)
            transposes(0, HI)
            matmuls_on_zeros(KEEP_WARM)
            load(5)
            interleave(2, LO)
            quantize(2, LO)
            interleave(0, HI)
            quantize(0, HI)
            transposes(1, HI)
            load(6)
            project(2, LO)
            interleave(1, HI)
            quantize(1, HI)
            transposes(2, HI)
            load(7)
            transposes(3, LO)
            interleave(2, HI)
            quantize(2, HI)
            reorder(4, LO)
            interleave(3, LO)
            quantize(3, LO)
            project(2, HI)
            reorder(4, HI)
            keep_q(2)
            transposes(3, HI)
            load(8)
            interleave(3, HI)
            quantize(3, HI)
            reorder(5)
            transposes(4)

            for n in range(4, n_slabs + 1):
                if n == n_slabs:
                    project(last_slab, BOTH, (0,))
                    leave_last(0)
                    project(last_slab, BOTH, (1,))
                    swap_first(0)
                    pick_first(0)
                    leave_last(1)
                    swap_first(1)
                    matmuls_on_zeros(2)
                    pick_first(1)
                    break
                project(n - 1)
                if n + 5 < n_slabs:
                    load(n + 5)
                if n < n_slabs:
                    interleave(n)
                    quantize(n)
                    if n + 2 < n_slabs:
                        reorder(n + 2)
                if slabs[n - 1][0] == "q":
                    keep_q(n - 1)
                else:
                    keep_k(n - 1)
                if n + 1 < n_slabs:
                    transposes(n + 1)
                if n == last_slab - 8:
                    load_lambda()
                if n == last_slab - 1:
                    exp_dots()
                    make_swap()
                    make_lambda_and_comb()
                if n == last_slab:
                    prepare(0)

        with ExitStack() as part2:
            soft = part2.enter_context(tc.tile_pool(name="soft", bufs=2))
            score_banks = part2.enter_context(tc.psum_pool(name="score_banks", bufs=BANKS_AHEAD))
            comb_banks = part2.enter_context(tc.psum_pool(name="comb_banks", bufs=2))

            k_cols = k_all[:].rearrange("p (m g e) -> p g m e", m=ROWS, e=2)
            out_rows = out.rearrange("batch pos hq h -> (batch pos) hq h")
            out_by_group = out_rows.rearrange("(g e s) hq h -> (e s hq) g h", e=2, s=2)
            out_by_pair = out_rows.rearrange("(g e s) hq h -> e (s hq) g h", e=2, s=2)
            n_chunks = len(CHUNKS)
            first = [sum(CHUNKS[:i]) for i in range(n_chunks)]
            plan = []
            for ch in range(n_chunks):
                for lo in range(0, CHUNKS[ch], GROUPS_IN_BANK):
                    plan.append((ch, lo, min(GROUPS_IN_BANK, CHUNKS[ch] - lo)))
            n_banks = len(plan)
            first_bank = [min(b for b in range(n_banks) if plan[b][0] == ch) for ch in range(n_chunks)]
            WIDEST = max(CHUNKS)
            bank_of = {}
            scores_of = {}
            shifted_of = {}
            neg_top_of = {}
            total_of = {}
            exp_of = {}
            low_of = {}
            att_of = {}
            combined_of = {}
            emitted = [0]

            def by_dma(ch):
                return ch < N_BY_DMA

            def short_exp(ch):
                return ch >= SHORT_EXP_FROM

            def score_matmuls(upto):
                while emitted[0] < min(upto, n_banks):
                    b = emitted[0]
                    ch, lo, count = plan[b]
                    bank = score_banks.tile([P, 512], F32, name="scores_bank")
                    for in_bank in range(count):
                        g = first[ch] + lo + in_bank
                        nc.tensor.matmul(
                            out=bank[:, 64 * in_bank:64 * in_bank + 64].rearrange("p (m e) -> p m e", e=2),
                            lhsT=padded_of[g // UNIT][:, P * (g % UNIT):P * (g % UNIT + 1)],
                            rhs=k_cols[:, g, :, :],
                            start=True,
                            stop=True,
                        )
                    bank_of[b] = bank
                    emitted[0] = b + 1

            def leave(ch):
                scores = soft.tile([P, WIDEST, ROWS], F32, name="scores")
                for b in range(n_banks):
                    if plan[b][0] != ch:
                        continue
                    lo, count = plan[b][1], plan[b][2]
                    view = bank_of[b][:].rearrange("p (g m e) -> p g m e", g=GROUPS_IN_BANK, e=2)
                    for e in range(2):
                        rows = slice(HALF_P * e, HALF_P * (e + 1))
                        nc.scalar.copy(out=scores[rows, lo:lo + count, :], in_=view[rows, 0:count, :, e])
                scores_of[ch] = scores

            def shift(ch):
                size = CHUNKS[ch]
                scores = scores_of[ch]
                if short_exp(ch):
                    neg_top = soft.tile([P, WIDEST, 1], F32, name="neg_top")
                    nc.vector.tensor_reduce(
                        out=neg_top[:, 0:size, :], in_=scores[:, 0:size, :], axis=AX.X, op=ALU.max, negate=True
                    )
                    neg_top_of[ch] = neg_top
                    return
                top = soft.tile([P, WIDEST, 1], F32, name="top")
                nc.vector.tensor_reduce(out=top[:, 0:size, :], in_=scores[:, 0:size, :], axis=AX.X, op=ALU.max)
                shifted = soft.tile([P, WIDEST, ROWS], F32, name="shifted")
                nc.vector.tensor_tensor(
                    out=shifted[:, 0:size, :], in0=scores[:, 0:size, :],
                    in1=top[:, 0:size, :].to_broadcast([P, size, ROWS]), op=ALU.subtract,
                )
                shifted_of[ch] = shifted

            def exponent(ch):
                size = CHUNKS[ch]
                ex = soft.tile([P, WIDEST, ROWS], F32, name="ex")
                exp_of[ch] = ex
                if short_exp(ch):
                    total = soft.tile([P, WIDEST, 1], F32, name="total")
                    for in_chunk in range(size):
                        nc.scalar.activation(
                            out=ex[:, in_chunk, :], in_=scores_of[ch][:, in_chunk, :], func=ACT.Exp,
                            bias=neg_top_of[ch][:, in_chunk, :], scale=1.0, accum_out=total[:, in_chunk, :],
                        )
                    total_of[ch] = total
                    return
                nc.scalar.activation(out=ex[:, 0:size, :], in_=shifted_of[ch][:, 0:size, :], func=ACT.Exp)
                low = soft.tile([P, WIDEST, H], F32, name="low")
                nc.scalar.activation(
                    out=low[:, 0:size, :], in_=ex[:, 0:size, 0:H], func=ACT.Copy, scale=pick[:, 0:1]
                )
                low_of[ch] = low

            def normalize(ch):
                size = CHUNKS[ch]
                ex = exp_of[ch]
                if short_exp(ch):
                    total = total_of[ch]
                else:
                    total = soft.tile([P, WIDEST, 1], F32, name="total")
                    nc.vector.tensor_reduce(out=total[:, 0:size, :], in_=ex[:, 0:size, :], axis=AX.X, op=ALU.add)
                rec = soft.tile([P, WIDEST, 1], F32, name="rec")
                nc.vector.reciprocal(out=rec[:, 0:size, :], in_=total[:, 0:size, :])
                if not by_dma(ch):
                    whole = soft.tile([P, WIDEST, ROWS], F32, name="whole")
                    nc.vector.tensor_tensor(
                        out=whole[:, 0:size, :],
                        in0=ex[:, 0:size, :],
                        in1=rec[:, 0:size, :].to_broadcast([P, size, ROWS]),
                        op=ALU.mult,
                    )
                    combined = comb_banks.tile([P, WIDEST * H], F32, name="combined")
                    for j, matrix in enumerate((comb_first, comb_second)):
                        nc.tensor.matmul(
                            out=combined[:, 0:size * H].rearrange("p (g h) -> p g h", h=H),
                            lhsT=matrix[:],
                            rhs=whole[:, 0:size, H * j:H * (j + 1)],
                            start=(j == 0),
                            stop=(j == 1),
                        )
                    combined_of[ch] = combined
                    return
                own = soft.tile([P, WIDEST, H], F32, name="own")
                nc.vector.scalar_tensor_tensor(
                    out=own[:, 0:size, :], in0=ex[:, 0:size, H:ROWS], scalar=lam_pick[:, 0:1],
                    in1=low_of[ch][:, 0:size, :], op0=ALU.mult, op1=ALU.add,
                )
                att = soft.tile([P, WIDEST, H], F32, name="att")
                nc.vector.tensor_tensor(
                    out=att[:, 0:size, :],
                    in0=own[:, 0:size, :],
                    in1=rec[:, 0:size, :].to_broadcast([P, size, H]),
                    op=ALU.mult,
                )
                if by_dma(ch):
                    for e in range(2):
                        nc.sync.dma_start(
                            out=moved[ch % 2][64 * e:64 * e + 32, 0:size, :], in_=att[64 * e + 32:64 * e + 64, 0:size, :]
                        )
                    att_of[ch] = att

            def finish(ch):
                size = CHUNKS[ch]
                res = soft.tile([P, WIDEST, H], F32, name="res")
                nc.vector.tensor_tensor(
                    out=res[:, 0:size, :], in0=att_of[ch][:, 0:size, :], in1=moved[ch % 2][:, 0:size, :], op=ALU.add
                )
                for e in range(2):
                    nc.sync.dma_start(
                        out=out_by_pair[e][:, first[ch]:first[ch] + size, :], in_=res[64 * e:64 * e + 32, 0:size, :]
                    )

            def store(ch):
                size = CHUNKS[ch]
                res = soft.tile([P, WIDEST, H], F32, name="res_of_chunk_%d" % ch)
                nc.scalar.copy(
                    out=res[0:HALF_P, 0:size, :].rearrange("p g h -> p (g h)"), in_=combined_of[ch][0:HALF_P, 0:size * H]
                )
                nc.sync.dma_start(out=out_by_group[:, first[ch]:first[ch] + size, :], in_=res[0:HALF_P, 0:size, :])

            for unit in range(1, 4):
                prepare(unit)
            for ch in range(n_chunks + 2):
                older_first = SHORT_EXP_FROM < ch <= n_chunks - 2
                if ch < n_chunks:
                    score_matmuls(first_bank[ch] + BANKS_AHEAD)
                    if not older_first:
                        leave(ch)
                if 1 <= ch <= n_chunks:
                    exponent(ch - 1)
                if older_first:
                    normalize(ch - 1)
                    leave(ch)
                if ch == n_chunks:
                    store(ch - 3)
                if ch >= 2 and not by_dma(ch - 2) and ch != n_chunks - 1:
                    store(ch - 2)
                if ch < n_chunks:
                    shift(ch)
                if 1 <= ch <= n_chunks and not older_first:
                    normalize(ch - 1)
                if ch >= 2 and by_dma(ch - 2):
                    finish(ch - 2)
                if ch + 4 < N_UNITS:
                    prepare(ch + 4)
